import numpy as np
import ml_dtypes


def mxq(x, axis, fmt="e4m3"):
    dtype, down = {"e4m3": (ml_dtypes.float8_e4m3fn, 7), "e5m2": (ml_dtypes.float8_e5m2, 14)}[fmt]
    v = np.moveaxis(np.asarray(x, np.float32).astype(ml_dtypes.bfloat16).astype(np.float64), axis, -1)
    blocks = v.reshape(v.shape[:-1] + (-1, 32))
    amax = np.abs(blocks).max(-1, keepdims=True)
    byte = np.maximum(np.where(amax > 0, np.frexp(amax)[1] - 1 + 127, 0) - down, 1)
    scale = np.exp2(byte - 127.0)
    codes = (blocks / scale).astype(np.float32).astype(dtype).astype(np.float64)
    return np.moveaxis((codes * scale).reshape(v.shape), -1, axis)


WIDE = False


def mx_kscale(k):
    if not WIDE:
        return np.ones(k)
    levels = np.array([10, -10, 5, -5, 0])
    a = np.random.permutation(np.resize(levels, k // 512 * 4)).reshape(k // 512, 4)
    idx = np.arange(k)
    return np.exp2(a[idx // 512, idx % 128 // 32])


BF16 = ml_dtypes.bfloat16


def bf(x):
    return np.asarray(x, np.float32).astype(BF16)


def f64(x):
    return np.asarray(x).astype(np.float64)


E2M1 = np.array([0.0, 0.5, 1.0, 1.5, 2.0, 3.0, 4.0, 6.0, -0.0, -0.5, -1.0, -1.5, -2.0, -3.0, -4.0, -6.0])


def pack_weight(w, fmt):
    k, n = w.shape
    w = f64(bf(w)).reshape(k // 32, 32, n)
    amax = np.abs(w).max(1)
    if fmt == "e4m3":
        byte = np.frexp(amax)[1] - 1 + 127 - 7
    else:
        mant, ex = np.frexp(amax / 6.0)
        byte = np.where(mant > 0.5, ex, ex - 1) + 127
    byte = np.clip(np.where(amax > 0, byte, 1), 1, 254)
    scaled = (w * np.exp2(127.0 - byte)[:, None, :]).reshape(k, n).astype(np.float32)
    by_word = np.ascontiguousarray(scaled.reshape(k // 512, 128, 4, n).transpose(0, 1, 3, 2))
    if fmt == "e4m3":
        words = by_word.astype(ml_dtypes.float8_e4m3fn).view(np.uint8)
    else:
        c = by_word.astype(ml_dtypes.float4_e2m1fn).view(np.uint8) & 0xF
        words = c[..., 0::2] | (c[..., 1::2] << 4)
    return np.ascontiguousarray(words), np.ascontiguousarray(byte.astype(np.uint8).reshape(k // 512, 16, n))


def unpack_weight(words, scales, fmt):
    g, p, n, _ = words.shape
    if fmt == "e4m3":
        vals = np.ascontiguousarray(words).view(ml_dtypes.float8_e4m3fn).astype(np.float64)
    else:
        nib = np.empty((g, p, n, 4), np.uint8)
        nib[..., 0::2] = words & 0xF
        nib[..., 1::2] = words >> 4
        vals = E2M1[nib]
    vals = vals * np.repeat(np.exp2(scales.astype(np.float64) - 127.0), 8, axis=1)[..., None]
    return vals.transpose(0, 1, 3, 2).reshape(g * 512, n)

def pack4(w):
    words, scales = pack_weight(w, "e2m1")
    return words.reshape(words.shape[0], 128, -1), scales


def unpack4(words, scales):
    return unpack_weight(words.reshape(words.shape[0], 128, -1, 2), scales, "e2m1")


B, N, D, H, HD, S, DO = 2, 4096, 1024, 2, 64, 11, 1024
E = H * HD
D4 = [0.4829629131445341, 0.8365163037378079, 0.2241438680420134, -0.1294095225512604]
T = len(D4)


def elu1(u):
    return np.where(u > 0.0, u, np.exp(np.minimum(u, 0.0)) - 1.0) + 1.0


def softplus(u):
    return np.log(1.0 + np.exp(u))


def shifted(t, o):
    if o == 0:
        return t
    return np.concatenate([np.zeros((B, H, o, HD)), t[:, :, :N - o, :]], axis=2)


def setup_inputs():
    s = mx_kscale(D)
    lg = np.random.standard_normal((B, H, N, S)) * 1.4
    g = np.exp(lg - lg.max(-1, keepdims=True))
    x = bf(np.random.standard_normal((B, N, D)) * s)
    w = np.random.standard_normal((3 * E, D)) * 0.6 / np.sqrt(D) / s
    words, scales = pack4(w.T)
    return {"x": x,
            "W_qkv_words": words,
            "W_qkv_scales": scales,
            "b_qkv": bf(np.random.standard_normal(3 * E) * 0.1),
            "gains": bf(g / g.sum(-1, keepdims=True)),
            "pos_bias": bf(np.random.standard_normal((S * T, H)) * 0.5),
            "identity_bypass": bf(-1.0 + 0.5 * np.random.standard_normal(H))}


def reference(x, W_qkv_words, W_qkv_scales, b_qkv, gains, pos_bias, identity_bypass):
    qkv = (mxq(f64(x), 2, "e4m3") @ unpack4(W_qkv_words, W_qkv_scales)) + f64(b_qkv)
    q, k, v = [t.reshape(B, N, H, HD).transpose(0, 2, 1, 3) for t in np.split(qkv, 3, axis=-1)]
    g, pb = f64(gains), f64(pos_bias)
    acc = np.zeros((B, H, N, HD))
    z = np.zeros((B, H, N, 1))
    tap = 0
    for j in range(S):
        d = 1 << j
        g_j = g[..., j][..., None]
        for tau, c in enumerate(D4):
            o = d * tau
            bias = pb[tap].reshape(1, H, 1, 1)
            tap += 1
            if o != 0 and o >= N:
                continue
            k_s, v_s = shifted(k, o), shifted(v, o)
            feat = elu1(np.sum(q * k_s, -1, keepdims=True) + bias)
            acc = acc + (g_j * c) * feat * v_s
            z = z + g_j * abs(c) * feat
    p = softplus(f64(identity_bypass)).reshape(1, H, 1, 1)
    local = elu1(np.sum(q * k, -1, keepdims=True))
    acc = acc + p * local * v
    z = z + p * local
    res = acc / (z + 1e-06)
    return res.transpose(0, 2, 1, 3).reshape(B, N, E)

@@ -1,0 +1,404 @@
+from contextlib import ExitStack
+
+import concourse.mybir as mybir
+from concourse.masks import make_identity
+
+F32 = mybir.dt.float32
+BF16 = mybir.dt.bfloat16
+U8 = mybir.dt.uint8
+U32 = mybir.dt.uint32
+I32 = mybir.dt.int32
+FP8X4 = mybir.dt.float8_e4m3fn_x4
+FP4X4 = mybir.dt.float4_e2m1fn_x4
+ALU = mybir.AluOpType
+ACT = mybir.ActivationFunctionType
+
+B, N, D, H, HD, S = 2, 4096, 1024, 2, 64, 11
+D4 = (0.4829629131445341, 0.8365163037378079, 0.2241438680420134, -0.1294095225512604)
+
+P = 128
+PACK = 4
+K_PASS = P * PACK
+PASSES = D // K_PASS
+CHUNK = 512
+BLOCKS = CHUNK // P
+PAD = P
+
+OFFSETS = tuple(1 << i for i in range(S + 1)) + tuple(3 << j for j in range(S)) + (0,)
+ZERO_COL = len(OFFSETS) - 1
+GROUP = S + 1
+TAUS = (1, 2, 3, 0)
+GROUP_COL = (0, 1, GROUP)
+SLOTS = GROUP * len(TAUS)
+LOCAL_SLOT = SLOTS - 1
+
+FLOPS = 2 * B * N * D * 3 * H * HD + B * H * N * (4 * S + 1) * 4 * HD
+
+
+def first_block(o, c0):
+    return min(BLOCKS, max(0, o // P - c0))
+
+
+def tile_dwarfattention_pa_t_kernel(
+    tc, x, W_qkv_words, W_qkv_scales, b_qkv, gains, pos_bias, identity_bypass, out
+):
+    nc = tc.nc
+    with ExitStack() as ctx:
+        const = ctx.enter_context(tc.tile_pool(name="const", bufs=1))
+        batch = ctx.enter_context(tc.tile_pool(name="batch", bufs=2))
+        xin = ctx.enter_context(tc.tile_pool(name="xin", bufs=2))
+        quant = ctx.enter_context(tc.tile_pool(name="quant", bufs=2))
+        prods = ctx.enter_context(tc.tile_pool(name="prods", bufs=4))
+        small = ctx.enter_context(tc.tile_pool(name="small", bufs=2))
+        psum_x = ctx.enter_context(tc.psum_pool(name="psum_x", bufs=2))
+        psum_q = ctx.enter_context(tc.psum_pool(name="psum_q", bufs=1))
+        psum_kv = ctx.enter_context(tc.psum_pool(name="psum_kv", bufs=1))
+        psum_s = ctx.enter_context(tc.psum_pool(name="psum_s", bufs=2))
+        psum_v = ctx.enter_context(tc.psum_pool(name="psum_v", bufs=2))
+
+        ident_f32 = const.tile([P, P], F32)
+        make_identity(nc, ident_f32[:])
+        ident_bf16 = const.tile([P, P], BF16)
+        make_identity(nc, ident_bf16[:])
+        zeros = const.tile([P, P], F32)
+        nc.vector.memset(zeros[:], 0.0)
+        one_col = const.tile([P, 1], F32)
+        nc.vector.memset(one_col[:], 1.0)
+        minus_one_col = const.tile([P, 1], F32)
+        nc.vector.memset(minus_one_col[:], -1.0)
+        head_of = const.tile([P, H], F32)
+        nc.vector.memset(head_of[:], 0.0)
+        for h in range(H):
+            nc.vector.memset(head_of[h * HD : (h + 1) * HD, h : h + 1], 1.0)
+
+        w_words = const.tile([P, PASSES, 2 * 3 * P], U8, align_bytes=64)
+        for g in range(PASSES):
+            nc.sync.dma_start(out=w_words[:, g, :].bitcast(I32), in_=W_qkv_words[g].bitcast(I32))
+        w_scales = const.tile([P, PASSES, 3 * P], U8, align_bytes=64)
+        nc.vector.memset(w_scales[:].bitcast(I32), 0)
+        for quadrant in range(4):
+            nc.sync.dma_start(
+                out=w_scales[32 * quadrant : 32 * quadrant + 4, :, :].bitcast(I32),
+                in_=W_qkv_scales[:, 4 * quadrant : 4 * quadrant + 4, :].rearrange("g r n -> r g n").bitcast(I32),
+            )
+
+        bias_rows = const.tile([P, P], BF16)
+        nc.vector.memset(bias_rows[:], 0.0)
+        nc.sync.dma_start(out=bias_rows[0:3, :], in_=b_qkv.rearrange("(r f) -> r f", f=P))
+        bias_ps = psum_x.tile([P, P], BF16, tag="xt")
+        nc.tensor.transpose(bias_ps[:], bias_rows[:], ident_bf16[:])
+        bias_col = const.tile([P, 3], F32)
+        nc.vector.tensor_copy(out=bias_col[:], in_=bias_ps[:, 0:3])
+
+        pos_bias_all = const.tile([P, 4 * S * H], BF16)
+        nc.sync.dma_start(out=pos_bias_all[:], in_=pos_bias.rearrange("r h -> (r h)").partition_broadcast(P))
+        bias_plus_1 = const.tile([P, H, SLOTS], F32)
+        nc.vector.memset(bias_plus_1[:], 1.0)
+        for group, tau in enumerate(TAUS):
+            nc.vector.tensor_scalar_add(
+                out=bias_plus_1[:, :, group * GROUP : group * GROUP + S],
+                in0=pos_bias_all[:].rearrange("p (j t h) -> p t h j", t=4, h=H)[:, tau],
+                scalar1=1.0,
+            )
+
+        bypass_bf16 = const.tile([P, H], BF16)
+        nc.sync.dma_start(out=bypass_bf16[:], in_=identity_bypass.partition_broadcast(P))
+        bypass = const.tile([P, H], F32)
+        nc.vector.tensor_copy(out=bypass[:], in_=bypass_bf16[:])
+        bypass_tail = const.tile([P, H], F32)
+        nc.scalar.activation(out=bypass_tail[:], in_=bypass[:], func=ACT.Abs)
+        nc.scalar.activation(out=bypass_tail[:], in_=bypass_tail[:], func=ACT.Exp, scale=-1.0)
+        nc.scalar.activation(out=bypass_tail[:], in_=bypass_tail[:], func=ACT.Ln, bias=one_col[:, 0:1])
+        local_gain = const.tile([P, H], F32)
+        nc.vector.scalar_tensor_tensor(
+            out=local_gain[:], in0=bypass[:], scalar=0.0, in1=bypass_tail[:], op0=ALU.max, op1=ALU.add
+        )
+
+        gains_rows = const.tile([P, P * S], BF16)
+        for b in range(B):
+            nc.sync.dma_start(
+                out=gains_rows[b * 64 : (b + 1) * 64, :],
+                in_=gains[b].rearrange("h (c p) j -> c h (p j)", p=P),
+            )
+        gains_by_scale = const.tile([P, S, P], BF16)
+        nc.vector.tensor_copy(out=gains_by_scale[:], in_=gains_rows[:].rearrange("r (p j) -> r j p", j=S))
+        slot_gain = const.tile([P, B * (N // P) * H, SLOTS], F32)
+        nc.gpsimd.memset(slot_gain[:], 0.0)
+        SCALES_PER_BANK = 8
+        for j0 in range(0, S, SCALES_PER_BANK):
+            scales_here = min(SCALES_PER_BANK, S - j0)
+            gains_ps = psum_x.tile([P, SCALES_PER_BANK, P], BF16, tag="xt")
+            for j in range(scales_here):
+                nc.tensor.transpose(gains_ps[:, j, :], gains_by_scale[:, j0 + j, :], ident_bf16[:])
+            for group, tau in enumerate(TAUS):
+                nc.vector.tensor_scalar_mul(
+                    out=slot_gain[:, :, group * GROUP + j0 : group * GROUP + j0 + scales_here],
+                    in0=gains_ps[:, 0:scales_here, :].rearrange("p j r -> p r j"),
+                    scalar1=abs(D4[tau]),
+                )
+        nc.vector.tensor_copy(
+            out=slot_gain[:].rearrange("p (c h) s -> p c h s", h=H)[:, :, :, LOCAL_SLOT],
+            in_=local_gain[:].unsqueeze(1).to_broadcast([P, B * (N // P), H]),
+        )
+
+        k_cols_of, v_cols_of, v_rows_of = {}, {}, {}
+        x_rows_of, grouped_of, q_ps_of, q_cols_of = {}, {}, {}, {}
+        dots_of, weight_of, one_over_z_of, acc_of = {}, {}, {}, {}
+        prod_of, shifted_of = {}, {}
+
+        def place(t):
+            b, chunk = divmod(t, N // CHUNK)
+            return b, chunk * CHUNK, chunk * BLOCKS
+
+        def load_x(t):
+            b, n0, c0 = place(t)
+            x_rows = xin.tile([P, BLOCKS, D], BF16)
+            nc.sync.dma_start(out=x_rows[:], in_=x[b, n0 : n0 + CHUNK, :].rearrange("(c p) d -> p c d", p=P))
+            x_rows_of[t] = x_rows
+
+        def transpose_x(t):
+            grouped = quant.tile([P, PASSES, CHUNK * PACK], BF16, align_bytes=64)
+            for g in range(PASSES):
+                grouped_words = grouped[:, g, :].bitcast(F32).rearrange("p (n u) -> p n u", u=2)
+                for half in range(2):
+                    xt = psum_x.tile([P, 2, 2 * P], F32)
+                    for c in range(2):
+                        words = x_rows_of[t][:, 2 * half + c, :].bitcast(F32)
+                        for u in range(2):
+                            nc.tensor.transpose(
+                                xt[:, u, c * P : (c + 1) * P],
+                                words[:, g * 2 * P + u : (g + 1) * 2 * P : 2],
+                                ident_f32[:],
+                            )
+                    nc.scalar.copy(
+                        out=grouped_words[:, half * 2 * P : (half + 1) * 2 * P, :],
+                        in_=xt[:].rearrange("p u n -> p n u"),
+                    )
+            grouped_of[t] = grouped
+
+        def project(t):
+            b, n0, c0 = place(t)
+            if n0 == 0:
+                k_cols = batch.tile([P, PAD + N], F32)
+                nc.vector.memset(k_cols[:, 0:PAD], 0.0)
+                v_cols = batch.tile([P, PAD + N], F32)
+                nc.vector.memset(v_cols[:, 0:PAD], 0.0)
+                v_rows = batch.tile([P, N // P, P], F32)
+                k_cols_of[b], v_cols_of[b], v_rows_of[b] = k_cols, v_cols, v_rows
+            x_codes = quant.tile([P, PASSES, CHUNK], U32, align_bytes=64)
+            x_scales = quant.tile([P, PASSES, CHUNK], U8, align_bytes=64)
+            for g in range(PASSES):
+                nc.vector.quantize_mx(
+                    out=x_codes[:, g, :].bitcast(FP8X4), scales=x_scales[:, g, :], in_=grouped_of[t][:, g, :]
+                )
+
+            def multiply(part, qkv_ps):
+                for g in range(PASSES):
+                    nc.tensor.matmul_mx(
+                        out=qkv_ps[:],
+                        lhsT=w_words[:, g, part * 2 * P : (part + 1) * 2 * P].bitcast(FP4X4),
+                        lhsT_scale=w_scales[:, g, part * P : (part + 1) * P],
+                        rhs=x_codes[:, g, :].bitcast(FP8X4),
+                        rhs_scale=x_scales[:, g, :],
+                        start=(g == 0),
+                        stop=(g == PASSES - 1),
+                    )
+
+            for part, cols in ((1, k_cols_of[b]), (2, v_cols_of[b])):
+                kv_ps = psum_kv.tile([P, CHUNK], F32)
+                multiply(part, kv_ps)
+                nc.scalar.activation(
+                    out=cols[:, PAD + n0 : PAD + n0 + CHUNK],
+                    in_=kv_ps[:],
+                    func=ACT.Identity,
+                    bias=bias_col[:, part : part + 1],
+                )
+            q_ps = psum_q.tile([P, CHUNK], F32)
+            multiply(0, q_ps)
+            q_cols = small.tile([P, CHUNK], F32)
+            nc.scalar.activation(out=q_cols[:], in_=q_ps[:], func=ACT.Identity, bias=bias_col[:, 0:1])
+            q_ps_of[t], q_cols_of[t] = q_ps, q_cols
+
+            v_ps = psum_v.tile([P, BLOCKS, P], F32)
+            for c in range(BLOCKS):
+                nc.tensor.transpose(
+                    v_ps[:, c, :], v_cols_of[b][:, PAD + n0 + c * P : PAD + n0 + (c + 1) * P], ident_f32[:]
+                )
+            nc.scalar.copy(out=v_rows_of[b][:, c0 : c0 + BLOCKS, :], in_=v_ps[:])
+            dots_ps = psum_s.tile([P, BLOCKS, H, len(OFFSETS)], F32)
+            dots_of[t] = dots_ps
+
+        def product(t, col):
+            b, n0, c0 = place(t)
+            o = OFFSETS[col]
+            first = first_block(o, c0)
+            if first == BLOCKS:
+                return
+            keys = k_cols_of[b][:, PAD + n0 + first * P - o : PAD + n0 + CHUNK - o]
+            if col % 2 == 0:
+                prod = prods.tile([P, CHUNK], F32, tag="prod_vector")
+                nc.vector.scalar_tensor_tensor(
+                    out=prod[:, first * P :],
+                    in0=q_ps_of[t][:, first * P :],
+                    scalar=bias_col[:, 0:1],
+                    in1=keys,
+                    op0=ALU.add,
+                    op1=ALU.mult,
+                )
+            else:
+                prod = prods.tile([P, CHUNK], F32, tag="prod_gpsimd")
+                nc.gpsimd.tensor_tensor(out=prod[:, first * P :], in0=q_cols_of[t][:, first * P :], in1=keys, op=ALU.mult)
+            prod_of[t, col] = prod
+
+        def head_sums(t, col):
+            b, n0, c0 = place(t)
+            first = first_block(OFFSETS[col], c0)
+            if first > 0:
+                nc.tensor.matmul(
+                    out=dots_of[t][:, 0:first, :, col],
+                    lhsT=zeros[:],
+                    rhs=zeros[:, 0 : first * H].rearrange("p (c h) -> p c h", h=H),
+                    start=True,
+                    stop=True,
+                )
+            for c in range(first, BLOCKS):
+                nc.tensor.matmul(
+                    out=dots_of[t][:, c, :, col],
+                    lhsT=prod_of[t, col][:, c * P : (c + 1) * P],
+                    rhs=head_of[:],
+                    start=True,
+                    stop=True,
+                )
+
+        def weights(t):
+            b, n0, c0 = place(t)
+            dots_ps = dots_of[t]
+            u1 = small.tile([P, BLOCKS, H, SLOTS], F32)
+            bias_view = bias_plus_1[:].unsqueeze(1).to_broadcast([P, BLOCKS, H, SLOTS])
+            for group, first_col in enumerate(GROUP_COL):
+                nc.vector.tensor_tensor(
+                    out=u1[:, :, :, group * GROUP : (group + 1) * GROUP],
+                    in0=dots_ps[:, :, :, first_col : first_col + GROUP],
+                    in1=bias_view[:, :, :, group * GROUP : (group + 1) * GROUP],
+                    op=ALU.add,
+                )
+            nc.vector.tensor_tensor(
+                out=u1[:, :, :, SLOTS - GROUP :],
+                in0=dots_ps[:, :, :, ZERO_COL : ZERO_COL + 1].to_broadcast([P, BLOCKS, H, GROUP]),
+                in1=bias_view[:, :, :, SLOTS - GROUP :],
+                op=ALU.add,
+            )
+            exp_u = small.tile([P, BLOCKS, H, SLOTS], F32)
+            nc.scalar.activation(out=exp_u[:], in_=u1[:], func=ACT.Exp, bias=minus_one_col[:, 0:1])
+            feat = small.tile([P, BLOCKS * H, SLOTS], F32)
+            nc.vector.scalar_tensor_tensor(
+                out=feat[:].rearrange("p r s -> p (r s)"),
+                in0=exp_u[:].rearrange("p c h s -> p (c h s)"),
+                scalar=1.0,
+                in1=u1[:].rearrange("p c h s -> p (c h s)"),
+                op0=ALU.min,
+                op1=ALU.max,
+            )
+            share = small.tile([P, BLOCKS * H, SLOTS], F32)
+            r0 = (b * (N // P) + c0) * H
+            nc.vector.tensor_tensor(out=share[:], in0=feat[:], in1=slot_gain[:, r0 : r0 + BLOCKS * H, :], op=ALU.mult)
+            weight = small.tile([P, BLOCKS * H, len(OFFSETS)], F32)
+            nc.vector.tensor_reduce(
+                out=weight[:, :, ZERO_COL], in_=share[:, :, SLOTS - GROUP :], axis=mybir.AxisListType.X, op=ALU.add
+            )
+            nc.vector.tensor_tensor(
+                out=weight[:, :, 0:GROUP],
+                in0=share[:, :, 0:GROUP],
+                in1=share[:, :, GROUP - 1 : 2 * GROUP - 1],
+                op=ALU.add,
+            )
+            nc.vector.tensor_scalar_mul(
+                out=weight[:, :, GROUP : GROUP + S], in0=share[:, :, 2 * GROUP : 2 * GROUP + S], scalar1=-1.0
+            )
+            z = small.tile([P, BLOCKS * H], F32)
+            nc.vector.tensor_reduce(out=z[:], in_=share[:], axis=mybir.AxisListType.X, op=ALU.add)
+            nc.vector.tensor_scalar_add(out=z[:], in0=z[:], scalar1=1e-06)
+            one_over_z = small.tile([P, BLOCKS * H], F32)
+            nc.vector.reciprocal(out=one_over_z[:], in_=z[:])
+            weight_of[t], one_over_z_of[t] = weight, one_over_z
+
+        def shifted_v(t, col):
+            b, n0, c0 = place(t)
+            o = OFFSETS[col]
+            first = first_block(o, c0)
+            if o % P == 0 or first == BLOCKS:
+                return
+            v_ps = psum_v.tile([P, BLOCKS, P], F32)
+            for c in range(first, BLOCKS):
+                start_col = PAD + n0 + c * P - o
+                nc.tensor.transpose(v_ps[:, c, :], v_cols_of[b][:, start_col : start_col + P], ident_f32[:])
+            shifted_of[t, col] = v_ps
+
+        def mix(t, col):
+            b, n0, c0 = place(t)
+            o = OFFSETS[col]
+            if col == ZERO_COL:
+                acc = small.tile([P, BLOCKS * H, HD], F32)
+                acc_of[t] = acc
+            acc = acc_of[t]
+            for c in range(first_block(o, c0), BLOCKS):
+                v_block = v_rows_of[b][:, c0 + c - o // P, :] if o % P == 0 else shifted_of[t, col][:, c, :]
+                for h in range(H):
+                    r = c * H + h
+                    if col == ZERO_COL:
+                        nc.vector.tensor_scalar_mul(
+                            out=acc[:, r, :],
+                            in0=v_block[:, h * HD : (h + 1) * HD],
+                            scalar1=weight_of[t][:, r, col : col + 1],
+                        )
+                    else:
+                        nc.vector.scalar_tensor_tensor(
+                            out=acc[:, r, :],
+                            in0=v_block[:, h * HD : (h + 1) * HD],
+                            scalar=weight_of[t][:, r, col : col + 1],
+                            in1=acc[:, r, :],
+                            op0=ALU.mult,
+                            op1=ALU.add,
+                        )
+
+        def finish(t):
+            b, n0, c0 = place(t)
+            result = small.tile([P, BLOCKS * H, HD], F32)
+            for r in range(BLOCKS * H):
+                nc.scalar.activation(
+                    out=result[:, r, :], in_=acc_of[t][:, r, :], func=ACT.Copy, scale=one_over_z_of[t][:, r : r + 1]
+                )
+            nc.sync.dma_start(
+                out=out[b, n0 : n0 + CHUNK, :].rearrange("(c p) f -> p c f", p=P),
+                in_=result[:].rearrange("p (c h) d -> p c (h d)", h=H),
+            )
+
+        CHUNKS = B * N // CHUNK
+        MIX_ORDER = (ZERO_COL,) + tuple(range(ZERO_COL))
+        SUM_LAG = 2
+
+        def when(stage, t, *args):
+            if 0 <= t < CHUNKS:
+                stage(t, *args)
+
+        with tc.manual_schedule():
+            load_x(0)
+            load_x(1)
+            transpose_x(0)
+            load_x(2)
+            project(0)
+            for t in range(-1, CHUNKS):
+                when(transpose_x, t + 2)
+                when(load_x, t + 4)
+                for step in range(len(OFFSETS)):
+                    when(product, t + 1, step)
+                    if step + 1 < len(OFFSETS):
+                        when(shifted_v, t, MIX_ORDER[step + 1])
+                    when(mix, t, MIX_ORDER[step])
+                    if step >= SUM_LAG:
+                        when(head_sums, t + 1, step - SUM_LAG)
+                for step in range(len(OFFSETS) - SUM_LAG, len(OFFSETS)):
+                    when(head_sums, t + 1, step)
+                when(finish, t)
+                when(project, t + 2)
+                when(weights, t + 1)

@@ -22,10 +22,13 @@ K_PASS = P * PACK
 PASSES = D // K_PASS
 CHUNK = 512
 BLOCKS = CHUNK // P
+CHUNKS = B * N // CHUNK
+ROWS = BLOCKS * H
 PAD = P
 
 OFFSETS = tuple(1 << i for i in range(S + 1)) + tuple(3 << j for j in range(S)) + (0,)
 ZERO_COL = len(OFFSETS) - 1
+MIX_ORDER = (ZERO_COL,) + tuple(range(ZERO_COL))
 GROUP = S + 1
 TAUS = (1, 2, 3, 0)
 GROUP_COL = (0, 1, GROUP)
@@ -48,29 +51,22 @@ def tile_dwarfattention_pa_t_kernel(
         batch = ctx.enter_context(tc.tile_pool(name="batch", bufs=2))
         xin = ctx.enter_context(tc.tile_pool(name="xin", bufs=2))
         quant = ctx.enter_context(tc.tile_pool(name="quant", bufs=2))
-        prods = ctx.enter_context(tc.tile_pool(name="prods", bufs=4))
+        prods = ctx.enter_context(tc.tile_pool(name="prods", bufs=3))
         small = ctx.enter_context(tc.tile_pool(name="small", bufs=2))
         psum_x = ctx.enter_context(tc.psum_pool(name="psum_x", bufs=2))
         psum_q = ctx.enter_context(tc.psum_pool(name="psum_q", bufs=1))
         psum_kv = ctx.enter_context(tc.psum_pool(name="psum_kv", bufs=1))
-        psum_s = ctx.enter_context(tc.psum_pool(name="psum_s", bufs=2))
+        psum_p = ctx.enter_context(tc.psum_pool(name="psum_p", bufs=2))
         psum_v = ctx.enter_context(tc.psum_pool(name="psum_v", bufs=2))
 
         ident_f32 = const.tile([P, P], F32)
         make_identity(nc, ident_f32[:])
         ident_bf16 = const.tile([P, P], BF16)
         make_identity(nc, ident_bf16[:])
-        zeros = const.tile([P, P], F32)
-        nc.vector.memset(zeros[:], 0.0)
         one_col = const.tile([P, 1], F32)
         nc.vector.memset(one_col[:], 1.0)
         minus_one_col = const.tile([P, 1], F32)
         nc.vector.memset(minus_one_col[:], -1.0)
-        head_of = const.tile([P, H], F32)
-        nc.vector.memset(head_of[:], 0.0)
-        for h in range(H):
-            nc.vector.memset(head_of[h * HD : (h + 1) * HD, h : h + 1], 1.0)
-
         w_words = const.tile([P, PASSES, 2 * 3 * P], U8, align_bytes=64)
         for g in range(PASSES):
             nc.sync.dma_start(out=w_words[:, g, :].bitcast(I32), in_=W_qkv_words[g].bitcast(I32))
@@ -92,12 +88,12 @@ def tile_dwarfattention_pa_t_kernel(
 
         pos_bias_all = const.tile([P, 4 * S * H], BF16)
         nc.sync.dma_start(out=pos_bias_all[:], in_=pos_bias.rearrange("r h -> (r h)").partition_broadcast(P))
-        bias_plus_1 = const.tile([P, H, SLOTS], F32)
+        bias_plus_1 = const.tile([P, SLOTS, H], F32)
         nc.vector.memset(bias_plus_1[:], 1.0)
         for group, tau in enumerate(TAUS):
             nc.vector.tensor_scalar_add(
-                out=bias_plus_1[:, :, group * GROUP : group * GROUP + S],
-                in0=pos_bias_all[:].rearrange("p (j t h) -> p t h j", t=4, h=H)[:, tau],
+                out=bias_plus_1[:, group * GROUP : group * GROUP + S, :],
+                in0=pos_bias_all[:].rearrange("p (j t h) -> p t j h", t=4, h=H)[:, tau],
                 scalar1=1.0,
             )
 
@@ -122,7 +118,7 @@ def tile_dwarfattention_pa_t_kernel(
             )
         gains_by_scale = const.tile([P, S, P], BF16)
         nc.vector.tensor_copy(out=gains_by_scale[:], in_=gains_rows[:].rearrange("r (p j) -> r j p", j=S))
-        slot_gain = const.tile([P, B * (N // P) * H, SLOTS], F32)
+        slot_gain = const.tile([P, CHUNKS, SLOTS, ROWS], F32)
         nc.gpsimd.memset(slot_gain[:], 0.0)
         SCALES_PER_BANK = 8
         for j0 in range(0, S, SCALES_PER_BANK):
@@ -132,31 +128,31 @@ def tile_dwarfattention_pa_t_kernel(
                 nc.tensor.transpose(gains_ps[:, j, :], gains_by_scale[:, j0 + j, :], ident_bf16[:])
             for group, tau in enumerate(TAUS):
                 nc.vector.tensor_scalar_mul(
-                    out=slot_gain[:, :, group * GROUP + j0 : group * GROUP + j0 + scales_here],
-                    in0=gains_ps[:, 0:scales_here, :].rearrange("p j r -> p r j"),
+                    out=slot_gain[:, :, group * GROUP + j0 : group * GROUP + j0 + scales_here, :],
+                    in0=gains_ps[:, 0:scales_here, :].rearrange("p j (t r) -> p t j r", r=ROWS),
                     scalar1=abs(D4[tau]),
                 )
         nc.vector.tensor_copy(
-            out=slot_gain[:].rearrange("p (c h) s -> p c h s", h=H)[:, :, :, LOCAL_SLOT],
-            in_=local_gain[:].unsqueeze(1).to_broadcast([P, B * (N // P), H]),
+            out=slot_gain[:, :, LOCAL_SLOT, :].rearrange("p t (c h) -> p t c h", h=H),
+            in_=local_gain[:].unsqueeze(1).unsqueeze(1).to_broadcast([P, CHUNKS, BLOCKS, H]),
         )
 
         k_cols_of, v_cols_of, v_rows_of = {}, {}, {}
         x_rows_of, grouped_of, q_ps_of, q_cols_of = {}, {}, {}, {}
         dots_of, weight_of, one_over_z_of, acc_of = {}, {}, {}, {}
-        prod_of, shifted_of = {}, {}
+        prod_of, prod_rows_of, shifted_of = {}, {}, {}
 
         def place(t):
             b, chunk = divmod(t, N // CHUNK)
             return b, chunk * CHUNK, chunk * BLOCKS
 
-        def load_x(t):
+        def load_x(t, step=0):
             b, n0, c0 = place(t)
             x_rows = xin.tile([P, BLOCKS, D], BF16)
             nc.sync.dma_start(out=x_rows[:], in_=x[b, n0 : n0 + CHUNK, :].rearrange("(c p) d -> p c d", p=P))
             x_rows_of[t] = x_rows
 
-        def transpose_x(t):
+        def transpose_x(t, step=0):
             grouped = quant.tile([P, PASSES, CHUNK * PACK], BF16, align_bytes=64)
             for g in range(PASSES):
                 grouped_words = grouped[:, g, :].bitcast(F32).rearrange("p (n u) -> p n u", u=2)
@@ -176,7 +172,7 @@ def tile_dwarfattention_pa_t_kernel(
                     )
             grouped_of[t] = grouped
 
-        def project(t):
+        def project(t, step=0):
             b, n0, c0 = place(t)
             if n0 == 0:
                 k_cols = batch.tile([P, PAD + N], F32)
@@ -225,8 +221,12 @@ def tile_dwarfattention_pa_t_kernel(
                     v_ps[:, c, :], v_cols_of[b][:, PAD + n0 + c * P : PAD + n0 + (c + 1) * P], ident_f32[:]
                 )
             nc.scalar.copy(out=v_rows_of[b][:, c0 : c0 + BLOCKS, :], in_=v_ps[:])
-            dots_ps = psum_s.tile([P, BLOCKS, H, len(OFFSETS)], F32)
-            dots_of[t] = dots_ps
+            dots = small.tile([P, len(OFFSETS), ROWS], F32)
+            nc.gpsimd.memset(dots[:], 0.0)
+            dots_of[t] = dots
+
+        def on_vector(col):
+            return col % 3 == 0
 
         def product(t, col):
             b, n0, c0 = place(t)
@@ -235,7 +235,7 @@ def tile_dwarfattention_pa_t_kernel(
             if first == BLOCKS:
                 return
             keys = k_cols_of[b][:, PAD + n0 + first * P - o : PAD + n0 + CHUNK - o]
-            if col % 2 == 0:
+            if on_vector(col):
                 prod = prods.tile([P, CHUNK], F32, tag="prod_vector")
                 nc.vector.scalar_tensor_tensor(
                     out=prod[:, first * P :],
@@ -250,80 +250,89 @@ def tile_dwarfattention_pa_t_kernel(
                 nc.gpsimd.tensor_tensor(out=prod[:, first * P :], in0=q_cols_of[t][:, first * P :], in1=keys, op=ALU.mult)
             prod_of[t, col] = prod
 
-        def head_sums(t, col):
+        def transpose_product(t, col):
             b, n0, c0 = place(t)
             first = first_block(OFFSETS[col], c0)
-            if first > 0:
-                nc.tensor.matmul(
-                    out=dots_of[t][:, 0:first, :, col],
-                    lhsT=zeros[:],
-                    rhs=zeros[:, 0 : first * H].rearrange("p (c h) -> p c h", h=H),
-                    start=True,
-                    stop=True,
-                )
+            if first == BLOCKS:
+                return
+            prod_rows = psum_p.tile([P, BLOCKS, P], F32)
             for c in range(first, BLOCKS):
-                nc.tensor.matmul(
-                    out=dots_of[t][:, c, :, col],
-                    lhsT=prod_of[t, col][:, c * P : (c + 1) * P],
-                    rhs=head_of[:],
-                    start=True,
-                    stop=True,
-                )
+                nc.tensor.transpose(prod_rows[:, c, :], prod_of[t, col][:, c * P : (c + 1) * P], ident_f32[:])
+            prod_rows_of[t, col] = prod_rows
 
-        def weights(t):
+        def sum_heads(t, col):
             b, n0, c0 = place(t)
-            dots_ps = dots_of[t]
-            u1 = small.tile([P, BLOCKS, H, SLOTS], F32)
-            bias_view = bias_plus_1[:].unsqueeze(1).to_broadcast([P, BLOCKS, H, SLOTS])
-            for group, first_col in enumerate(GROUP_COL):
-                nc.vector.tensor_tensor(
-                    out=u1[:, :, :, group * GROUP : (group + 1) * GROUP],
-                    in0=dots_ps[:, :, :, first_col : first_col + GROUP],
-                    in1=bias_view[:, :, :, group * GROUP : (group + 1) * GROUP],
+            first = first_block(OFFSETS[col], c0)
+            if first == BLOCKS:
+                return
+            by_head = prod_rows_of[t, col][:].rearrange("p c (h d) -> p (c h) d", h=H)
+            if on_vector(col):
+                nc.vector.tensor_reduce(
+                    out=dots_of[t][:, col, first * H :],
+                    in_=by_head[:, first * H :, :],
+                    axis=mybir.AxisListType.X,
                     op=ALU.add,
                 )
-            nc.vector.tensor_tensor(
-                out=u1[:, :, :, SLOTS - GROUP :],
-                in0=dots_ps[:, :, :, ZERO_COL : ZERO_COL + 1].to_broadcast([P, BLOCKS, H, GROUP]),
-                in1=bias_view[:, :, :, SLOTS - GROUP :],
-                op=ALU.add,
-            )
-            exp_u = small.tile([P, BLOCKS, H, SLOTS], F32)
+            else:
+                unused = prods.tile([P, ROWS, HD], F32)
+                for r in range(first * H, ROWS):
+                    nc.scalar.activation(
+                        out=unused[:, r, :], in_=by_head[:, r, :], func=ACT.Copy, accum_out=dots_of[t][:, col, r : r + 1]
+                    )
+
+        def weights(t, step=0):
+            dots = dots_of[t]
+            u1 = small.tile([P, SLOTS, ROWS], F32)
+            for group in range(len(TAUS)):
+                slots = slice(group * GROUP, (group + 1) * GROUP)
+                if group < len(GROUP_COL):
+                    dots_read = dots[:, GROUP_COL[group] : GROUP_COL[group] + GROUP, :]
+                else:
+                    dots_read = dots[:, ZERO_COL : ZERO_COL + 1, :].to_broadcast([P, GROUP, ROWS])
+                nc.vector.tensor_tensor(
+                    out=u1[:, slots, :].rearrange("p s (c h) -> p s c h", h=H),
+                    in0=dots_read.rearrange("p s (c h) -> p s c h", h=H),
+                    in1=bias_plus_1[:, slots, :].unsqueeze(2).to_broadcast([P, GROUP, BLOCKS, H]),
+                    op=ALU.add,
+                )
+            exp_u = small.tile([P, SLOTS, ROWS], F32)
             nc.scalar.activation(out=exp_u[:], in_=u1[:], func=ACT.Exp, bias=minus_one_col[:, 0:1])
-            feat = small.tile([P, BLOCKS * H, SLOTS], F32)
+            feat = small.tile([P, SLOTS, ROWS], F32)
             nc.vector.scalar_tensor_tensor(
-                out=feat[:].rearrange("p r s -> p (r s)"),
-                in0=exp_u[:].rearrange("p c h s -> p (c h s)"),
+                out=feat[:].rearrange("p s r -> p (s r)"),
+                in0=exp_u[:].rearrange("p s r -> p (s r)"),
                 scalar=1.0,
-                in1=u1[:].rearrange("p c h s -> p (c h s)"),
+                in1=u1[:].rearrange("p s r -> p (s r)"),
                 op0=ALU.min,
                 op1=ALU.max,
             )
-            share = small.tile([P, BLOCKS * H, SLOTS], F32)
-            r0 = (b * (N // P) + c0) * H
-            nc.vector.tensor_tensor(out=share[:], in0=feat[:], in1=slot_gain[:, r0 : r0 + BLOCKS * H, :], op=ALU.mult)
-            weight = small.tile([P, BLOCKS * H, len(OFFSETS)], F32)
+            share = small.tile([P, SLOTS, ROWS], F32)
+            nc.vector.tensor_tensor(out=share[:], in0=feat[:], in1=slot_gain[:, t, :, :], op=ALU.mult)
+            weight = small.tile([P, len(OFFSETS), ROWS], F32)
             nc.vector.tensor_reduce(
-                out=weight[:, :, ZERO_COL], in_=share[:, :, SLOTS - GROUP :], axis=mybir.AxisListType.X, op=ALU.add
-            )
-            nc.vector.tensor_tensor(
-                out=weight[:, :, 0:GROUP],
-                in0=share[:, :, 0:GROUP],
-                in1=share[:, :, GROUP - 1 : 2 * GROUP - 1],
+                out=weight[:, ZERO_COL, :],
+                in_=share[:, SLOTS - GROUP :, :].rearrange("p s r -> p r s"),
+                axis=mybir.AxisListType.X,
                 op=ALU.add,
             )
-            nc.vector.tensor_scalar_mul(
-                out=weight[:, :, GROUP : GROUP + S], in0=share[:, :, 2 * GROUP : 2 * GROUP + S], scalar1=-1.0
+            nc.vector.tensor_tensor(
+                out=weight[:, 0:GROUP, :], in0=share[:, 0:GROUP, :], in1=share[:, GROUP - 1 : 2 * GROUP - 1, :], op=ALU.add
             )
-            z = small.tile([P, BLOCKS * H], F32)
-            nc.vector.tensor_reduce(out=z[:], in_=share[:], axis=mybir.AxisListType.X, op=ALU.add)
+            nc.vector.tensor_scalar_mul(
+                out=weight[:, GROUP : GROUP + S, :], in0=share[:, 2 * GROUP : 2 * GROUP + S, :], scalar1=-1.0
+            )
+            z = small.tile([P, ROWS], F32)
+            nc.vector.tensor_reduce(
+                out=z[:], in_=share[:].rearrange("p s r -> p r s"), axis=mybir.AxisListType.X, op=ALU.add
+            )
             nc.vector.tensor_scalar_add(out=z[:], in0=z[:], scalar1=1e-06)
-            one_over_z = small.tile([P, BLOCKS * H], F32)
+            one_over_z = small.tile([P, ROWS], F32)
             nc.vector.reciprocal(out=one_over_z[:], in_=z[:])
             weight_of[t], one_over_z_of[t] = weight, one_over_z
 
-        def shifted_v(t, col):
+        def shifted_v(t, step):
             b, n0, c0 = place(t)
+            col = MIX_ORDER[step]
             o = OFFSETS[col]
             first = first_block(o, c0)
             if o % P == 0 or first == BLOCKS:
@@ -334,11 +343,12 @@ def tile_dwarfattention_pa_t_kernel(
                 nc.tensor.transpose(v_ps[:, c, :], v_cols_of[b][:, start_col : start_col + P], ident_f32[:])
             shifted_of[t, col] = v_ps
 
-        def mix(t, col):
+        def mix(t, step):
             b, n0, c0 = place(t)
+            col = MIX_ORDER[step]
             o = OFFSETS[col]
             if col == ZERO_COL:
-                acc = small.tile([P, BLOCKS * H, HD], F32)
+                acc = small.tile([P, ROWS, HD], F32)
                 acc_of[t] = acc
             acc = acc_of[t]
             for c in range(first_block(o, c0), BLOCKS):
@@ -349,22 +359,22 @@ def tile_dwarfattention_pa_t_kernel(
                         nc.vector.tensor_scalar_mul(
                             out=acc[:, r, :],
                             in0=v_block[:, h * HD : (h + 1) * HD],
-                            scalar1=weight_of[t][:, r, col : col + 1],
+                            scalar1=weight_of[t][:, col, r : r + 1],
                         )
                     else:
                         nc.vector.scalar_tensor_tensor(
                             out=acc[:, r, :],
                             in0=v_block[:, h * HD : (h + 1) * HD],
-                            scalar=weight_of[t][:, r, col : col + 1],
+                            scalar=weight_of[t][:, col, r : r + 1],
                             in1=acc[:, r, :],
                             op0=ALU.mult,
                             op1=ALU.add,
                         )
 
-        def finish(t):
+        def finish(t, step=0):
             b, n0, c0 = place(t)
-            result = small.tile([P, BLOCKS * H, HD], F32)
-            for r in range(BLOCKS * H):
+            result = small.tile([P, ROWS, HD], F32)
+            for r in range(ROWS):
                 nc.scalar.activation(
                     out=result[:, r, :], in_=acc_of[t][:, r, :], func=ACT.Copy, scale=one_over_z_of[t][:, r : r + 1]
                 )
@@ -373,13 +383,9 @@ def tile_dwarfattention_pa_t_kernel(
                 in_=result[:].rearrange("p (c h) d -> p c (h d)", h=H),
             )
 
-        CHUNKS = B * N // CHUNK
-        MIX_ORDER = (ZERO_COL,) + tuple(range(ZERO_COL))
-        SUM_LAG = 2
-
-        def when(stage, t, *args):
-            if 0 <= t < CHUNKS:
-                stage(t, *args)
+        def when(stage, t, step=0):
+            if 0 <= t < CHUNKS and 0 <= step < len(OFFSETS):
+                stage(t, step)
 
         with tc.manual_schedule():
             load_x(0)
@@ -390,15 +396,12 @@ def tile_dwarfattention_pa_t_kernel(
             for t in range(-1, CHUNKS):
                 when(transpose_x, t + 2)
                 when(load_x, t + 4)
-                for step in range(len(OFFSETS)):
+                for step in range(len(OFFSETS) + 2):
                     when(product, t + 1, step)
-                    if step + 1 < len(OFFSETS):
-                        when(shifted_v, t, MIX_ORDER[step + 1])
-                    when(mix, t, MIX_ORDER[step])
-                    if step >= SUM_LAG:
-                        when(head_sums, t + 1, step - SUM_LAG)
-                for step in range(len(OFFSETS) - SUM_LAG, len(OFFSETS)):
-                    when(head_sums, t + 1, step)
+                    when(transpose_product, t + 1, step - 1)
+                    when(shifted_v, t, step + 1)
+                    when(sum_heads, t + 1, step - 2)
+                    when(mix, t, step)
                 when(finish, t)
                 when(project, t + 2)
                 when(weights, t + 1)

@@ -24,11 +24,12 @@ CHUNK = 512
 BLOCKS = CHUNK // P
 CHUNKS = B * N // CHUNK
 ROWS = BLOCKS * H
-PAD = P
 
 OFFSETS = tuple(1 << i for i in range(S + 1)) + tuple(3 << j for j in range(S)) + (0,)
 ZERO_COL = len(OFFSETS) - 1
-MIX_ORDER = (ZERO_COL,) + tuple(range(ZERO_COL))
+NEAR_COLS = tuple(col for col, o in enumerate(OFFSETS) if o % P != 0)
+FAR_COLS = tuple(col for col, o in enumerate(OFFSETS) if o % P == 0)
+HALO = max(OFFSETS[col] for col in NEAR_COLS)
 GROUP = S + 1
 TAUS = (1, 2, 3, 0)
 GROUP_COL = (0, 1, GROUP)
@@ -38,8 +39,19 @@ LOCAL_SLOT = SLOTS - 1
 FLOPS = 2 * B * N * D * 3 * H * HD + B * H * N * (4 * S + 1) * 4 * HD
 
 
-def first_block(o, c0):
-    return min(BLOCKS, max(0, o // P - c0))
+def alternate(first, second):
+    mixed = []
+    for i in range(max(len(first), len(second))):
+        mixed.extend(first[i : i + 1])
+        mixed.extend(second[i : i + 1])
+    return tuple(mixed)
+
+
+ORDER = (ZERO_COL,) + alternate(NEAR_COLS, FAR_COLS[:-1])
+
+
+def first_block(col, c0):
+    return min(BLOCKS, max(0, OFFSETS[col] // P - c0)) if col in FAR_COLS else 0
 
 
 def tile_dwarfattention_pa_t_kernel(
@@ -51,11 +63,11 @@ def tile_dwarfattention_pa_t_kernel(
         batch = ctx.enter_context(tc.tile_pool(name="batch", bufs=2))
         xin = ctx.enter_context(tc.tile_pool(name="xin", bufs=2))
         quant = ctx.enter_context(tc.tile_pool(name="quant", bufs=2))
+        cols = ctx.enter_context(tc.tile_pool(name="cols", bufs=3))
         prods = ctx.enter_context(tc.tile_pool(name="prods", bufs=3))
         small = ctx.enter_context(tc.tile_pool(name="small", bufs=2))
         psum_x = ctx.enter_context(tc.psum_pool(name="psum_x", bufs=2))
-        psum_q = ctx.enter_context(tc.psum_pool(name="psum_q", bufs=1))
-        psum_kv = ctx.enter_context(tc.psum_pool(name="psum_kv", bufs=1))
+        psum_mx = ctx.enter_context(tc.psum_pool(name="psum_mx", bufs=2))
         psum_p = ctx.enter_context(tc.psum_pool(name="psum_p", bufs=2))
         psum_v = ctx.enter_context(tc.psum_pool(name="psum_v", bufs=2))
 
@@ -137,8 +149,9 @@ def tile_dwarfattention_pa_t_kernel(
             in_=local_gain[:].unsqueeze(1).unsqueeze(1).to_broadcast([P, CHUNKS, BLOCKS, H]),
         )
 
-        k_cols_of, v_cols_of, v_rows_of = {}, {}, {}
-        x_rows_of, grouped_of, q_ps_of, q_cols_of = {}, {}, {}, {}
+        k_rows_of, v_rows_of = {}, {}
+        x_rows_of, grouped_of = {}, {}
+        q_cols_of, k_cols_of, v_cols_of, q_rows_of = {}, {}, {}, {}
         dots_of, weight_of, one_over_z_of, acc_of = {}, {}, {}, {}
         prod_of, prod_rows_of, shifted_of = {}, {}, {}
 
@@ -146,13 +159,13 @@ def tile_dwarfattention_pa_t_kernel(
             b, chunk = divmod(t, N // CHUNK)
             return b, chunk * CHUNK, chunk * BLOCKS
 
-        def load_x(t, step=0):
+        def load_x(t, col=0):
             b, n0, c0 = place(t)
             x_rows = xin.tile([P, BLOCKS, D], BF16)
             nc.sync.dma_start(out=x_rows[:], in_=x[b, n0 : n0 + CHUNK, :].rearrange("(c p) d -> p c d", p=P))
             x_rows_of[t] = x_rows
 
-        def transpose_x(t, step=0):
+        def transpose_x(t, col=0):
             grouped = quant.tile([P, PASSES, CHUNK * PACK], BF16, align_bytes=64)
             for g in range(PASSES):
                 grouped_words = grouped[:, g, :].bitcast(F32).rearrange("p (n u) -> p n u", u=2)
@@ -172,23 +185,34 @@ def tile_dwarfattention_pa_t_kernel(
                     )
             grouped_of[t] = grouped
 
-        def project(t, step=0):
+        def to_rows(columns, rows):
+            rows_ps = psum_v.tile([P, BLOCKS, P], F32)
+            for c in range(BLOCKS):
+                nc.tensor.transpose(rows_ps[:, c, :], columns[:, c * P : (c + 1) * P], ident_f32[:])
+            nc.scalar.copy(out=rows, in_=rows_ps[:])
+
+        def project(t, col=0):
             b, n0, c0 = place(t)
             if n0 == 0:
-                k_cols = batch.tile([P, PAD + N], F32)
-                nc.vector.memset(k_cols[:, 0:PAD], 0.0)
-                v_cols = batch.tile([P, PAD + N], F32)
-                nc.vector.memset(v_cols[:, 0:PAD], 0.0)
+                k_rows = batch.tile([P, N // P, P], F32)
                 v_rows = batch.tile([P, N // P, P], F32)
-                k_cols_of[b], v_cols_of[b], v_rows_of[b] = k_cols, v_cols, v_rows
+                k_rows_of[b], v_rows_of[b] = k_rows, v_rows
             x_codes = quant.tile([P, PASSES, CHUNK], U32, align_bytes=64)
             x_scales = quant.tile([P, PASSES, CHUNK], U8, align_bytes=64)
             for g in range(PASSES):
                 nc.vector.quantize_mx(
                     out=x_codes[:, g, :].bitcast(FP8X4), scales=x_scales[:, g, :], in_=grouped_of[t][:, g, :]
                 )
-
-            def multiply(part, qkv_ps):
+            q_cols = cols.tile([P, CHUNK], F32)
+            k_cols = cols.tile([P, HALO + CHUNK], F32)
+            v_cols = cols.tile([P, HALO + CHUNK], F32)
+            for here, before in ((k_cols, k_cols_of), (v_cols, v_cols_of)):
+                if n0 == 0:
+                    nc.gpsimd.memset(here[:, 0:HALO], 0.0)
+                else:
+                    nc.scalar.copy(out=here[:, 0:HALO], in_=before[t - 1][:, CHUNK : HALO + CHUNK])
+            for part, destination in enumerate((q_cols[:], k_cols[:, HALO:], v_cols[:, HALO:])):
+                qkv_ps = psum_mx.tile([P, CHUNK], F32)
                 for g in range(PASSES):
                     nc.tensor.matmul_mx(
                         out=qkv_ps[:],
@@ -199,70 +223,55 @@ def tile_dwarfattention_pa_t_kernel(
                         start=(g == 0),
                         stop=(g == PASSES - 1),
                     )
-
-            for part, cols in ((1, k_cols_of[b]), (2, v_cols_of[b])):
-                kv_ps = psum_kv.tile([P, CHUNK], F32)
-                multiply(part, kv_ps)
                 nc.scalar.activation(
-                    out=cols[:, PAD + n0 : PAD + n0 + CHUNK],
-                    in_=kv_ps[:],
-                    func=ACT.Identity,
-                    bias=bias_col[:, part : part + 1],
+                    out=destination, in_=qkv_ps[:], func=ACT.Identity, bias=bias_col[:, part : part + 1]
                 )
-            q_ps = psum_q.tile([P, CHUNK], F32)
-            multiply(0, q_ps)
-            q_cols = small.tile([P, CHUNK], F32)
-            nc.scalar.activation(out=q_cols[:], in_=q_ps[:], func=ACT.Identity, bias=bias_col[:, 0:1])
-            q_ps_of[t], q_cols_of[t] = q_ps, q_cols
-
-            v_ps = psum_v.tile([P, BLOCKS, P], F32)
-            for c in range(BLOCKS):
-                nc.tensor.transpose(
-                    v_ps[:, c, :], v_cols_of[b][:, PAD + n0 + c * P : PAD + n0 + (c + 1) * P], ident_f32[:]
-                )
-            nc.scalar.copy(out=v_rows_of[b][:, c0 : c0 + BLOCKS, :], in_=v_ps[:])
+            q_rows = cols.tile([P, BLOCKS, P], F32)
+            to_rows(q_cols[:], q_rows[:])
+            to_rows(k_cols[:, HALO:], k_rows_of[b][:, c0 : c0 + BLOCKS, :])
+            to_rows(v_cols[:, HALO:], v_rows_of[b][:, c0 : c0 + BLOCKS, :])
+            q_cols_of[t], k_cols_of[t], v_cols_of[t], q_rows_of[t] = q_cols, k_cols, v_cols, q_rows
             dots = small.tile([P, len(OFFSETS), ROWS], F32)
             nc.gpsimd.memset(dots[:], 0.0)
             dots_of[t] = dots
 
         def on_vector(col):
-            return col % 3 == 0
+            return col % 4 == 0
 
         def product(t, col):
             b, n0, c0 = place(t)
             o = OFFSETS[col]
-            first = first_block(o, c0)
+            first = first_block(col, c0)
             if first == BLOCKS:
                 return
-            keys = k_cols_of[b][:, PAD + n0 + first * P - o : PAD + n0 + CHUNK - o]
-            if on_vector(col):
-                prod = prods.tile([P, CHUNK], F32, tag="prod_vector")
-                nc.vector.scalar_tensor_tensor(
-                    out=prod[:, first * P :],
-                    in0=q_ps_of[t][:, first * P :],
-                    scalar=bias_col[:, 0:1],
-                    in1=keys,
-                    op0=ALU.add,
-                    op1=ALU.mult,
+            engine = nc.vector if on_vector(col) else nc.gpsimd
+            if col in FAR_COLS:
+                prod = prods.tile([P, BLOCKS, P], F32, tag="prod_far")
+                engine.tensor_tensor(
+                    out=prod[:, first:, :],
+                    in0=q_rows_of[t][:, first:, :],
+                    in1=k_rows_of[b][:, c0 + first - o // P : c0 + BLOCKS - o // P, :],
+                    op=ALU.mult,
                 )
+                prod_rows_of[t, col] = prod
             else:
-                prod = prods.tile([P, CHUNK], F32, tag="prod_gpsimd")
-                nc.gpsimd.tensor_tensor(out=prod[:, first * P :], in0=q_cols_of[t][:, first * P :], in1=keys, op=ALU.mult)
-            prod_of[t, col] = prod
+                prod = prods.tile([P, CHUNK], F32, tag="prod_near")
+                engine.tensor_tensor(
+                    out=prod[:], in0=q_cols_of[t][:], in1=k_cols_of[t][:, HALO - o : HALO - o + CHUNK], op=ALU.mult
+                )
+                prod_of[t, col] = prod
 
         def transpose_product(t, col):
-            b, n0, c0 = place(t)
-            first = first_block(OFFSETS[col], c0)
-            if first == BLOCKS:
+            if col in FAR_COLS:
                 return
             prod_rows = psum_p.tile([P, BLOCKS, P], F32)
-            for c in range(first, BLOCKS):
+            for c in range(BLOCKS):
                 nc.tensor.transpose(prod_rows[:, c, :], prod_of[t, col][:, c * P : (c + 1) * P], ident_f32[:])
             prod_rows_of[t, col] = prod_rows
 
         def sum_heads(t, col):
             b, n0, c0 = place(t)
-            first = first_block(OFFSETS[col], c0)
+            first = first_block(col, c0)
             if first == BLOCKS:
                 return
             by_head = prod_rows_of[t, col][:].rearrange("p c (h d) -> p (c h) d", h=H)
@@ -280,7 +289,7 @@ def tile_dwarfattention_pa_t_kernel(
                         out=unused[:, r, :], in_=by_head[:, r, :], func=ACT.Copy, accum_out=dots_of[t][:, col, r : r + 1]
                     )
 
-        def weights(t, step=0):
+        def weights(t, col=0):
             dots = dots_of[t]
             u1 = small.tile([P, SLOTS, ROWS], F32)
             for group in range(len(TAUS)):
@@ -330,29 +339,28 @@ def tile_dwarfattention_pa_t_kernel(
             nc.vector.reciprocal(out=one_over_z[:], in_=z[:])
             weight_of[t], one_over_z_of[t] = weight, one_over_z
 
-        def shifted_v(t, step):
-            b, n0, c0 = place(t)
-            col = MIX_ORDER[step]
-            o = OFFSETS[col]
-            first = first_block(o, c0)
-            if o % P == 0 or first == BLOCKS:
+        def shifted_v(t, col):
+            if col in FAR_COLS:
                 return
-            v_ps = psum_v.tile([P, BLOCKS, P], F32)
-            for c in range(first, BLOCKS):
-                start_col = PAD + n0 + c * P - o
-                nc.tensor.transpose(v_ps[:, c, :], v_cols_of[b][:, start_col : start_col + P], ident_f32[:])
+            start_col = HALO - OFFSETS[col]
+            v_ps = psum_v.tile([P, BLOCKS, P], F32, tag="rows_ps")
+            for c in range(BLOCKS):
+                nc.tensor.transpose(
+                    v_ps[:, c, :], v_cols_of[t][:, start_col + c * P : start_col + (c + 1) * P], ident_f32[:]
+                )
             shifted_of[t, col] = v_ps
 
-        def mix(t, step):
+        def mix(t, col):
             b, n0, c0 = place(t)
-            col = MIX_ORDER[step]
-            o = OFFSETS[col]
             if col == ZERO_COL:
                 acc = small.tile([P, ROWS, HD], F32)
                 acc_of[t] = acc
             acc = acc_of[t]
-            for c in range(first_block(o, c0), BLOCKS):
-                v_block = v_rows_of[b][:, c0 + c - o // P, :] if o % P == 0 else shifted_of[t, col][:, c, :]
+            for c in range(first_block(col, c0), BLOCKS):
+                if col in FAR_COLS:
+                    v_block = v_rows_of[b][:, c0 + c - OFFSETS[col] // P, :]
+                else:
+                    v_block = shifted_of[t, col][:, c, :]
                 for h in range(H):
                     r = c * H + h
                     if col == ZERO_COL:
@@ -371,7 +379,7 @@ def tile_dwarfattention_pa_t_kernel(
                             op1=ALU.add,
                         )
 
-        def finish(t, step=0):
+        def finish(t, col=0):
             b, n0, c0 = place(t)
             result = small.tile([P, ROWS, HD], F32)
             for r in range(ROWS):
@@ -384,8 +392,8 @@ def tile_dwarfattention_pa_t_kernel(
             )
 
         def when(stage, t, step=0):
-            if 0 <= t < CHUNKS and 0 <= step < len(OFFSETS):
-                stage(t, step)
+            if 0 <= t < CHUNKS and 0 <= step < len(ORDER):
+                stage(t, ORDER[step])
 
         with tc.manual_schedule():
             load_x(0)
@@ -396,7 +404,7 @@ def tile_dwarfattention_pa_t_kernel(
             for t in range(-1, CHUNKS):
                 when(transpose_x, t + 2)
                 when(load_x, t + 4)
-                for step in range(len(OFFSETS) + 2):
+                for step in range(len(ORDER) + 2):
                     when(product, t + 1, step)
                     when(transpose_product, t + 1, step - 1)
                     when(shifted_v, t, step + 1)

@@ -149,23 +149,23 @@ def tile_dwarfattention_pa_t_kernel(
             in_=local_gain[:].unsqueeze(1).unsqueeze(1).to_broadcast([P, CHUNKS, BLOCKS, H]),
         )
 
-        k_rows_of, v_rows_of = {}, {}
+        k_rows_of, v_cols_of = {}, {}
         x_rows_of, grouped_of = {}, {}
-        q_cols_of, k_cols_of, v_cols_of, q_rows_of = {}, {}, {}, {}
-        dots_of, weight_of, one_over_z_of, acc_of = {}, {}, {}, {}
+        q_cols_of, k_cols_of, q_rows_of = {}, {}, {}
+        dots_of, u1_of, exp_u_of, weight_of, one_over_z_of, acc_of = {}, {}, {}, {}, {}, {}
         prod_of, prod_rows_of, shifted_of = {}, {}, {}
 
         def place(t):
             b, chunk = divmod(t, N // CHUNK)
             return b, chunk * CHUNK, chunk * BLOCKS
 
-        def load_x(t, col=0):
+        def load_x(t):
             b, n0, c0 = place(t)
             x_rows = xin.tile([P, BLOCKS, D], BF16)
             nc.sync.dma_start(out=x_rows[:], in_=x[b, n0 : n0 + CHUNK, :].rearrange("(c p) d -> p c d", p=P))
             x_rows_of[t] = x_rows
 
-        def transpose_x(t, col=0):
+        def transpose_x(t):
             grouped = quant.tile([P, PASSES, CHUNK * PACK], BF16, align_bytes=64)
             for g in range(PASSES):
                 grouped_words = grouped[:, g, :].bitcast(F32).rearrange("p (n u) -> p n u", u=2)
@@ -186,17 +186,18 @@ def tile_dwarfattention_pa_t_kernel(
             grouped_of[t] = grouped
 
         def to_rows(columns, rows):
-            rows_ps = psum_v.tile([P, BLOCKS, P], F32)
+            rows_ps = psum_x.tile([P, BLOCKS, P], F32, tag="xt")
             for c in range(BLOCKS):
                 nc.tensor.transpose(rows_ps[:, c, :], columns[:, c * P : (c + 1) * P], ident_f32[:])
             nc.scalar.copy(out=rows, in_=rows_ps[:])
 
-        def project(t, col=0):
+        def project(t):
             b, n0, c0 = place(t)
             if n0 == 0:
                 k_rows = batch.tile([P, N // P, P], F32)
-                v_rows = batch.tile([P, N // P, P], F32)
-                k_rows_of[b], v_rows_of[b] = k_rows, v_rows
+                v_cols = batch.tile([P, HALO + N], F32)
+                nc.gpsimd.memset(v_cols[:, 0:HALO], 0.0)
+                k_rows_of[b], v_cols_of[b] = k_rows, v_cols
             x_codes = quant.tile([P, PASSES, CHUNK], U32, align_bytes=64)
             x_scales = quant.tile([P, PASSES, CHUNK], U8, align_bytes=64)
             for g in range(PASSES):
@@ -205,13 +206,12 @@ def tile_dwarfattention_pa_t_kernel(
                 )
             q_cols = cols.tile([P, CHUNK], F32)
             k_cols = cols.tile([P, HALO + CHUNK], F32)
-            v_cols = cols.tile([P, HALO + CHUNK], F32)
-            for here, before in ((k_cols, k_cols_of), (v_cols, v_cols_of)):
-                if n0 == 0:
-                    nc.gpsimd.memset(here[:, 0:HALO], 0.0)
-                else:
-                    nc.scalar.copy(out=here[:, 0:HALO], in_=before[t - 1][:, CHUNK : HALO + CHUNK])
-            for part, destination in enumerate((q_cols[:], k_cols[:, HALO:], v_cols[:, HALO:])):
+            if n0 == 0:
+                nc.gpsimd.memset(k_cols[:, 0:HALO], 0.0)
+            else:
+                nc.scalar.copy(out=k_cols[:, 0:HALO], in_=k_cols_of[t - 1][:, CHUNK : HALO + CHUNK])
+            v_here = v_cols_of[b][:, HALO + n0 : HALO + n0 + CHUNK]
+            for part, destination in enumerate((q_cols[:], k_cols[:, HALO:], v_here)):
                 qkv_ps = psum_mx.tile([P, CHUNK], F32)
                 for g in range(PASSES):
                     nc.tensor.matmul_mx(
@@ -229,14 +229,13 @@ def tile_dwarfattention_pa_t_kernel(
             q_rows = cols.tile([P, BLOCKS, P], F32)
             to_rows(q_cols[:], q_rows[:])
             to_rows(k_cols[:, HALO:], k_rows_of[b][:, c0 : c0 + BLOCKS, :])
-            to_rows(v_cols[:, HALO:], v_rows_of[b][:, c0 : c0 + BLOCKS, :])
-            q_cols_of[t], k_cols_of[t], v_cols_of[t], q_rows_of[t] = q_cols, k_cols, v_cols, q_rows
-            dots = small.tile([P, len(OFFSETS), ROWS], F32)
+            q_cols_of[t], k_cols_of[t], q_rows_of[t] = q_cols, k_cols, q_rows
+            dots = cols.tile([P, len(OFFSETS), ROWS], F32)
             nc.gpsimd.memset(dots[:], 0.0)
             dots_of[t] = dots
 
-        def on_vector(col):
-            return col % 4 == 0
+        def summed_by_vector(col):
+            return col % 6 == 0
 
         def product(t, col):
             b, n0, c0 = place(t)
@@ -244,10 +243,9 @@ def tile_dwarfattention_pa_t_kernel(
             first = first_block(col, c0)
             if first == BLOCKS:
                 return
-            engine = nc.vector if on_vector(col) else nc.gpsimd
             if col in FAR_COLS:
                 prod = prods.tile([P, BLOCKS, P], F32, tag="prod_far")
-                engine.tensor_tensor(
+                nc.gpsimd.tensor_tensor(
                     out=prod[:, first:, :],
                     in0=q_rows_of[t][:, first:, :],
                     in1=k_rows_of[b][:, c0 + first - o // P : c0 + BLOCKS - o // P, :],
@@ -256,7 +254,7 @@ def tile_dwarfattention_pa_t_kernel(
                 prod_rows_of[t, col] = prod
             else:
                 prod = prods.tile([P, CHUNK], F32, tag="prod_near")
-                engine.tensor_tensor(
+                nc.gpsimd.tensor_tensor(
                     out=prod[:], in0=q_cols_of[t][:], in1=k_cols_of[t][:, HALO - o : HALO - o + CHUNK], op=ALU.mult
                 )
                 prod_of[t, col] = prod
@@ -275,7 +273,7 @@ def tile_dwarfattention_pa_t_kernel(
             if first == BLOCKS:
                 return
             by_head = prod_rows_of[t, col][:].rearrange("p c (h d) -> p (c h) d", h=H)
-            if on_vector(col):
+            if summed_by_vector(col):
                 nc.vector.tensor_reduce(
                     out=dots_of[t][:, col, first * H :],
                     in_=by_head[:, first * H :, :],
@@ -289,7 +287,7 @@ def tile_dwarfattention_pa_t_kernel(
                         out=unused[:, r, :], in_=by_head[:, r, :], func=ACT.Copy, accum_out=dots_of[t][:, col, r : r + 1]
                     )
 
-        def weights(t, col=0):
+        def scores(t):
             dots = dots_of[t]
             u1 = small.tile([P, SLOTS, ROWS], F32)
             for group in range(len(TAUS)):
@@ -306,6 +304,10 @@ def tile_dwarfattention_pa_t_kernel(
                 )
             exp_u = small.tile([P, SLOTS, ROWS], F32)
             nc.scalar.activation(out=exp_u[:], in_=u1[:], func=ACT.Exp, bias=minus_one_col[:, 0:1])
+            u1_of[t], exp_u_of[t] = u1, exp_u
+
+        def weights(t):
+            u1, exp_u = u1_of[t], exp_u_of[t]
             feat = small.tile([P, SLOTS, ROWS], F32)
             nc.vector.scalar_tensor_tensor(
                 out=feat[:].rearrange("p s r -> p (s r)"),
@@ -340,14 +342,14 @@ def tile_dwarfattention_pa_t_kernel(
             weight_of[t], one_over_z_of[t] = weight, one_over_z
 
         def shifted_v(t, col):
-            if col in FAR_COLS:
+            b, n0, c0 = place(t)
+            first = first_block(col, c0)
+            if first == BLOCKS:
                 return
-            start_col = HALO - OFFSETS[col]
-            v_ps = psum_v.tile([P, BLOCKS, P], F32, tag="rows_ps")
-            for c in range(BLOCKS):
-                nc.tensor.transpose(
-                    v_ps[:, c, :], v_cols_of[t][:, start_col + c * P : start_col + (c + 1) * P], ident_f32[:]
-                )
+            v_ps = psum_v.tile([P, BLOCKS, P], F32)
+            for c in range(first, BLOCKS):
+                start_col = HALO + n0 + c * P - OFFSETS[col]
+                nc.tensor.transpose(v_ps[:, c, :], v_cols_of[b][:, start_col : start_col + P], ident_f32[:])
             shifted_of[t, col] = v_ps
 
         def mix(t, col):
@@ -356,30 +358,21 @@ def tile_dwarfattention_pa_t_kernel(
                 acc = small.tile([P, ROWS, HD], F32)
                 acc_of[t] = acc
             acc = acc_of[t]
-            for c in range(first_block(col, c0), BLOCKS):
-                if col in FAR_COLS:
-                    v_block = v_rows_of[b][:, c0 + c - OFFSETS[col] // P, :]
+            for r in range(first_block(col, c0) * H, ROWS):
+                v_head = shifted_of[t, col][:].rearrange("p c (h d) -> p (c h) d", h=H)[:, r, :]
+                if col == ZERO_COL:
+                    nc.vector.tensor_scalar_mul(out=acc[:, r, :], in0=v_head, scalar1=weight_of[t][:, col, r : r + 1])
                 else:
-                    v_block = shifted_of[t, col][:, c, :]
-                for h in range(H):
-                    r = c * H + h
-                    if col == ZERO_COL:
-                        nc.vector.tensor_scalar_mul(
-                            out=acc[:, r, :],
-                            in0=v_block[:, h * HD : (h + 1) * HD],
-                            scalar1=weight_of[t][:, col, r : r + 1],
-                        )
-                    else:
-                        nc.vector.scalar_tensor_tensor(
-                            out=acc[:, r, :],
-                            in0=v_block[:, h * HD : (h + 1) * HD],
-                            scalar=weight_of[t][:, col, r : r + 1],
-                            in1=acc[:, r, :],
-                            op0=ALU.mult,
-                            op1=ALU.add,
-                        )
+                    nc.vector.scalar_tensor_tensor(
+                        out=acc[:, r, :],
+                        in0=v_head,
+                        scalar=weight_of[t][:, col, r : r + 1],
+                        in1=acc[:, r, :],
+                        op0=ALU.mult,
+                        op1=ALU.add,
+                    )
 
-        def finish(t, col=0):
+        def finish(t):
             b, n0, c0 = place(t)
             result = small.tile([P, ROWS, HD], F32)
             for r in range(ROWS):
@@ -391,7 +384,11 @@ def tile_dwarfattention_pa_t_kernel(
                 in_=result[:].rearrange("p (c h) d -> p c (h d)", h=H),
             )
 
-        def when(stage, t, step=0):
+        def for_chunk(stage, t):
+            if 0 <= t < CHUNKS:
+                stage(t)
+
+        def for_column(stage, t, step):
             if 0 <= t < CHUNKS and 0 <= step < len(ORDER):
                 stage(t, ORDER[step])
 
@@ -401,15 +398,18 @@ def tile_dwarfattention_pa_t_kernel(
             transpose_x(0)
             load_x(2)
             project(0)
-            for t in range(-1, CHUNKS):
-                when(transpose_x, t + 2)
-                when(load_x, t + 4)
+            for t in range(-2, CHUNKS):
+                for_chunk(transpose_x, t + 3)
+                for_chunk(load_x, t + 5)
+                for_chunk(scores, t + 1)
+                for_column(shifted_v, t, 0)
                 for step in range(len(ORDER) + 2):
-                    when(product, t + 1, step)
-                    when(transpose_product, t + 1, step - 1)
-                    when(shifted_v, t, step + 1)
-                    when(sum_heads, t + 1, step - 2)
-                    when(mix, t, step)
-                when(finish, t)
-                when(project, t + 2)
-                when(weights, t + 1)
+                    for_column(product, t + 2, step)
+                    for_column(shifted_v, t, step + 1)
+                    for_column(transpose_product, t + 2, step - 1)
+                    for_column(sum_heads, t + 2, step - 2)
+                    for_column(mix, t, step)
+                    if step == len(ORDER) // 2:
+                        for_chunk(project, t + 3)
+                for_chunk(finish, t)
+                for_chunk(weights, t + 1)

@@ -12,6 +12,7 @@ FP8X4 = mybir.dt.float8_e4m3fn_x4
 FP4X4 = mybir.dt.float4_e2m1fn_x4
 ALU = mybir.AluOpType
 ACT = mybir.ActivationFunctionType
+AXIS = mybir.AxisListType
 
 B, N, D, H, HD, S = 2, 4096, 1024, 2, 64, 11
 D4 = (0.4829629131445341, 0.8365163037378079, 0.2241438680420134, -0.1294095225512604)
@@ -20,38 +21,64 @@ P = 128
 PACK = 4
 K_PASS = P * PACK
 PASSES = D // K_PASS
-CHUNK = 512
-BLOCKS = CHUNK // P
-CHUNKS = B * N // CHUNK
-ROWS = BLOCKS * H
+PLACES = N // P
+CHUNK = 4
+CHUNKS = PLACES // CHUNK
 
 OFFSETS = tuple(1 << i for i in range(S + 1)) + tuple(3 << j for j in range(S)) + (0,)
-ZERO_COL = len(OFFSETS) - 1
-NEAR_COLS = tuple(col for col, o in enumerate(OFFSETS) if o % P != 0)
-FAR_COLS = tuple(col for col, o in enumerate(OFFSETS) if o % P == 0)
-HALO = max(OFFSETS[col] for col in NEAR_COLS)
+COLS = len(OFFSETS)
+ZERO_COL = COLS - 1
 GROUP = S + 1
 TAUS = (1, 2, 3, 0)
 GROUP_COL = (0, 1, GROUP)
 SLOTS = GROUP * len(TAUS)
 LOCAL_SLOT = SLOTS - 1
 
+QUAD = P // PLACES
+QUADS = COLS // QUAD
+BANK_QUADS = 4
+STEP_D = 16
+HALF_D = HD // 2
+PIECES = HALF_D // STEP_D
+QUAD_ORDER = (0, 5, 1, 4, 3, 2)
+STEPS = 2 * QUADS * PIECES
+MIX_PLACES = PLACES // 2
+MIX_CELLS = MIX_PLACES // 2
+NEAR_MOVES = 2
+LAG = 7
+STAGES = tuple((b, h) for b in range(B) for h in range(H))
+
 FLOPS = 2 * B * N * D * 3 * H * HD + B * H * N * (4 * S + 1) * 4 * HD
 
 
-def alternate(first, second):
-    mixed = []
-    for i in range(max(len(first), len(second))):
-        mixed.extend(first[i : i + 1])
-        mixed.extend(second[i : i + 1])
-    return tuple(mixed)
+def parts(o):
+    move, rest = divmod(o, PLACES)
+    if rest == 0:
+        return ((0, PLACES, move, 0),)
+    return ((rest, PLACES, move, 0), (0, rest, move + 1, PLACES - rest))
 
 
-ORDER = (ZERO_COL,) + alternate(NEAR_COLS, FAR_COLS[:-1])
+def moves_of(col):
+    return tuple(part[2] for part in parts(OFFSETS[col]) if part[2] > 0)
 
 
-def first_block(col, c0):
-    return min(BLOCKS, max(0, OFFSETS[col] // P - c0)) if col in FAR_COLS else 0
+def is_far(col):
+    return OFFSETS[col] > NEAR_MOVES * PLACES and OFFSETS[col] % PLACES == 0
+
+
+FAR_COLS = tuple(col for col in range(COLS) if is_far(col))
+NEAR_COLS = tuple(col for col in range(COLS) if not is_far(col) and col != ZERO_COL)
+
+
+def mix_order(half):
+    order = [FAR_COLS[0], ZERO_COL, FAR_COLS[1], FAR_COLS[2]]
+    far, near = list(FAR_COLS[3:]), list(NEAR_COLS)
+    while near:
+        order.append(near[0])
+        near = near[1:]
+        order.extend(far[:1])
+        far = far[1:]
+    return order if half == 0 else list(reversed(order))
 
 
 def tile_dwarfattention_pa_t_kernel(
@@ -60,21 +87,28 @@ def tile_dwarfattention_pa_t_kernel(
     nc = tc.nc
     with ExitStack() as ctx:
         const = ctx.enter_context(tc.tile_pool(name="const", bufs=1))
-        batch = ctx.enter_context(tc.tile_pool(name="batch", bufs=2))
-        xin = ctx.enter_context(tc.tile_pool(name="xin", bufs=2))
-        quant = ctx.enter_context(tc.tile_pool(name="quant", bufs=2))
-        cols = ctx.enter_context(tc.tile_pool(name="cols", bufs=3))
-        prods = ctx.enter_context(tc.tile_pool(name="prods", bufs=3))
-        small = ctx.enter_context(tc.tile_pool(name="small", bufs=2))
+        qkv = ctx.enter_context(tc.tile_pool(name="qkv", bufs=4))
+        prods = ctx.enter_context(tc.tile_pool(name="prods", bufs=2))
+        table = ctx.enter_context(tc.tile_pool(name="table", bufs=1))
+        phase = ctx.enter_context(tc.tile_pool(name="phase", bufs=1))
         psum_x = ctx.enter_context(tc.psum_pool(name="psum_x", bufs=2))
-        psum_mx = ctx.enter_context(tc.psum_pool(name="psum_mx", bufs=2))
-        psum_p = ctx.enter_context(tc.psum_pool(name="psum_p", bufs=2))
-        psum_v = ctx.enter_context(tc.psum_pool(name="psum_v", bufs=2))
+        psum_dots = ctx.enter_context(tc.psum_pool(name="psum_dots", bufs=1))
+        psum_acc = ctx.enter_context(tc.psum_pool(name="psum_acc", bufs=4))
 
-        ident_f32 = const.tile([P, P], F32)
-        make_identity(nc, ident_f32[:])
-        ident_bf16 = const.tile([P, P], BF16)
-        make_identity(nc, ident_bf16[:])
+        x_rows_of, grouped_of, codes_of, qkv_ps_of = {}, {}, {}, {}
+
+        def load_x(b, j):
+            x_rows = phase.tile([P, CHUNK, D], BF16, bufs=2, offset=0, align_bytes=64)
+            nc.sync.dma_start(
+                out=x_rows[:], in_=x[b].rearrange("(p c) d -> p c d", c=PLACES)[:, j * CHUNK : (j + 1) * CHUNK, :]
+            )
+            x_rows_of[b, j] = x_rows
+
+        load_x(0, 0)
+        load_x(0, 1)
+
+        ident = const.tile([P, P], F32)
+        make_identity(nc, ident[:])
         one_col = const.tile([P, 1], F32)
         nc.vector.memset(one_col[:], 1.0)
         minus_one_col = const.tile([P, 1], F32)
@@ -89,14 +123,10 @@ def tile_dwarfattention_pa_t_kernel(
                 out=w_scales[32 * quadrant : 32 * quadrant + 4, :, :].bitcast(I32),
                 in_=W_qkv_scales[:, 4 * quadrant : 4 * quadrant + 4, :].rearrange("g r n -> r g n").bitcast(I32),
             )
-
-        bias_rows = const.tile([P, P], BF16)
-        nc.vector.memset(bias_rows[:], 0.0)
-        nc.sync.dma_start(out=bias_rows[0:3, :], in_=b_qkv.rearrange("(r f) -> r f", f=P))
-        bias_ps = psum_x.tile([P, P], BF16, tag="xt")
-        nc.tensor.transpose(bias_ps[:], bias_rows[:], ident_bf16[:])
-        bias_col = const.tile([P, 3], F32)
-        nc.vector.tensor_copy(out=bias_col[:], in_=bias_ps[:, 0:3])
+        bias_bf16 = const.tile([P, 3 * P], BF16)
+        nc.sync.dma_start(out=bias_bf16[:], in_=b_qkv.partition_broadcast(P))
+        bias = const.tile([P, 3, H, HD], F32)
+        nc.vector.tensor_copy(out=bias[:].rearrange("p r h d -> p (r h d)"), in_=bias_bf16[:])
 
         pos_bias_all = const.tile([P, 4 * S * H], BF16)
         nc.sync.dma_start(out=pos_bias_all[:], in_=pos_bias.rearrange("r h -> (r h)").partition_broadcast(P))
@@ -122,294 +152,484 @@ def tile_dwarfattention_pa_t_kernel(
             out=local_gain[:], in0=bypass[:], scalar=0.0, in1=bypass_tail[:], op0=ALU.max, op1=ALU.add
         )
 
-        gains_rows = const.tile([P, P * S], BF16)
-        for b in range(B):
-            nc.sync.dma_start(
-                out=gains_rows[b * 64 : (b + 1) * 64, :],
-                in_=gains[b].rearrange("h (c p) j -> c h (p j)", p=P),
-            )
-        gains_by_scale = const.tile([P, S, P], BF16)
-        nc.vector.tensor_copy(out=gains_by_scale[:], in_=gains_rows[:].rearrange("r (p j) -> r j p", j=S))
-        slot_gain = const.tile([P, CHUNKS, SLOTS, ROWS], F32)
+        gains_in = const.tile([P, B, H, PLACES, S], BF16)
+        for b, h in STAGES:
+            nc.sync.dma_start(out=gains_in[:, b, h, :, :], in_=gains[b, h].rearrange("(p c) j -> p c j", c=PLACES))
+        slot_gain = const.tile([P, SLOTS, PLACES], F32)
         nc.gpsimd.memset(slot_gain[:], 0.0)
-        SCALES_PER_BANK = 8
-        for j0 in range(0, S, SCALES_PER_BANK):
-            scales_here = min(SCALES_PER_BANK, S - j0)
-            gains_ps = psum_x.tile([P, SCALES_PER_BANK, P], BF16, tag="xt")
-            for j in range(scales_here):
-                nc.tensor.transpose(gains_ps[:, j, :], gains_by_scale[:, j0 + j, :], ident_bf16[:])
-            for group, tau in enumerate(TAUS):
-                nc.vector.tensor_scalar_mul(
-                    out=slot_gain[:, :, group * GROUP + j0 : group * GROUP + j0 + scales_here, :],
-                    in0=gains_ps[:, 0:scales_here, :].rearrange("p j (t r) -> p t j r", r=ROWS),
-                    scalar1=abs(D4[tau]),
-                )
-        nc.vector.tensor_copy(
-            out=slot_gain[:, :, LOCAL_SLOT, :].rearrange("p t (c h) -> p t c h", h=H),
-            in_=local_gain[:].unsqueeze(1).unsqueeze(1).to_broadcast([P, CHUNKS, BLOCKS, H]),
+
+        token = const.tile([P, PLACES], F32)
+        nc.gpsimd.iota(
+            token[:], pattern=[[1, PLACES]], base=0, channel_multiplier=PLACES, allow_small_or_imprecise_dtypes=True
         )
+        reached = const.tile([P, COLS, PLACES], F32)
+        for col, o in enumerate(OFFSETS):
+            nc.vector.tensor_single_scalar(out=reached[:, col, :], in_=token[:], scalar=float(o), op=ALU.is_ge)
 
-        k_rows_of, v_cols_of = {}, {}
-        x_rows_of, grouped_of = {}, {}
-        q_cols_of, k_cols_of, q_rows_of = {}, {}, {}
-        dots_of, u1_of, exp_u_of, weight_of, one_over_z_of, acc_of = {}, {}, {}, {}, {}, {}
-        prod_of, prod_rows_of, shifted_of = {}, {}, {}
+        k_moved = []
+        for i in range(6):
+            moved = const.tile([P, HALF_D, PLACES], F32, name="k_moved_%d" % i)
+            nc.gpsimd.memset(moved[:], 0.0)
+            k_moved.append(moved)
 
-        def place(t):
-            b, chunk = divmod(t, N // CHUNK)
-            return b, chunk * CHUNK, chunk * BLOCKS
+        def move_down(dst, src, move):
+            rows = P - move
+            first = rows // 16 * 16 if move < 16 else rows
+            nc.sync.dma_start(out=dst[move : move + first], in_=src[0:first])
+            if first < rows:
+                nc.sync.dma_start(out=dst[move + first : P], in_=src[first:rows])
 
-        def load_x(t):
-            b, n0, c0 = place(t)
-            x_rows = xin.tile([P, BLOCKS, D], BF16)
-            nc.sync.dma_start(out=x_rows[:], in_=x[b, n0 : n0 + CHUNK, :].rearrange("(c p) d -> p c d", p=P))
-            x_rows_of[t] = x_rows
+        q_of, k_of, v_of = {}, {}, {}
 
-        def transpose_x(t):
-            grouped = quant.tile([P, PASSES, CHUNK * PACK], BF16, align_bytes=64)
+        def transpose_x(b, j):
+            grouped = phase.tile([P, PASSES, CHUNK * P * PACK], BF16, bufs=2, offset=16384, align_bytes=64)
             for g in range(PASSES):
                 grouped_words = grouped[:, g, :].bitcast(F32).rearrange("p (n u) -> p n u", u=2)
                 for half in range(2):
-                    xt = psum_x.tile([P, 2, 2 * P], F32)
+                    xt = psum_x.tile([P, 2, 2 * P], F32, tag="xt")
                     for c in range(2):
-                        words = x_rows_of[t][:, 2 * half + c, :].bitcast(F32)
+                        words = x_rows_of[b, j][:, 2 * half + c, :].bitcast(F32)
                         for u in range(2):
                             nc.tensor.transpose(
                                 xt[:, u, c * P : (c + 1) * P],
                                 words[:, g * 2 * P + u : (g + 1) * 2 * P : 2],
-                                ident_f32[:],
+                                ident[:],
                             )
                     nc.scalar.copy(
                         out=grouped_words[:, half * 2 * P : (half + 1) * 2 * P, :],
                         in_=xt[:].rearrange("p u n -> p n u"),
                     )
-            grouped_of[t] = grouped
+            grouped_of[b, j] = grouped
 
-        def to_rows(columns, rows):
-            rows_ps = psum_x.tile([P, BLOCKS, P], F32, tag="xt")
-            for c in range(BLOCKS):
-                nc.tensor.transpose(rows_ps[:, c, :], columns[:, c * P : (c + 1) * P], ident_f32[:])
-            nc.scalar.copy(out=rows, in_=rows_ps[:])
-
-        def project(t):
-            b, n0, c0 = place(t)
-            if n0 == 0:
-                k_rows = batch.tile([P, N // P, P], F32)
-                v_cols = batch.tile([P, HALO + N], F32)
-                nc.gpsimd.memset(v_cols[:, 0:HALO], 0.0)
-                k_rows_of[b], v_cols_of[b] = k_rows, v_cols
-            x_codes = quant.tile([P, PASSES, CHUNK], U32, align_bytes=64)
-            x_scales = quant.tile([P, PASSES, CHUNK], U8, align_bytes=64)
+        def quantise_x(b, j):
+            x_codes = phase.tile([P, PASSES, CHUNK * P], U32, bufs=2, offset=32768, align_bytes=64)
+            x_scales = phase.tile([P, PASSES, CHUNK * P], U8, bufs=2, offset=40960, align_bytes=64)
             for g in range(PASSES):
                 nc.vector.quantize_mx(
-                    out=x_codes[:, g, :].bitcast(FP8X4), scales=x_scales[:, g, :], in_=grouped_of[t][:, g, :]
+                    out=x_codes[:, g, :].bitcast(FP8X4), scales=x_scales[:, g, :], in_=grouped_of[b, j][:, g, :]
                 )
-            q_cols = cols.tile([P, CHUNK], F32)
-            k_cols = cols.tile([P, HALO + CHUNK], F32)
-            if n0 == 0:
-                nc.gpsimd.memset(k_cols[:, 0:HALO], 0.0)
-            else:
-                nc.scalar.copy(out=k_cols[:, 0:HALO], in_=k_cols_of[t - 1][:, CHUNK : HALO + CHUNK])
-            v_here = v_cols_of[b][:, HALO + n0 : HALO + n0 + CHUNK]
-            for part, destination in enumerate((q_cols[:], k_cols[:, HALO:], v_here)):
-                qkv_ps = psum_mx.tile([P, CHUNK], F32)
-                for g in range(PASSES):
-                    nc.tensor.matmul_mx(
-                        out=qkv_ps[:],
-                        lhsT=w_words[:, g, part * 2 * P : (part + 1) * 2 * P].bitcast(FP4X4),
-                        lhsT_scale=w_scales[:, g, part * P : (part + 1) * P],
-                        rhs=x_codes[:, g, :].bitcast(FP8X4),
-                        rhs_scale=x_scales[:, g, :],
-                        start=(g == 0),
-                        stop=(g == PASSES - 1),
+            codes_of[b, j] = x_codes, x_scales
+
+        def multiply(b, j):
+            x_codes, x_scales = codes_of[b, j]
+            for part in range(3):
+                qkv_ps = psum_acc.tile([P, CHUNK, P], F32, tag="acc")
+                for c in range(CHUNK):
+                    tokens = slice(c * P, (c + 1) * P)
+                    for g in range(PASSES):
+                        nc.tensor.matmul_mx(
+                            out=qkv_ps[:, c, :],
+                            lhsT=x_codes[:, g, tokens].bitcast(FP8X4),
+                            lhsT_scale=x_scales[:, g, tokens],
+                            rhs=w_words[:, g, part * 2 * P : (part + 1) * 2 * P].bitcast(FP4X4),
+                            rhs_scale=w_scales[:, g, part * P : (part + 1) * P],
+                            start=(g == 0),
+                            stop=(g == PASSES - 1),
+                        )
+                qkv_ps_of[b, j, part] = qkv_ps
+
+        def keep(b, j):
+            if j == 0:
+                for h in range(H):
+                    q = qkv.tile([P, HD, PLACES], F32)
+                    k = qkv.tile([P, HD, PLACES], F32)
+                    v = qkv.tile([P, PLACES, HD], F32)
+                    q_of[b, h], k_of[b, h], v_of[b, h] = q, k, v
+            places = slice(j * CHUNK, (j + 1) * CHUNK)
+            for part, kept in enumerate((q_of, k_of, v_of)):
+                for h in range(H):
+                    in_ps = qkv_ps_of[b, j, part][:, :, h * HD : (h + 1) * HD]
+                    if part < 2:
+                        nc.vector.tensor_tensor(
+                            out=kept[b, h][:, :, places],
+                            in0=in_ps.rearrange("p c d -> p d c"),
+                            in1=bias[:, part, h, :].unsqueeze(2).to_broadcast([P, HD, CHUNK]),
+                            op=ALU.add,
+                        )
+                    else:
+                        nc.vector.tensor_tensor(
+                            out=kept[b, h][:, places, :],
+                            in0=in_ps,
+                            in1=bias[:, part, h, :].unsqueeze(1).to_broadcast([P, CHUNK, HD]),
+                            op=ALU.add,
+                        )
+
+        prod_of, dots_ps_of, k_buf_of = {}, {}, {}
+
+        def step_place(step):
+            half, rest = divmod(step, QUADS * PIECES)
+            i, piece = divmod(rest, PIECES)
+            return half, QUAD_ORDER[i], piece
+
+        def k_item_steps():
+            items, last_use = [], {}
+            for s in range(len(STAGES)):
+                for step in range(STEPS):
+                    half, quad, piece = step_place(step)
+                    for col in range(quad * QUAD, (quad + 1) * QUAD):
+                        for move in moves_of(col):
+                            item = (s, half, move)
+                            if item not in last_use:
+                                items.append(item)
+                            last_use[item] = s * STEPS + step
+            return items, last_use
+
+        k_items, k_last_use = k_item_steps()
+        k_free, k_busy = list(k_moved), {}
+
+        def move_k(t):
+            for item in list(k_busy):
+                if k_last_use[item] < t:
+                    k_free.append(k_busy.pop(item))
+            while k_free and k_items:
+                item = k_items.pop(0)
+                if STAGES[item[0]] not in k_of:
+                    k_items.insert(0, item)
+                    return
+                moved = k_free.pop(0)
+                s, half, move = item
+                move_down(moved, k_of[STAGES[s]][:, half * HALF_D : (half + 1) * HALF_D, :], move)
+                k_busy[item] = moved
+                k_buf_of[item] = moved
+
+        def products(s, step):
+            half, quad, piece = step_place(step)
+            d0 = half * HALF_D + piece * STEP_D
+            prod = prods.tile([P, STEP_D, QUAD, PLACES], F32)
+            for i in range(QUAD):
+                for first, last, move, source in parts(OFFSETS[quad * QUAD + i]):
+                    if move == 0:
+                        k_read = k_of[STAGES[s]][:, d0 : d0 + STEP_D, :]
+                    else:
+                        k_read = k_buf_of[s, half, move][:, piece * STEP_D : (piece + 1) * STEP_D, :]
+                    nc.vector.tensor_tensor(
+                        out=prod[:, :, i, first:last],
+                        in0=q_of[STAGES[s]][:, d0 : d0 + STEP_D, first:last],
+                        in1=k_read[:, :, source : source + last - first],
+                        op=ALU.mult,
                     )
-                nc.scalar.activation(
-                    out=destination, in_=qkv_ps[:], func=ACT.Identity, bias=bias_col[:, part : part + 1]
+            prod_of[s, step] = prod
+
+        def bank_steps(bank):
+            return [step for step in range(STEPS) if step_place(step)[1] // BANK_QUADS == bank]
+
+        def sum_products(s, step):
+            half, quad, piece = step_place(step)
+            bank = quad // BANK_QUADS
+            steps = bank_steps(bank)
+            if step == steps[0]:
+                if bank == 0:
+                    dots_a = psum_dots.tile([P, BANK_QUADS, P], F32)
+                    dots_ps_of[s, bank] = dots_a
+                else:
+                    dots_b = psum_dots.tile([P, QUADS - BANK_QUADS, P], F32)
+                    dots_ps_of[s, bank] = dots_b
+            for d in range(STEP_D):
+                nc.tensor.matmul(
+                    dots_ps_of[s, bank][:, quad % BANK_QUADS, :],
+                    lhsT=prod_of[s, step][:, d, :, :].rearrange("p i c -> p (i c)"),
+                    rhs=ident[:],
+                    start=(step == steps[0] and d == 0),
+                    stop=(step == steps[-1] and d == STEP_D - 1),
+                    is_transpose=True,
                 )
-            q_rows = cols.tile([P, BLOCKS, P], F32)
-            to_rows(q_cols[:], q_rows[:])
-            to_rows(k_cols[:, HALO:], k_rows_of[b][:, c0 : c0 + BLOCKS, :])
-            q_cols_of[t], k_cols_of[t], q_rows_of[t] = q_cols, k_cols, q_rows
-            dots = cols.tile([P, len(OFFSETS), ROWS], F32)
-            nc.gpsimd.memset(dots[:], 0.0)
-            dots_of[t] = dots
 
-        def summed_by_vector(col):
-            return col % 6 == 0
+        turned_of, back_of, dots_of, u1_of, exp_u_of, positive_of = {}, {}, {}, {}, {}, {}
+        weight_of, one_over_z_of = {}, {}
 
-        def product(t, col):
-            b, n0, c0 = place(t)
-            o = OFFSETS[col]
-            first = first_block(col, c0)
-            if first == BLOCKS:
-                return
-            if col in FAR_COLS:
-                prod = prods.tile([P, BLOCKS, P], F32, tag="prod_far")
-                nc.gpsimd.tensor_tensor(
-                    out=prod[:, first:, :],
-                    in0=q_rows_of[t][:, first:, :],
-                    in1=k_rows_of[b][:, c0 + first - o // P : c0 + BLOCKS - o // P, :],
+        def dots_out(s):
+            turned = table.tile([P, QUADS, P], F32, offset=0)
+            nc.scalar.copy(out=turned[:, 0:BANK_QUADS, :], in_=dots_ps_of[s, 0][:])
+            nc.scalar.copy(out=turned[:, BANK_QUADS:QUADS, :], in_=dots_ps_of[s, 1][:])
+            turned_of[s] = turned
+
+        def dots_back(s):
+            for bank in range(2):
+                quads = range(QUADS)[bank * BANK_QUADS : (bank + 1) * BANK_QUADS]
+                back = psum_x.tile([P, BANK_QUADS, P], F32, tag="xt")
+                for quad in quads:
+                    nc.tensor.transpose(back[:, quad % BANK_QUADS, :], turned_of[s][:, quad, :], ident[:])
+                back_of[s, bank] = back
+
+        def dots_masked(s):
+            dots = table.tile([P, COLS, PLACES], F32, offset=12288)
+            for bank in range(2):
+                first = bank * BANK_QUADS * QUAD
+                last = min(COLS, first + BANK_QUADS * QUAD)
+                nc.vector.tensor_tensor(
+                    out=dots[:, first:last, :],
+                    in0=back_of[s, bank][:].rearrange("p q (i c) -> p (q i) c", i=QUAD)[:, 0 : last - first, :],
+                    in1=reached[:, first:last, :],
                     op=ALU.mult,
                 )
-                prod_rows_of[t, col] = prod
-            else:
-                prod = prods.tile([P, CHUNK], F32, tag="prod_near")
-                nc.gpsimd.tensor_tensor(
-                    out=prod[:], in0=q_cols_of[t][:], in1=k_cols_of[t][:, HALO - o : HALO - o + CHUNK], op=ALU.mult
-                )
-                prod_of[t, col] = prod
+            dots_of[s] = dots
 
-        def transpose_product(t, col):
-            if col in FAR_COLS:
-                return
-            prod_rows = psum_p.tile([P, BLOCKS, P], F32)
-            for c in range(BLOCKS):
-                nc.tensor.transpose(prod_rows[:, c, :], prod_of[t, col][:, c * P : (c + 1) * P], ident_f32[:])
-            prod_rows_of[t, col] = prod_rows
-
-        def sum_heads(t, col):
-            b, n0, c0 = place(t)
-            first = first_block(col, c0)
-            if first == BLOCKS:
-                return
-            by_head = prod_rows_of[t, col][:].rearrange("p c (h d) -> p (c h) d", h=H)
-            if summed_by_vector(col):
-                nc.vector.tensor_reduce(
-                    out=dots_of[t][:, col, first * H :],
-                    in_=by_head[:, first * H :, :],
-                    axis=mybir.AxisListType.X,
-                    op=ALU.add,
-                )
-            else:
-                unused = prods.tile([P, ROWS, HD], F32)
-                for r in range(first * H, ROWS):
-                    nc.scalar.activation(
-                        out=unused[:, r, :], in_=by_head[:, r, :], func=ACT.Copy, accum_out=dots_of[t][:, col, r : r + 1]
-                    )
-
-        def scores(t):
-            dots = dots_of[t]
-            u1 = small.tile([P, SLOTS, ROWS], F32)
+        def scores(s):
+            h = STAGES[s][1]
+            u1 = table.tile([P, SLOTS, PLACES], F32, offset=6144)
             for group in range(len(TAUS)):
                 slots = slice(group * GROUP, (group + 1) * GROUP)
                 if group < len(GROUP_COL):
-                    dots_read = dots[:, GROUP_COL[group] : GROUP_COL[group] + GROUP, :]
+                    dots_read = dots_of[s][:, GROUP_COL[group] : GROUP_COL[group] + GROUP, :]
                 else:
-                    dots_read = dots[:, ZERO_COL : ZERO_COL + 1, :].to_broadcast([P, GROUP, ROWS])
+                    dots_read = dots_of[s][:, ZERO_COL : ZERO_COL + 1, :].to_broadcast([P, GROUP, PLACES])
                 nc.vector.tensor_tensor(
-                    out=u1[:, slots, :].rearrange("p s (c h) -> p s c h", h=H),
-                    in0=dots_read.rearrange("p s (c h) -> p s c h", h=H),
-                    in1=bias_plus_1[:, slots, :].unsqueeze(2).to_broadcast([P, GROUP, BLOCKS, H]),
+                    out=u1[:, slots, :],
+                    in0=dots_read,
+                    in1=bias_plus_1[:, slots, h : h + 1].to_broadcast([P, GROUP, PLACES]),
                     op=ALU.add,
                 )
-            exp_u = small.tile([P, SLOTS, ROWS], F32)
+            exp_u = table.tile([P, SLOTS, PLACES], F32, offset=0)
             nc.scalar.activation(out=exp_u[:], in_=u1[:], func=ACT.Exp, bias=minus_one_col[:, 0:1])
-            u1_of[t], exp_u_of[t] = u1, exp_u
+            u1_of[s], exp_u_of[s] = u1, exp_u
 
-        def weights(t):
-            u1, exp_u = u1_of[t], exp_u_of[t]
-            feat = small.tile([P, SLOTS, ROWS], F32)
+        def gains_of_slots(s):
+            b, h = STAGES[s]
+            for group, tau in enumerate(TAUS):
+                nc.gpsimd.tensor_scalar(
+                    out=slot_gain[:, group * GROUP : group * GROUP + S, :],
+                    in0=gains_in[:, b, h, :, :].rearrange("p c j -> p j c"),
+                    scalar1=abs(D4[tau]),
+                    scalar2=0.0,
+                    op0=ALU.mult,
+                    op1=ALU.add,
+                )
+            nc.gpsimd.tensor_copy(
+                out=slot_gain[:, LOCAL_SLOT, :], in_=local_gain[:, h : h + 1].to_broadcast([P, PLACES])
+            )
+
+        def shares(s):
+            u1, exp_u = u1_of[s], exp_u_of[s]
             nc.vector.scalar_tensor_tensor(
-                out=feat[:].rearrange("p s r -> p (s r)"),
-                in0=exp_u[:].rearrange("p s r -> p (s r)"),
+                out=exp_u[:].rearrange("p s c -> p (s c)"),
+                in0=exp_u[:].rearrange("p s c -> p (s c)"),
                 scalar=1.0,
-                in1=u1[:].rearrange("p s r -> p (s r)"),
+                in1=u1[:].rearrange("p s c -> p (s c)"),
                 op0=ALU.min,
                 op1=ALU.max,
             )
-            share = small.tile([P, SLOTS, ROWS], F32)
-            nc.vector.tensor_tensor(out=share[:], in0=feat[:], in1=slot_gain[:, t, :, :], op=ALU.mult)
-            weight = small.tile([P, len(OFFSETS), ROWS], F32)
+            nc.vector.tensor_tensor(out=exp_u[:], in0=exp_u[:], in1=slot_gain[:], op=ALU.mult)
+
+        def positive_weights(s):
+            share = exp_u_of[s]
+            positive = table.tile([P, COLS, PLACES], F32, offset=15360)
+            nc.vector.tensor_tensor(
+                out=positive[:, 0:GROUP, :], in0=share[:, 0:GROUP, :], in1=share[:, GROUP - 1 : 2 * GROUP - 1, :], op=ALU.add
+            )
+            nc.vector.tensor_copy(out=positive[:, GROUP : GROUP + S, :], in_=share[:, 2 * GROUP : 2 * GROUP + S, :])
             nc.vector.tensor_reduce(
-                out=weight[:, ZERO_COL, :],
-                in_=share[:, SLOTS - GROUP :, :].rearrange("p s r -> p r s"),
-                axis=mybir.AxisListType.X,
+                out=positive[:, ZERO_COL, :],
+                in_=share[:, SLOTS - GROUP :, :].rearrange("p s c -> p c s"),
+                axis=AXIS.X,
                 op=ALU.add,
             )
+            positive_of[s] = positive
+
+        def weights(s):
+            positive = positive_of[s]
+            weight = table.tile([P, COLS, PLACES], F32, bufs=2, offset=18432)
             nc.vector.tensor_tensor(
-                out=weight[:, 0:GROUP, :], in0=share[:, 0:GROUP, :], in1=share[:, GROUP - 1 : 2 * GROUP - 1, :], op=ALU.add
+                out=weight[:, 0:GROUP, :], in0=positive[:, 0:GROUP, :], in1=reached[:, 0:GROUP, :], op=ALU.mult
             )
-            nc.vector.tensor_scalar_mul(
-                out=weight[:, GROUP : GROUP + S, :], in0=share[:, 2 * GROUP : 2 * GROUP + S, :], scalar1=-1.0
+            nc.vector.scalar_tensor_tensor(
+                out=weight[:, GROUP : GROUP + S, :],
+                in0=positive[:, GROUP : GROUP + S, :],
+                scalar=-1.0,
+                in1=reached[:, GROUP : GROUP + S, :],
+                op0=ALU.mult,
+                op1=ALU.mult,
             )
-            z = small.tile([P, ROWS], F32)
+            nc.vector.tensor_copy(out=weight[:, ZERO_COL, :], in_=positive[:, ZERO_COL, :])
+            z = table.tile([P, PLACES], F32, offset=24576)
             nc.vector.tensor_reduce(
-                out=z[:], in_=share[:].rearrange("p s r -> p r s"), axis=mybir.AxisListType.X, op=ALU.add
+                out=z[:], in_=positive[:].rearrange("p o c -> p c o"), axis=AXIS.X, op=ALU.add
             )
             nc.vector.tensor_scalar_add(out=z[:], in0=z[:], scalar1=1e-06)
-            one_over_z = small.tile([P, ROWS], F32)
+            one_over_z = table.tile([P, PLACES], F32, bufs=2, offset=24704)
             nc.vector.reciprocal(out=one_over_z[:], in_=z[:])
-            weight_of[t], one_over_z_of[t] = weight, one_over_z
+            weight_of[s], one_over_z_of[s] = weight, one_over_z
 
-        def shifted_v(t, col):
-            b, n0, c0 = place(t)
-            first = first_block(col, c0)
-            if first == BLOCKS:
-                return
-            v_ps = psum_v.tile([P, BLOCKS, P], F32)
-            for c in range(first, BLOCKS):
-                start_col = HALO + n0 + c * P - OFFSETS[col]
-                nc.tensor.transpose(v_ps[:, c, :], v_cols_of[b][:, start_col : start_col + P], ident_f32[:])
-            shifted_of[t, col] = v_ps
+        v_near_of, v_far_of, weighted_of, acc_of, acc_cols_of, fin_of = {}, {}, {}, {}, {}, {}
+        v_near, v_far, v_busy = [], [], {}
+        units = [(s, half, i) for s in range(len(STAGES)) for half in range(2) for i in range(COLS)]
+        v_items = []
+        v_last_use = {}
+        for number, (s, half, i) in enumerate(units):
+            col = mix_order(half)[i]
+            for move in moves_of(col):
+                item = (s, half, move) if is_far(col) else (s, None, move)
+                if item not in v_last_use:
+                    v_items.append(item)
+                v_last_use[item] = number
 
-        def mix(t, col):
-            b, n0, c0 = place(t)
-            if col == ZERO_COL:
-                acc = small.tile([P, ROWS, HD], F32)
-                acc_of[t] = acc
-            acc = acc_of[t]
-            for r in range(first_block(col, c0) * H, ROWS):
-                v_head = shifted_of[t, col][:].rearrange("p c (h d) -> p (c h) d", h=H)[:, r, :]
-                if col == ZERO_COL:
-                    nc.vector.tensor_scalar_mul(out=acc[:, r, :], in0=v_head, scalar1=weight_of[t][:, col, r : r + 1])
-                else:
-                    nc.vector.scalar_tensor_tensor(
-                        out=acc[:, r, :],
-                        in0=v_head,
-                        scalar=weight_of[t][:, col, r : r + 1],
-                        in1=acc[:, r, :],
-                        op0=ALU.mult,
-                        op1=ALU.add,
-                    )
+        def make_v_buffers():
+            for i in range(NEAR_MOVES):
+                moved = phase.tile([P, PLACES, HD], F32, offset=8192 * i, name="v_near_%d" % i)
+                nc.gpsimd.memset(moved[:], 0.0)
+                v_near.append(moved)
+            for i in range(3):
+                moved = phase.tile([P, MIX_PLACES, HD], F32, offset=16384 + 4096 * i, name="v_far_%d" % i)
+                nc.gpsimd.memset(moved[:], 0.0)
+                v_far.append(moved)
 
-        def finish(t):
-            b, n0, c0 = place(t)
-            result = small.tile([P, ROWS, HD], F32)
-            for r in range(ROWS):
-                nc.scalar.activation(
-                    out=result[:, r, :], in_=acc_of[t][:, r, :], func=ACT.Copy, scale=one_over_z_of[t][:, r : r + 1]
+        def move_v(number):
+            for item in list(v_busy):
+                if v_last_use[item] < number:
+                    (v_near if item[1] is None else v_far).append(v_busy.pop(item))
+            for near in (True, False):
+                free = v_near if near else v_far
+                waiting = [item for item in v_items if (item[1] is None) == near]
+                while free and waiting:
+                    s, half, move = waiting.pop(0)
+                    v_items.remove((s, half, move))
+                    moved = free.pop(0)
+                    v = v_of[STAGES[s]]
+                    if near:
+                        move_down(moved, v[:], move)
+                        v_near_of[s, move] = moved
+                    else:
+                        move_down(moved, v[:, half * MIX_PLACES : (half + 1) * MIX_PLACES, :], move)
+                        v_far_of[s, half, move] = moved
+                    v_busy[s, half, move] = moved
+
+        def weigh(number, by_vector):
+            s, half, i = units[number]
+            col = mix_order(half)[i]
+            weighted = phase.tile([P, MIX_PLACES, HD], F32, bufs=4, offset=28672)
+            for first, last, move, source in parts(OFFSETS[col]):
+                for place in range(max(first, half * MIX_PLACES), min(last, (half + 1) * MIX_PLACES)):
+                    c = place - half * MIX_PLACES
+                    read = source + place - first
+                    if move == 0:
+                        v_read = v_of[STAGES[s]][:, read, :]
+                    elif is_far(col):
+                        v_read = v_far_of[s, half, move][:, read - half * MIX_PLACES, :]
+                    else:
+                        v_read = v_near_of[s, move][:, read, :]
+                    scale = weight_of[s][:, col, place : place + 1]
+                    if c >= MIX_PLACES - by_vector:
+                        nc.vector.tensor_scalar_mul(out=weighted[:, c, :], in0=v_read, scalar1=scale)
+                    else:
+                        nc.scalar.activation(out=weighted[:, c, :], in_=v_read, func=ACT.Copy, scale=scale)
+            weighted_of[number] = weighted
+
+        def sum_weighted(number):
+            s, half, i = units[number]
+            if i == 0:
+                for bank in range(MIX_CELLS // 4):
+                    acc = psum_acc.tile([P, 4, P], F32, tag="acc")
+                    acc_of[s, half, bank] = acc
+            for cell in range(MIX_CELLS):
+                nc.tensor.matmul(
+                    acc_of[s, half, cell // 4][:, cell % 4, :],
+                    lhsT=weighted_of[number][:, 2 * cell : 2 * cell + 2, :].rearrange("p c d -> p (c d)"),
+                    rhs=ident[:],
+                    start=(i == 0 and cell % 4 == 0),
+                    stop=(i == COLS - 1 and cell % 4 == 3),
+                    is_transpose=True,
                 )
-            nc.sync.dma_start(
-                out=out[b, n0 : n0 + CHUNK, :].rearrange("(c p) f -> p c f", p=P),
-                in_=result[:].rearrange("p (c h) d -> p c (h d)", h=H),
-            )
 
-        def for_chunk(stage, t):
-            if 0 <= t < CHUNKS:
-                stage(t)
+        def mix_out(s, half):
+            acc_cols = phase.tile([P, MIX_CELLS, P], F32, offset=45056)
+            for bank in range(MIX_CELLS // 4):
+                nc.scalar.copy(out=acc_cols[:, 4 * bank : 4 * bank + 4, :], in_=acc_of[s, half, bank][:])
+            acc_cols_of[s, half] = acc_cols
 
-        def for_column(stage, t, step):
-            if 0 <= t < CHUNKS and 0 <= step < len(ORDER):
-                stage(t, ORDER[step])
+        def mix_back(s, half):
+            for bank in range(MIX_CELLS // 4):
+                fin = psum_x.tile([P, 4, P], F32, tag="xt")
+                for cell in range(4):
+                    nc.tensor.transpose(fin[:, cell, :], acc_cols_of[s, half][:, 4 * bank + cell, :], ident[:])
+                fin_of[s, half, bank] = fin
+
+        def finish(s, half):
+            b, h = STAGES[s]
+            for bank in range(MIX_CELLS // 4):
+                place = half * MIX_PLACES + 8 * bank
+                result = phase.tile([P, 8, HD], F32, bufs=2, offset=49152)
+                nc.vector.tensor_tensor(
+                    out=result[:],
+                    in0=fin_of[s, half, bank][:].rearrange("p k (c d) -> p (k c) d", d=HD),
+                    in1=one_over_z_of[s][:, place : place + 8].unsqueeze(2).to_broadcast([P, 8, HD]),
+                    op=ALU.mult,
+                )
+                nc.sync.dma_start(
+                    out=out[b].rearrange("(p c) f -> p c f", c=PLACES)[:, place : place + 8, h * HD : (h + 1) * HD],
+                    in_=result[:],
+                )
 
         with tc.manual_schedule():
-            load_x(0)
-            load_x(1)
-            transpose_x(0)
-            load_x(2)
-            project(0)
-            for t in range(-2, CHUNKS):
-                for_chunk(transpose_x, t + 3)
-                for_chunk(load_x, t + 5)
-                for_chunk(scores, t + 1)
-                for_column(shifted_v, t, 0)
-                for step in range(len(ORDER) + 2):
-                    for_column(product, t + 2, step)
-                    for_column(shifted_v, t, step + 1)
-                    for_column(transpose_product, t + 2, step - 1)
-                    for_column(sum_heads, t + 2, step - 2)
-                    for_column(mix, t, step)
-                    if step == len(ORDER) // 2:
-                        for_chunk(project, t + 3)
-                for_chunk(finish, t)
-                for_chunk(weights, t + 1)
+            transpose_x(0, 0)
+            for j in range(CHUNKS):
+                if j + 2 < CHUNKS:
+                    load_x(0, j + 2)
+                if j + 1 < CHUNKS:
+                    transpose_x(0, j + 1)
+                quantise_x(0, j)
+                multiply(0, j)
+                keep(0, j)
+            move_k(0)
+            load_x(1, 0)
+            load_x(1, 1)
+            gains_of_slots(0)
+
+            dot_steps = len(STAGES) * STEPS
+            last_unit = len(units) - 1
+            first_mix = STEPS + LAG
+            end = first_mix + len(units) // 2 + 5
+            mix_done = {}
+            for t in range(end):
+                s, step = divmod(t, STEPS)
+                if t < dot_steps:
+                    move_k(t)
+                    products(s, step)
+                if 1 <= t <= dot_steps:
+                    sum_products((t - 1) // STEPS, (t - 1) % STEPS)
+                if t < 3 * CHUNKS:
+                    j, turn = divmod(t, 3)
+                    if turn == 0:
+                        transpose_x(1, j)
+                        if j + 2 < CHUNKS:
+                            load_x(1, j + 2)
+                    elif turn == 1:
+                        quantise_x(1, j)
+                        multiply(1, j)
+                    else:
+                        keep(1, j)
+                if t == 3 * CHUNKS:
+                    make_v_buffers()
+                done = s - 1
+                if 0 <= done < len(STAGES):
+                    if step == 0:
+                        dots_out(done)
+                    elif step == 1:
+                        dots_back(done)
+                    elif step == 2:
+                        dots_masked(done)
+                        scores(done)
+                    elif step == 4:
+                        shares(done)
+                        if done + 1 < len(STAGES):
+                            gains_of_slots(done + 1)
+                    elif step == 5:
+                        positive_weights(done)
+                    elif step == 6:
+                        weights(done)
+                first = 2 * (t - first_mix)
+                if t >= 3 * CHUNKS and first <= last_unit:
+                    move_v(max(0, first))
+                for number in (first - 2, first - 1):
+                    if 0 <= number <= last_unit:
+                        sum_weighted(number)
+                for number in (first, first + 1):
+                    if 0 <= number <= last_unit:
+                        weigh(number, 3 if t < dot_steps else 10)
+                        if units[number][2] == COLS - 1:
+                            mix_done[units[number][:2]] = t
+                for stage_half, when in mix_done.items():
+                    if t == when + 2:
+                        mix_out(*stage_half)
+                    elif t == when + 3:
+                        mix_back(*stage_half)
+                    elif t == when + 4:
+                        finish(*stage_half)

@@ -45,6 +45,12 @@ STEPS = 2 * QUADS * PIECES
 MIX_PLACES = PLACES // 2
 MIX_CELLS = MIX_PLACES // 2
 NEAR_MOVES = 2
+PAD = 32
+PLACE_X, PLACE_Y, PLACE_Z = (PAD + (PAD + P) * i for i in range(3))
+K_PLACE = (PLACE_X, PLACE_Z, PLACE_X, PLACE_Y)
+V_PLACE = (PLACE_Y, PLACE_Z, PLACE_X, PLACE_Z)
+K_PARK_STEP = (0, 2, 26, 58)
+V_PARK_STEP = (4, 50, 74, 82)
 LAG = 7
 STAGES = tuple((b, h) for b in range(B) for h in range(H))
 
@@ -172,12 +178,24 @@ def tile_dwarfattention_pa_t_kernel(
             nc.gpsimd.memset(moved[:], 0.0)
             k_moved.append(moved)
 
-        def move_down(dst, src, move):
-            rows = P - move
-            first = rows // 16 * 16 if move < 16 else rows
-            nc.sync.dma_start(out=dst[move : move + first], in_=src[0:first])
-            if first < rows:
-                nc.sync.dma_start(out=dst[move + first : P], in_=src[first:rows])
+        parked = out.rearrange("b (r t) f -> (b r) (t f)", t=16)
+        for place in (PLACE_X, PLACE_Y, PLACE_Z):
+            for part in range(2):
+                nc.sync.dma_start(
+                    out=parked[place - PAD : place, part * 1024 : (part + 1) * 1024],
+                    in_=k_moved[0][0:PAD].rearrange("p d c -> p (d c)"),
+                )
+
+        def load_moved(dst, place, move, columns):
+            first = 0 if move <= PAD else move
+            while first < P:
+                rows = P - first
+                while rows & (rows - 1):
+                    rows = rows & (rows - 1)
+                nc.sync.dma_start(
+                    out=dst[first : first + rows], in_=parked[place + first - move : place + first - move + rows, columns]
+                )
+                first += rows
 
         q_of, k_of, v_of = {}, {}, {}
 
@@ -231,7 +249,7 @@ def tile_dwarfattention_pa_t_kernel(
         def keep(b, j):
             if j == 0:
                 for h in range(H):
-                    q = qkv.tile([P, HD, PLACES], F32)
+                    q = qkv.tile([P, HD, PLACES], F32, tag="q")
                     k = qkv.tile([P, HD, PLACES], F32)
                     v = qkv.tile([P, PLACES, HD], F32)
                     q_of[b, h], k_of[b, h], v_of[b, h] = q, k, v
@@ -275,7 +293,13 @@ def tile_dwarfattention_pa_t_kernel(
             return items, last_use
 
         k_items, k_last_use = k_item_steps()
-        k_free, k_busy = list(k_moved), {}
+        k_free, k_busy, k_parked = list(k_moved), {}, []
+
+        def park_k(s):
+            nc.sync.dma_start(
+                out=parked[K_PLACE[s] : K_PLACE[s] + P, :], in_=k_of[STAGES[s]][:].rearrange("p d c -> p (d c)")
+            )
+            k_parked.append(s)
 
         def move_k(t):
             for item in list(k_busy):
@@ -283,12 +307,14 @@ def tile_dwarfattention_pa_t_kernel(
                     k_free.append(k_busy.pop(item))
             while k_free and k_items:
                 item = k_items.pop(0)
-                if STAGES[item[0]] not in k_of:
+                if item[0] not in k_parked:
                     k_items.insert(0, item)
                     return
                 moved = k_free.pop(0)
                 s, half, move = item
-                move_down(moved, k_of[STAGES[s]][:, half * HALF_D : (half + 1) * HALF_D, :], move)
+                load_moved(
+                    moved[:].rearrange("p d c -> p (d c)"), K_PLACE[s], move, slice(half * HALF_D * PLACES, (half + 1) * HALF_D * PLACES)
+                )
                 k_busy[item] = moved
                 k_buf_of[item] = moved
 
@@ -450,7 +476,14 @@ def tile_dwarfattention_pa_t_kernel(
             weight_of[s], one_over_z_of[s] = weight, one_over_z
 
         v_near_of, v_far_of, weighted_of, acc_of, acc_cols_of, fin_of = {}, {}, {}, {}, {}, {}
-        v_near, v_far, v_busy = [], [], {}
+        v_near, v_far, v_busy, v_parked = [], [], {}, []
+
+        def park_v(s):
+            nc.sync.dma_start(
+                out=parked[V_PLACE[s] : V_PLACE[s] + P, :], in_=v_of[STAGES[s]][:].rearrange("p c d -> p (c d)")
+            )
+            v_parked.append(s)
+
         units = [(s, half, i) for s in range(len(STAGES)) for half in range(2) for i in range(COLS)]
         v_items = []
         v_last_use = {}
@@ -478,17 +511,16 @@ def tile_dwarfattention_pa_t_kernel(
                     (v_near if item[1] is None else v_far).append(v_busy.pop(item))
             for near in (True, False):
                 free = v_near if near else v_far
-                waiting = [item for item in v_items if (item[1] is None) == near]
+                waiting = [item for item in v_items if (item[1] is None) == near and item[0] in v_parked]
                 while free and waiting:
                     s, half, move = waiting.pop(0)
                     v_items.remove((s, half, move))
                     moved = free.pop(0)
-                    v = v_of[STAGES[s]]
+                    columns = slice(0, PLACES * HD) if near else slice(half * MIX_PLACES * HD, (half + 1) * MIX_PLACES * HD)
+                    load_moved(moved[:].rearrange("p c d -> p (c d)"), V_PLACE[s], move, columns)
                     if near:
-                        move_down(moved, v[:], move)
                         v_near_of[s, move] = moved
                     else:
-                        move_down(moved, v[:, half * MIX_PLACES : (half + 1) * MIX_PLACES, :], move)
                         v_far_of[s, half, move] = moved
                     v_busy[s, half, move] = moved
 
@@ -542,21 +574,28 @@ def tile_dwarfattention_pa_t_kernel(
                     nc.tensor.transpose(fin[:, cell, :], acc_cols_of[s, half][:, 4 * bank + cell, :], ident[:])
                 fin_of[s, half, bank] = fin
 
+        result_of = {}
+
         def finish(s, half):
-            b, h = STAGES[s]
+            if half == 0:
+                result = qkv.tile([P, PLACES, HD], F32, tag="q")
+                result_of[s] = result
             for bank in range(MIX_CELLS // 4):
                 place = half * MIX_PLACES + 8 * bank
-                result = phase.tile([P, 8, HD], F32, bufs=2, offset=49152)
                 nc.vector.tensor_tensor(
-                    out=result[:],
+                    out=result_of[s][:, place : place + 8, :],
                     in0=fin_of[s, half, bank][:].rearrange("p k (c d) -> p (k c) d", d=HD),
                     in1=one_over_z_of[s][:, place : place + 8].unsqueeze(2).to_broadcast([P, 8, HD]),
                     op=ALU.mult,
                 )
-                nc.sync.dma_start(
-                    out=out[b].rearrange("(p c) f -> p c f", c=PLACES)[:, place : place + 8, h * HD : (h + 1) * HD],
-                    in_=result[:],
-                )
+
+        def store(s, half):
+            b, h = STAGES[s]
+            places = slice(half * MIX_PLACES, (half + 1) * MIX_PLACES)
+            nc.sync.dma_start(
+                out=out[b].rearrange("(p c) f -> p c f", c=PLACES)[:, places, h * HD : (h + 1) * HD],
+                in_=result_of[s][:, places, :],
+            )
 
         with tc.manual_schedule():
             transpose_x(0, 0)
@@ -568,6 +607,7 @@ def tile_dwarfattention_pa_t_kernel(
                 quantise_x(0, j)
                 multiply(0, j)
                 keep(0, j)
+            park_k(0)
             move_k(0)
             load_x(1, 0)
             load_x(1, 1)
@@ -580,6 +620,11 @@ def tile_dwarfattention_pa_t_kernel(
             mix_done = {}
             for t in range(end):
                 s, step = divmod(t, STEPS)
+                for other in range(1, len(STAGES)):
+                    if t == K_PARK_STEP[other]:
+                        park_k(other)
+                if t in V_PARK_STEP:
+                    park_v(V_PARK_STEP.index(t))
                 if t < dot_steps:
                     move_k(t)
                     products(s, step)
@@ -633,3 +678,10 @@ def tile_dwarfattention_pa_t_kernel(
                         mix_back(*stage_half)
                     elif t == when + 4:
                         finish(*stage_half)
+                if t == dot_steps + LAG + 2:
+                    for done in range(2):
+                        for half in range(2):
+                            store(done, half)
+            for done in range(2, 4):
+                for half in range(2):
+                    store(done, half)

@@ -40,18 +40,20 @@ BANK_QUADS = 4
 STEP_D = 16
 HALF_D = HD // 2
 PIECES = HALF_D // STEP_D
+K_BUFFERS = 8
 QUAD_ORDER = (0, 5, 1, 4, 3, 2)
 STEPS = 2 * QUADS * PIECES
 MIX_PLACES = PLACES // 2
 MIX_CELLS = MIX_PLACES // 2
-NEAR_MOVES = 2
 PAD = 32
-PLACE_X, PLACE_Y, PLACE_Z = (PAD + (PAD + P) * i for i in range(3))
-K_PLACE = (PLACE_X, PLACE_Z, PLACE_X, PLACE_Y)
-V_PLACE = (PLACE_Y, PLACE_Z, PLACE_X, PLACE_Z)
-K_PARK_STEP = (0, 2, 26, 58)
-V_PARK_STEP = (4, 50, 74, 82)
-LAG = 7
+ROW = HD * PLACES
+K_PLACE = (PAD, 2 * PAD + P, PAD, 2 * PAD + P)
+K_PARK_STEP = (0, 2, 26, 50)
+WEIGHT_ROW = COLS * PLACES
+MOST = max(OFFSETS) // PLACES
+WEIGHT_PLACE = tuple((2 * (PAD + P)) * ROW + i * (P + MOST) * WEIGHT_ROW for i in range(2))
+EXTRA_COL = COLS
+LAG = 9
 STAGES = tuple((b, h) for b in range(B) for h in range(H))
 
 FLOPS = 2 * B * N * D * 3 * H * HD + B * H * N * (4 * S + 1) * 4 * HD
@@ -68,23 +70,30 @@ def moves_of(col):
     return tuple(part[2] for part in parts(OFFSETS[col]) if part[2] > 0)
 
 
-def is_far(col):
-    return OFFSETS[col] > NEAR_MOVES * PLACES and OFFSETS[col] % PLACES == 0
+MIX_ORDER = (ZERO_COL,) + tuple(col for col in range(COLS) if col != ZERO_COL)
 
 
-FAR_COLS = tuple(col for col in range(COLS) if is_far(col))
-NEAR_COLS = tuple(col for col in range(COLS) if not is_far(col) and col != ZERO_COL)
+def moved_weight_col(col, part):
+    first, last, move, source = part
+    if move == 0:
+        return None
+    return EXTRA_COL if first == 0 and len(parts(OFFSETS[col])) == 2 and parts(OFFSETS[col])[0][2] > 0 else col
 
 
-def mix_order(half):
-    order = [FAR_COLS[0], ZERO_COL, FAR_COLS[1], FAR_COLS[2]]
-    far, near = list(FAR_COLS[3:]), list(NEAR_COLS)
-    while near:
-        order.append(near[0])
-        near = near[1:]
-        order.extend(far[:1])
-        far = far[1:]
-    return order if half == 0 else list(reversed(order))
+def moved_weight_runs():
+    wanted = []
+    for col in range(COLS):
+        for part in parts(OFFSETS[col]):
+            to = moved_weight_col(col, part)
+            if to is not None:
+                wanted.append((part[2], col, to))
+    runs = []
+    for move, col, to in wanted:
+        if runs and runs[-1][0] == move and runs[-1][2] == col and runs[-1][3] + col - runs[-1][1] == to:
+            runs[-1] = (move, runs[-1][1], col + 1, runs[-1][3])
+        else:
+            runs.append((move, col, col + 1, to))
+    return runs
 
 
 def tile_dwarfattention_pa_t_kernel(
@@ -113,8 +122,10 @@ def tile_dwarfattention_pa_t_kernel(
         load_x(0, 0)
         load_x(0, 1)
 
-        ident = const.tile([P, P], F32)
-        make_identity(nc, ident[:])
+        ident_twice = const.tile([P, 2 * P], F32)
+        make_identity(nc, ident_twice[:, 0:P])
+        make_identity(nc, ident_twice[:, P : 2 * P])
+        ident = ident_twice[:, 0:P]
         one_col = const.tile([P, 1], F32)
         nc.vector.memset(one_col[:], 1.0)
         minus_one_col = const.tile([P, 1], F32)
@@ -173,13 +184,21 @@ def tile_dwarfattention_pa_t_kernel(
             nc.vector.tensor_single_scalar(out=reached[:, col, :], in_=token[:], scalar=float(o), op=ALU.is_ge)
 
         k_moved = []
-        for i in range(6):
+        for i in range(K_BUFFERS):
             moved = const.tile([P, HALF_D, PLACES], F32, name="k_moved_%d" % i)
             nc.gpsimd.memset(moved[:], 0.0)
             k_moved.append(moved)
 
         parked = out.rearrange("b (r t) f -> (b r) (t f)", t=16)
-        for place in (PLACE_X, PLACE_Y, PLACE_Z):
+        flat = out.rearrange("b n f -> (b n f)")
+        weights_parked = [
+            flat[at : at + (P + MOST) * WEIGHT_ROW].rearrange("(r w) -> r w", w=WEIGHT_ROW) for at in WEIGHT_PLACE
+        ]
+        for place in weights_parked:
+            nc.sync.dma_start(
+                out=place[P : P + MOST, :], in_=k_moved[0][0:MOST].rearrange("p d c -> p (d c)")[:, 0:WEIGHT_ROW]
+            )
+        for place in K_PLACE[0:2]:
             for part in range(2):
                 nc.sync.dma_start(
                     out=parked[place - PAD : place, part * 1024 : (part + 1) * 1024],
@@ -211,7 +230,7 @@ def tile_dwarfattention_pa_t_kernel(
                             nc.tensor.transpose(
                                 xt[:, u, c * P : (c + 1) * P],
                                 words[:, g * 2 * P + u : (g + 1) * 2 * P : 2],
-                                ident[:],
+                                ident,
                             )
                     nc.scalar.copy(
                         out=grouped_words[:, half * 2 * P : (half + 1) * 2 * P, :],
@@ -354,14 +373,14 @@ def tile_dwarfattention_pa_t_kernel(
                 nc.tensor.matmul(
                     dots_ps_of[s, bank][:, quad % BANK_QUADS, :],
                     lhsT=prod_of[s, step][:, d, :, :].rearrange("p i c -> p (i c)"),
-                    rhs=ident[:],
+                    rhs=ident,
                     start=(step == steps[0] and d == 0),
                     stop=(step == steps[-1] and d == STEP_D - 1),
                     is_transpose=True,
                 )
 
         turned_of, back_of, dots_of, u1_of, exp_u_of, positive_of = {}, {}, {}, {}, {}, {}
-        weight_of, one_over_z_of = {}, {}
+        weight_of, moved_weight_of, one_over_z_of = {}, {}, {}
 
         def dots_out(s):
             turned = table.tile([P, QUADS, P], F32, offset=0)
@@ -374,7 +393,7 @@ def tile_dwarfattention_pa_t_kernel(
                 quads = range(QUADS)[bank * BANK_QUADS : (bank + 1) * BANK_QUADS]
                 back = psum_x.tile([P, BANK_QUADS, P], F32, tag="xt")
                 for quad in quads:
-                    nc.tensor.transpose(back[:, quad % BANK_QUADS, :], turned_of[s][:, quad, :], ident[:])
+                    nc.tensor.transpose(back[:, quad % BANK_QUADS, :], turned_of[s][:, quad, :], ident)
                 back_of[s, bank] = back
 
         def dots_masked(s):
@@ -454,6 +473,7 @@ def tile_dwarfattention_pa_t_kernel(
         def weights(s):
             positive = positive_of[s]
             weight = table.tile([P, COLS, PLACES], F32, bufs=2, offset=18432)
+            weight_of[s] = weight
             nc.vector.tensor_tensor(
                 out=weight[:, 0:GROUP, :], in0=positive[:, 0:GROUP, :], in1=reached[:, 0:GROUP, :], op=ALU.mult
             )
@@ -473,76 +493,57 @@ def tile_dwarfattention_pa_t_kernel(
             nc.vector.tensor_scalar_add(out=z[:], in0=z[:], scalar1=1e-06)
             one_over_z = table.tile([P, PLACES], F32, bufs=2, offset=24704)
             nc.vector.reciprocal(out=one_over_z[:], in_=z[:])
-            weight_of[s], one_over_z_of[s] = weight, one_over_z
+            one_over_z_of[s] = one_over_z
 
-        v_near_of, v_far_of, weighted_of, acc_of, acc_cols_of, fin_of = {}, {}, {}, {}, {}, {}
-        v_near, v_far, v_busy, v_parked = [], [], {}, []
+        def move_weights(s):
+            place = weights_parked[s % 2]
+            nc.sync.dma_start(out=place[0:P, :], in_=weight_of[s][:].rearrange("p o c -> p (o c)"))
+            moved = table.tile([P, COLS + 1, PLACES], F32, bufs=2, offset=24960)
+            for move, first, last, to in moved_weight_runs():
+                nc.sync.dma_start(
+                    out=moved[:, to : to + last - first, :].rearrange("p o c -> p (o c)"),
+                    in_=place[move : move + P, first * PLACES : last * PLACES],
+                )
+            moved_weight_of[s] = moved
 
-        def park_v(s):
-            nc.sync.dma_start(
-                out=parked[V_PLACE[s] : V_PLACE[s] + P, :], in_=v_of[STAGES[s]][:].rearrange("p c d -> p (c d)")
-            )
-            v_parked.append(s)
-
+        weighted_of, acc_of, acc_cols_of, fin_of = {}, {}, {}, {}
         units = [(s, half, i) for s in range(len(STAGES)) for half in range(2) for i in range(COLS)]
-        v_items = []
-        v_last_use = {}
-        for number, (s, half, i) in enumerate(units):
-            col = mix_order(half)[i]
-            for move in moves_of(col):
-                item = (s, half, move) if is_far(col) else (s, None, move)
-                if item not in v_last_use:
-                    v_items.append(item)
-                v_last_use[item] = number
 
-        def make_v_buffers():
-            for i in range(NEAR_MOVES):
-                moved = phase.tile([P, PLACES, HD], F32, offset=8192 * i, name="v_near_%d" % i)
-                nc.gpsimd.memset(moved[:], 0.0)
-                v_near.append(moved)
-            for i in range(3):
-                moved = phase.tile([P, MIX_PLACES, HD], F32, offset=16384 + 4096 * i, name="v_far_%d" % i)
-                nc.gpsimd.memset(moved[:], 0.0)
-                v_far.append(moved)
-
-        def move_v(number):
-            for item in list(v_busy):
-                if v_last_use[item] < number:
-                    (v_near if item[1] is None else v_far).append(v_busy.pop(item))
-            for near in (True, False):
-                free = v_near if near else v_far
-                waiting = [item for item in v_items if (item[1] is None) == near and item[0] in v_parked]
-                while free and waiting:
-                    s, half, move = waiting.pop(0)
-                    v_items.remove((s, half, move))
-                    moved = free.pop(0)
-                    columns = slice(0, PLACES * HD) if near else slice(half * MIX_PLACES * HD, (half + 1) * MIX_PLACES * HD)
-                    load_moved(moved[:].rearrange("p c d -> p (c d)"), V_PLACE[s], move, columns)
-                    if near:
-                        v_near_of[s, move] = moved
-                    else:
-                        v_far_of[s, half, move] = moved
-                    v_busy[s, half, move] = moved
+        def cells(col, half):
+            found = []
+            for cell in range(MIX_CELLS):
+                place = half * MIX_PLACES + 2 * cell
+                moves = [[part[2] for part in parts(OFFSETS[col]) if part[0] <= p < part[1]][0] for p in (place, place + 1)]
+                if moves[0] == moves[1]:
+                    found.append((cell, 2 * cell, moves[0]))
+                else:
+                    found.append((cell, 2 * cell, moves[0]))
+                    found.append((cell, MIX_PLACES, moves[1]))
+            return found
 
         def weigh(number, by_vector):
             s, half, i = units[number]
-            col = mix_order(half)[i]
-            weighted = phase.tile([P, MIX_PLACES, HD], F32, bufs=4, offset=28672)
-            for first, last, move, source in parts(OFFSETS[col]):
+            col = MIX_ORDER[i]
+            weighted = phase.tile([P, MIX_PLACES + 2, HD], F32, bufs=4, offset=0)
+            split = [found[0] for found in cells(col, half) if found[1] == MIX_PLACES]
+            for cell in split:
+                nc.vector.memset(weighted[:, 2 * cell + 1, :], 0.0)
+                nc.vector.memset(weighted[:, MIX_PLACES, :], 0.0)
+            for part in parts(OFFSETS[col]):
+                first, last, move, source = part
+                moved_col = moved_weight_col(col, part)
                 for place in range(max(first, half * MIX_PLACES), min(last, (half + 1) * MIX_PLACES)):
                     c = place - half * MIX_PLACES
-                    read = source + place - first
-                    if move == 0:
-                        v_read = v_of[STAGES[s]][:, read, :]
-                    elif is_far(col):
-                        v_read = v_far_of[s, half, move][:, read - half * MIX_PLACES, :]
+                    slot = MIX_PLACES + 1 if c % 2 == 1 and c // 2 in split else c
+                    v_read = v_of[STAGES[s]][:, source + place - first, :]
+                    if moved_col is None:
+                        scale = weight_of[s][:, col, place : place + 1]
                     else:
-                        v_read = v_near_of[s, move][:, read, :]
-                    scale = weight_of[s][:, col, place : place + 1]
+                        scale = moved_weight_of[s][:, moved_col, place : place + 1]
                     if c >= MIX_PLACES - by_vector:
-                        nc.vector.tensor_scalar_mul(out=weighted[:, c, :], in0=v_read, scalar1=scale)
+                        nc.vector.tensor_scalar_mul(out=weighted[:, slot, :], in0=v_read, scalar1=scale)
                     else:
-                        nc.scalar.activation(out=weighted[:, c, :], in_=v_read, func=ACT.Copy, scale=scale)
+                        nc.scalar.activation(out=weighted[:, slot, :], in_=v_read, func=ACT.Copy, scale=scale)
             weighted_of[number] = weighted
 
         def sum_weighted(number):
@@ -551,18 +552,18 @@ def tile_dwarfattention_pa_t_kernel(
                 for bank in range(MIX_CELLS // 4):
                     acc = psum_acc.tile([P, 4, P], F32, tag="acc")
                     acc_of[s, half, bank] = acc
-            for cell in range(MIX_CELLS):
+            for cell, slot, move in cells(MIX_ORDER[i], half):
                 nc.tensor.matmul(
                     acc_of[s, half, cell // 4][:, cell % 4, :],
-                    lhsT=weighted_of[number][:, 2 * cell : 2 * cell + 2, :].rearrange("p c d -> p (c d)"),
-                    rhs=ident[:],
+                    lhsT=weighted_of[number][:, slot : slot + 2, :].rearrange("p c d -> p (c d)"),
+                    rhs=ident_twice[:, P - move : 2 * P - move],
                     start=(i == 0 and cell % 4 == 0),
                     stop=(i == COLS - 1 and cell % 4 == 3),
                     is_transpose=True,
                 )
 
         def mix_out(s, half):
-            acc_cols = phase.tile([P, MIX_CELLS, P], F32, offset=45056)
+            acc_cols = phase.tile([P, MIX_CELLS, P], F32, offset=20480)
             for bank in range(MIX_CELLS // 4):
                 nc.scalar.copy(out=acc_cols[:, 4 * bank : 4 * bank + 4, :], in_=acc_of[s, half, bank][:])
             acc_cols_of[s, half] = acc_cols
@@ -571,7 +572,7 @@ def tile_dwarfattention_pa_t_kernel(
             for bank in range(MIX_CELLS // 4):
                 fin = psum_x.tile([P, 4, P], F32, tag="xt")
                 for cell in range(4):
-                    nc.tensor.transpose(fin[:, cell, :], acc_cols_of[s, half][:, 4 * bank + cell, :], ident[:])
+                    nc.tensor.transpose(fin[:, cell, :], acc_cols_of[s, half][:, 4 * bank + cell, :], ident)
                 fin_of[s, half, bank] = fin
 
         result_of = {}
@@ -623,8 +624,6 @@ def tile_dwarfattention_pa_t_kernel(
                 for other in range(1, len(STAGES)):
                     if t == K_PARK_STEP[other]:
                         park_k(other)
-                if t in V_PARK_STEP:
-                    park_v(V_PARK_STEP.index(t))
                 if t < dot_steps:
                     move_k(t)
                     products(s, step)
@@ -641,8 +640,6 @@ def tile_dwarfattention_pa_t_kernel(
                         multiply(1, j)
                     else:
                         keep(1, j)
-                if t == 3 * CHUNKS:
-                    make_v_buffers()
                 done = s - 1
                 if 0 <= done < len(STAGES):
                     if step == 0:
@@ -660,15 +657,14 @@ def tile_dwarfattention_pa_t_kernel(
                         positive_weights(done)
                     elif step == 6:
                         weights(done)
+                        move_weights(done)
                 first = 2 * (t - first_mix)
-                if t >= 3 * CHUNKS and first <= last_unit:
-                    move_v(max(0, first))
                 for number in (first - 2, first - 1):
                     if 0 <= number <= last_unit:
                         sum_weighted(number)
                 for number in (first, first + 1):
                     if 0 <= number <= last_unit:
-                        weigh(number, 3 if t < dot_steps else 10)
+                        weigh(number, 0 if t < dot_steps else 9)
                         if units[number][2] == COLS - 1:
                             mix_done[units[number][:2]] = t
                 for stage_half, when in mix_done.items():
@@ -678,7 +674,7 @@ def tile_dwarfattention_pa_t_kernel(
                         mix_back(*stage_half)
                     elif t == when + 4:
                         finish(*stage_half)
-                if t == dot_steps + LAG + 2:
+                if t == dot_steps + 4:
                     for done in range(2):
                         for half in range(2):
                             store(done, half)

@@ -30,31 +30,34 @@ COLS = len(OFFSETS)
 ZERO_COL = COLS - 1
 GROUP = S + 1
 TAUS = (1, 2, 3, 0)
-GROUP_COL = (0, 1, GROUP)
-SLOTS = GROUP * len(TAUS)
-LOCAL_SLOT = SLOTS - 1
+GROUP_COL = (0, 1, GROUP, ZERO_COL)
+HALF_COLS = COLS // 2
+HALF_SLOTS = 2 * GROUP
 
 QUAD = P // PLACES
 QUADS = COLS // QUAD
-BANK_QUADS = 4
-STEP_D = 16
-HALF_D = HD // 2
-PIECES = HALF_D // STEP_D
-K_BUFFERS = 8
-QUAD_ORDER = (0, 5, 1, 4, 3, 2)
-STEPS = 2 * QUADS * PIECES
+GROUP_QUADS = QUADS // 2
+STEP_D = 8
+QUARTER_D = HD // 4
+PIECES = QUARTER_D // STEP_D
+STEPS = 4 * PIECES
+K_BUFFERS = 16
+UNITS_A_STEP = 2 * HALF_COLS // STEPS
 MIX_PLACES = PLACES // 2
 MIX_CELLS = MIX_PLACES // 2
 PAD = 32
 ROW = HD * PLACES
 K_PLACE = (PAD, 2 * PAD + P, PAD, 2 * PAD + P)
-K_PARK_STEP = (0, 2, 26, 50)
-WEIGHT_ROW = COLS * PLACES
+K_PARK_STEP = (0, 2, 2 * STEPS + 2, 4 * STEPS + 2)
+WEIGHT_ROW = HALF_COLS * PLACES
 MOST = max(OFFSETS) // PLACES
 WEIGHT_PLACE = tuple((2 * (PAD + P)) * ROW + i * (P + MOST) * WEIGHT_ROW for i in range(2))
-EXTRA_COL = COLS
-LAG = 9
+MASKED_COLS = tuple(col for col in range(COLS) if OFFSETS[col] > PAD * PLACES)
+EXTRA_COL = HALF_COLS
+HEAD = 2
+LAG = 6
 STAGES = tuple((b, h) for b in range(B) for h in range(H))
+HALF_STAGES = 2 * len(STAGES)
 
 FLOPS = 2 * B * N * D * 3 * H * HD + B * H * N * (4 * S + 1) * 4 * HD
 
@@ -70,23 +73,23 @@ def moves_of(col):
     return tuple(part[2] for part in parts(OFFSETS[col]) if part[2] > 0)
 
 
-MIX_ORDER = (ZERO_COL,) + tuple(col for col in range(COLS) if col != ZERO_COL)
+MIX_ORDER = (tuple(range(2, HALF_COLS)) + (0, 1), (ZERO_COL,) + tuple(range(HALF_COLS, ZERO_COL)))
 
 
 def moved_weight_col(col, part):
     first, last, move, source = part
     if move == 0:
         return None
-    return EXTRA_COL if first == 0 and len(parts(OFFSETS[col])) == 2 and parts(OFFSETS[col])[0][2] > 0 else col
+    return EXTRA_COL if first == 0 and len(parts(OFFSETS[col])) == 2 and parts(OFFSETS[col])[0][2] > 0 else col % HALF_COLS
 
 
-def moved_weight_runs():
+def moved_weight_runs(group):
     wanted = []
-    for col in range(COLS):
+    for col in range(group * HALF_COLS, (group + 1) * HALF_COLS):
         for part in parts(OFFSETS[col]):
             to = moved_weight_col(col, part)
             if to is not None:
-                wanted.append((part[2], col, to))
+                wanted.append((part[2], col % HALF_COLS, to))
     runs = []
     for move, col, to in wanted:
         if runs and runs[-1][0] == move and runs[-1][2] == col and runs[-1][3] + col - runs[-1][1] == to:
@@ -103,11 +106,11 @@ def tile_dwarfattention_pa_t_kernel(
     with ExitStack() as ctx:
         const = ctx.enter_context(tc.tile_pool(name="const", bufs=1))
         qkv = ctx.enter_context(tc.tile_pool(name="qkv", bufs=4))
-        prods = ctx.enter_context(tc.tile_pool(name="prods", bufs=2))
+        prods = ctx.enter_context(tc.tile_pool(name="prods", bufs=3))
         table = ctx.enter_context(tc.tile_pool(name="table", bufs=1))
         phase = ctx.enter_context(tc.tile_pool(name="phase", bufs=1))
         psum_x = ctx.enter_context(tc.psum_pool(name="psum_x", bufs=2))
-        psum_dots = ctx.enter_context(tc.psum_pool(name="psum_dots", bufs=1))
+        psum_dots = ctx.enter_context(tc.psum_pool(name="psum_dots", bufs=2))
         psum_acc = ctx.enter_context(tc.psum_pool(name="psum_acc", bufs=4))
 
         x_rows_of, grouped_of, codes_of, qkv_ps_of = {}, {}, {}, {}
@@ -147,7 +150,7 @@ def tile_dwarfattention_pa_t_kernel(
 
         pos_bias_all = const.tile([P, 4 * S * H], BF16)
         nc.sync.dma_start(out=pos_bias_all[:], in_=pos_bias.rearrange("r h -> (r h)").partition_broadcast(P))
-        bias_plus_1 = const.tile([P, SLOTS, H], F32)
+        bias_plus_1 = const.tile([P, len(TAUS) * GROUP, H], F32)
         nc.vector.memset(bias_plus_1[:], 1.0)
         for group, tau in enumerate(TAUS):
             nc.vector.tensor_scalar_add(
@@ -172,20 +175,20 @@ def tile_dwarfattention_pa_t_kernel(
         gains_in = const.tile([P, B, H, PLACES, S], BF16)
         for b, h in STAGES:
             nc.sync.dma_start(out=gains_in[:, b, h, :, :], in_=gains[b, h].rearrange("(p c) j -> p c j", c=PLACES))
-        slot_gain = const.tile([P, SLOTS, PLACES], F32)
+        slot_gain = const.tile([P, HALF_SLOTS, PLACES], F32)
         nc.gpsimd.memset(slot_gain[:], 0.0)
 
         token = const.tile([P, PLACES], F32)
         nc.gpsimd.iota(
             token[:], pattern=[[1, PLACES]], base=0, channel_multiplier=PLACES, allow_small_or_imprecise_dtypes=True
         )
-        reached = const.tile([P, COLS, PLACES], F32)
-        for col, o in enumerate(OFFSETS):
-            nc.vector.tensor_single_scalar(out=reached[:, col, :], in_=token[:], scalar=float(o), op=ALU.is_ge)
+        reached = const.tile([P, len(MASKED_COLS), PLACES], F32)
+        for i, col in enumerate(MASKED_COLS):
+            nc.vector.tensor_single_scalar(out=reached[:, i, :], in_=token[:], scalar=float(OFFSETS[col]), op=ALU.is_ge)
 
         k_moved = []
         for i in range(K_BUFFERS):
-            moved = const.tile([P, HALF_D, PLACES], F32, name="k_moved_%d" % i)
+            moved = const.tile([P, QUARTER_D, PLACES], F32, name="k_moved_%d" % i)
             nc.gpsimd.memset(moved[:], 0.0)
             k_moved.append(moved)
 
@@ -195,13 +198,16 @@ def tile_dwarfattention_pa_t_kernel(
             flat[at : at + (P + MOST) * WEIGHT_ROW].rearrange("(r w) -> r w", w=WEIGHT_ROW) for at in WEIGHT_PLACE
         ]
         for place in weights_parked:
-            nc.sync.dma_start(
-                out=place[P : P + MOST, :], in_=k_moved[0][0:MOST].rearrange("p d c -> p (d c)")[:, 0:WEIGHT_ROW]
-            )
-        for place in K_PLACE[0:2]:
-            for part in range(2):
+            for part in range(0, WEIGHT_ROW, QUARTER_D * PLACES):
+                width = min(QUARTER_D * PLACES, WEIGHT_ROW - part)
                 nc.sync.dma_start(
-                    out=parked[place - PAD : place, part * 1024 : (part + 1) * 1024],
+                    out=place[P : P + MOST, part : part + width],
+                    in_=k_moved[0][0:MOST].rearrange("p d c -> p (d c)")[:, 0:width],
+                )
+        for place in K_PLACE[0:2]:
+            for part in range(0, ROW, QUARTER_D * PLACES):
+                nc.sync.dma_start(
+                    out=parked[place - PAD : place, part : part + QUARTER_D * PLACES],
                     in_=k_moved[0][0:PAD].rearrange("p d c -> p (d c)"),
                 )
 
@@ -293,22 +299,19 @@ def tile_dwarfattention_pa_t_kernel(
 
         prod_of, dots_ps_of, k_buf_of = {}, {}, {}
 
-        def step_place(step):
-            half, rest = divmod(step, QUADS * PIECES)
-            i, piece = divmod(rest, PIECES)
-            return half, QUAD_ORDER[i], piece
+        def columns_of(u):
+            return range(u % 2 * HALF_COLS, (u % 2 + 1) * HALF_COLS)
 
         def k_item_steps():
             items, last_use = [], {}
-            for s in range(len(STAGES)):
+            for u in range(HALF_STAGES):
                 for step in range(STEPS):
-                    half, quad, piece = step_place(step)
-                    for col in range(quad * QUAD, (quad + 1) * QUAD):
+                    for col in columns_of(u):
                         for move in moves_of(col):
-                            item = (s, half, move)
+                            item = (u, step // PIECES, move)
                             if item not in last_use:
                                 items.append(item)
-                            last_use[item] = s * STEPS + step
+                            last_use[item] = u * STEPS + step
             return items, last_use
 
         k_items, k_last_use = k_item_steps()
@@ -326,188 +329,177 @@ def tile_dwarfattention_pa_t_kernel(
                     k_free.append(k_busy.pop(item))
             while k_free and k_items:
                 item = k_items.pop(0)
-                if item[0] not in k_parked:
+                if item[0] // 2 not in k_parked:
                     k_items.insert(0, item)
                     return
                 moved = k_free.pop(0)
-                s, half, move = item
-                load_moved(
-                    moved[:].rearrange("p d c -> p (d c)"), K_PLACE[s], move, slice(half * HALF_D * PLACES, (half + 1) * HALF_D * PLACES)
-                )
+                u, quarter, move = item
+                d_columns = slice(quarter * QUARTER_D * PLACES, (quarter + 1) * QUARTER_D * PLACES)
+                load_moved(moved[:].rearrange("p d c -> p (d c)"), K_PLACE[u // 2], move, d_columns)
                 k_busy[item] = moved
                 k_buf_of[item] = moved
 
-        def products(s, step):
-            half, quad, piece = step_place(step)
-            d0 = half * HALF_D + piece * STEP_D
-            prod = prods.tile([P, STEP_D, QUAD, PLACES], F32)
-            for i in range(QUAD):
-                for first, last, move, source in parts(OFFSETS[quad * QUAD + i]):
+        def products(u, step):
+            quarter, piece = divmod(step, PIECES)
+            stage = STAGES[u // 2]
+            d0 = step * STEP_D
+            prod = prods.tile([P, STEP_D, GROUP_QUADS, QUAD, PLACES], F32)
+            for i, col in enumerate(columns_of(u)):
+                for first, last, move, source in parts(OFFSETS[col]):
                     if move == 0:
-                        k_read = k_of[STAGES[s]][:, d0 : d0 + STEP_D, :]
+                        k_read = k_of[stage][:, d0 : d0 + STEP_D, :]
                     else:
-                        k_read = k_buf_of[s, half, move][:, piece * STEP_D : (piece + 1) * STEP_D, :]
+                        k_read = k_buf_of[u, quarter, move][:, piece * STEP_D : (piece + 1) * STEP_D, :]
                     nc.vector.tensor_tensor(
-                        out=prod[:, :, i, first:last],
-                        in0=q_of[STAGES[s]][:, d0 : d0 + STEP_D, first:last],
+                        out=prod[:, :, i // QUAD, i % QUAD, first:last],
+                        in0=q_of[stage][:, d0 : d0 + STEP_D, first:last],
                         in1=k_read[:, :, source : source + last - first],
                         op=ALU.mult,
                     )
-            prod_of[s, step] = prod
+            prod_of[u, step] = prod
 
-        def bank_steps(bank):
-            return [step for step in range(STEPS) if step_place(step)[1] // BANK_QUADS == bank]
-
-        def sum_products(s, step):
-            half, quad, piece = step_place(step)
-            bank = quad // BANK_QUADS
-            steps = bank_steps(bank)
-            if step == steps[0]:
-                if bank == 0:
-                    dots_a = psum_dots.tile([P, BANK_QUADS, P], F32)
-                    dots_ps_of[s, bank] = dots_a
-                else:
-                    dots_b = psum_dots.tile([P, QUADS - BANK_QUADS, P], F32)
-                    dots_ps_of[s, bank] = dots_b
+        def sum_products(u, step):
+            if step == 0:
+                dots_ps = psum_dots.tile([P, GROUP_QUADS, P], F32)
+                dots_ps_of[u] = dots_ps
             for d in range(STEP_D):
-                nc.tensor.matmul(
-                    dots_ps_of[s, bank][:, quad % BANK_QUADS, :],
-                    lhsT=prod_of[s, step][:, d, :, :].rearrange("p i c -> p (i c)"),
-                    rhs=ident,
-                    start=(step == steps[0] and d == 0),
-                    stop=(step == steps[-1] and d == STEP_D - 1),
-                    is_transpose=True,
-                )
+                for quad in range(GROUP_QUADS):
+                    nc.tensor.matmul(
+                        dots_ps_of[u][:, quad, :],
+                        lhsT=prod_of[u, step][:, d, quad, :, :].rearrange("p i c -> p (i c)"),
+                        rhs=ident,
+                        start=(step == 0 and d == 0 and quad == 0),
+                        stop=(step == STEPS - 1 and d == STEP_D - 1 and quad == GROUP_QUADS - 1),
+                        is_transpose=True,
+                    )
 
-        turned_of, back_of, dots_of, u1_of, exp_u_of, positive_of = {}, {}, {}, {}, {}, {}
-        weight_of, moved_weight_of, one_over_z_of = {}, {}, {}
+        turned_of, dots_of, u1_of, exp_u_of, positive_of = {}, {}, {}, {}, {}
+        weight_of, moved_weight_of = {}, {}
+        z_of, one_over_z_of = {}, {}
 
-        def dots_out(s):
-            turned = table.tile([P, QUADS, P], F32, offset=0)
-            nc.scalar.copy(out=turned[:, 0:BANK_QUADS, :], in_=dots_ps_of[s, 0][:])
-            nc.scalar.copy(out=turned[:, BANK_QUADS:QUADS, :], in_=dots_ps_of[s, 1][:])
-            turned_of[s] = turned
+        def dots_out(u):
+            turned = table.tile([P, GROUP_QUADS, P], F32, offset=0)
+            nc.scalar.copy(out=turned[:], in_=dots_ps_of[u][:])
+            turned_of[u] = turned
 
-        def dots_back(s):
-            for bank in range(2):
-                quads = range(QUADS)[bank * BANK_QUADS : (bank + 1) * BANK_QUADS]
-                back = psum_x.tile([P, BANK_QUADS, P], F32, tag="xt")
-                for quad in quads:
-                    nc.tensor.transpose(back[:, quad % BANK_QUADS, :], turned_of[s][:, quad, :], ident)
-                back_of[s, bank] = back
+        def dots_back(u):
+            back = psum_x.tile([P, GROUP_QUADS, P], F32, tag="xt")
+            for quad in range(GROUP_QUADS):
+                nc.tensor.transpose(back[:, quad, :], turned_of[u][:, quad, :], ident)
+            dots = table.tile([P, HALF_COLS, PLACES], F32, offset=6144)
+            nc.scalar.copy(out=dots[:], in_=back[:].rearrange("p q (i c) -> p (q i) c", i=QUAD))
+            dots_of[u] = dots
 
-        def dots_masked(s):
-            dots = table.tile([P, COLS, PLACES], F32, offset=12288)
-            for bank in range(2):
-                first = bank * BANK_QUADS * QUAD
-                last = min(COLS, first + BANK_QUADS * QUAD)
-                nc.vector.tensor_tensor(
-                    out=dots[:, first:last, :],
-                    in0=back_of[s, bank][:].rearrange("p q (i c) -> p (q i) c", i=QUAD)[:, 0 : last - first, :],
-                    in1=reached[:, first:last, :],
-                    op=ALU.mult,
-                )
-            dots_of[s] = dots
+        def mask_dots(u):
+            for i, col in enumerate(MASKED_COLS):
+                if col in columns_of(u):
+                    dot = dots_of[u][:, col % HALF_COLS, :]
+                    nc.vector.tensor_tensor(out=dot, in0=dot, in1=reached[:, i, :], op=ALU.mult)
 
-        def scores(s):
-            h = STAGES[s][1]
-            u1 = table.tile([P, SLOTS, PLACES], F32, offset=6144)
-            for group in range(len(TAUS)):
-                slots = slice(group * GROUP, (group + 1) * GROUP)
-                if group < len(GROUP_COL):
-                    dots_read = dots_of[s][:, GROUP_COL[group] : GROUP_COL[group] + GROUP, :]
+        def scores(u):
+            h = STAGES[u // 2][1]
+            u1 = table.tile([P, HALF_SLOTS, PLACES], F32, offset=3072)
+            for i in range(2):
+                group = u % 2 * 2 + i
+                col = GROUP_COL[group] % HALF_COLS
+                slots = min(GROUP, HALF_COLS - col) if TAUS[group] > 0 else GROUP
+                if TAUS[group] > 0:
+                    dots_read = dots_of[u][:, col : col + slots, :]
                 else:
-                    dots_read = dots_of[s][:, ZERO_COL : ZERO_COL + 1, :].to_broadcast([P, GROUP, PLACES])
+                    dots_read = dots_of[u][:, col : col + 1, :].to_broadcast([P, slots, PLACES])
+                at = group * GROUP
                 nc.vector.tensor_tensor(
-                    out=u1[:, slots, :],
+                    out=u1[:, i * GROUP : i * GROUP + slots, :],
                     in0=dots_read,
-                    in1=bias_plus_1[:, slots, h : h + 1].to_broadcast([P, GROUP, PLACES]),
+                    in1=bias_plus_1[:, at : at + slots, h : h + 1].to_broadcast([P, slots, PLACES]),
                     op=ALU.add,
                 )
-            exp_u = table.tile([P, SLOTS, PLACES], F32, offset=0)
-            nc.scalar.activation(out=exp_u[:], in_=u1[:], func=ACT.Exp, bias=minus_one_col[:, 0:1])
-            u1_of[s], exp_u_of[s] = u1, exp_u
+            used = GROUP + slots
+            exp_u = table.tile([P, HALF_SLOTS, PLACES], F32, offset=0)
+            nc.scalar.activation(out=exp_u[:, 0:used, :], in_=u1[:, 0:used, :], func=ACT.Exp, bias=minus_one_col[:, 0:1])
+            u1_of[u], exp_u_of[u] = u1, exp_u
 
-        def gains_of_slots(s):
-            b, h = STAGES[s]
-            for group, tau in enumerate(TAUS):
+        def gains_of_slots(u):
+            b, h = STAGES[u // 2]
+            for i in range(2):
+                tau = TAUS[u % 2 * 2 + i]
                 nc.gpsimd.tensor_scalar(
-                    out=slot_gain[:, group * GROUP : group * GROUP + S, :],
+                    out=slot_gain[:, i * GROUP : i * GROUP + S, :],
                     in0=gains_in[:, b, h, :, :].rearrange("p c j -> p j c"),
                     scalar1=abs(D4[tau]),
                     scalar2=0.0,
                     op0=ALU.mult,
                     op1=ALU.add,
                 )
-            nc.gpsimd.tensor_copy(
-                out=slot_gain[:, LOCAL_SLOT, :], in_=local_gain[:, h : h + 1].to_broadcast([P, PLACES])
-            )
+                if tau == 0:
+                    nc.gpsimd.tensor_copy(
+                        out=slot_gain[:, HALF_SLOTS - 1, :], in_=local_gain[:, h : h + 1].to_broadcast([P, PLACES])
+                    )
 
-        def shares(s):
-            u1, exp_u = u1_of[s], exp_u_of[s]
+        def shares(u):
+            used = HALF_SLOTS - 1 if u % 2 == 0 else HALF_SLOTS
+            u1, exp_u = u1_of[u][:, 0:used, :], exp_u_of[u][:, 0:used, :]
             nc.vector.scalar_tensor_tensor(
-                out=exp_u[:].rearrange("p s c -> p (s c)"),
-                in0=exp_u[:].rearrange("p s c -> p (s c)"),
+                out=exp_u.rearrange("p s c -> p (s c)"),
+                in0=exp_u.rearrange("p s c -> p (s c)"),
                 scalar=1.0,
-                in1=u1[:].rearrange("p s c -> p (s c)"),
+                in1=u1.rearrange("p s c -> p (s c)"),
                 op0=ALU.min,
                 op1=ALU.max,
             )
-            nc.vector.tensor_tensor(out=exp_u[:], in0=exp_u[:], in1=slot_gain[:], op=ALU.mult)
+            nc.vector.tensor_tensor(out=exp_u, in0=exp_u, in1=slot_gain[:, 0:used, :], op=ALU.mult)
 
-        def positive_weights(s):
-            share = exp_u_of[s]
-            positive = table.tile([P, COLS, PLACES], F32, offset=15360)
-            nc.vector.tensor_tensor(
-                out=positive[:, 0:GROUP, :], in0=share[:, 0:GROUP, :], in1=share[:, GROUP - 1 : 2 * GROUP - 1, :], op=ALU.add
-            )
-            nc.vector.tensor_copy(out=positive[:, GROUP : GROUP + S, :], in_=share[:, 2 * GROUP : 2 * GROUP + S, :])
-            nc.vector.tensor_reduce(
-                out=positive[:, ZERO_COL, :],
-                in_=share[:, SLOTS - GROUP :, :].rearrange("p s c -> p c s"),
-                axis=AXIS.X,
-                op=ALU.add,
-            )
-            positive_of[s] = positive
+        def positive_weights(u):
+            share = exp_u_of[u]
+            positive = table.tile([P, HALF_COLS, PLACES], F32, offset=7680)
+            if u % 2 == 0:
+                nc.vector.tensor_tensor(
+                    out=positive[:], in0=share[:, 0:GROUP, :], in1=share[:, GROUP - 1 : 2 * GROUP - 1, :], op=ALU.add
+                )
+            else:
+                nc.vector.tensor_copy(out=positive[:, 0:S, :], in_=share[:, 0:S, :])
+                nc.vector.tensor_reduce(
+                    out=positive[:, S, :],
+                    in_=share[:, GROUP:, :].rearrange("p s c -> p c s"),
+                    axis=AXIS.X,
+                    op=ALU.add,
+                )
+            positive_of[u] = positive
 
-        def weights(s):
-            positive = positive_of[s]
-            weight = table.tile([P, COLS, PLACES], F32, bufs=2, offset=18432)
-            weight_of[s] = weight
-            nc.vector.tensor_tensor(
-                out=weight[:, 0:GROUP, :], in0=positive[:, 0:GROUP, :], in1=reached[:, 0:GROUP, :], op=ALU.mult
-            )
-            nc.vector.scalar_tensor_tensor(
-                out=weight[:, GROUP : GROUP + S, :],
-                in0=positive[:, GROUP : GROUP + S, :],
-                scalar=-1.0,
-                in1=reached[:, GROUP : GROUP + S, :],
-                op0=ALU.mult,
-                op1=ALU.mult,
-            )
-            nc.vector.tensor_copy(out=weight[:, ZERO_COL, :], in_=positive[:, ZERO_COL, :])
-            z = table.tile([P, PLACES], F32, offset=24576)
-            nc.vector.tensor_reduce(
-                out=z[:], in_=positive[:].rearrange("p o c -> p c o"), axis=AXIS.X, op=ALU.add
-            )
-            nc.vector.tensor_scalar_add(out=z[:], in0=z[:], scalar1=1e-06)
-            one_over_z = table.tile([P, PLACES], F32, bufs=2, offset=24704)
-            nc.vector.reciprocal(out=one_over_z[:], in_=z[:])
-            one_over_z_of[s] = one_over_z
+        def weights(u):
+            positive = positive_of[u]
+            weight = table.tile([P, HALF_COLS, PLACES], F32, bufs=2, offset=9216)
+            weight_of[u] = weight
+            if u % 2 == 0:
+                nc.scalar.copy(out=weight[:], in_=positive[:])
+            else:
+                nc.scalar.activation(out=weight[:, 0:S, :], in_=positive[:, 0:S, :], func=ACT.Copy, scale=-1.0)
+                nc.scalar.copy(out=weight[:, S, :], in_=positive[:, S, :])
+            z = table.tile([P, PLACES], F32, bufs=2, offset=12288)
+            nc.vector.tensor_reduce(out=z[:], in_=positive[:].rearrange("p o c -> p c o"), axis=AXIS.X, op=ALU.add)
+            if u % 2 == 0:
+                z_of[u // 2] = z
+            else:
+                one_over_z = table.tile([P, PLACES], F32, bufs=2, offset=12544)
+                nc.vector.scalar_tensor_tensor(
+                    out=one_over_z[:], in0=z[:], scalar=1e-06, in1=z_of[u // 2][:], op0=ALU.add, op1=ALU.add
+                )
+                nc.vector.reciprocal(out=one_over_z[:], in_=one_over_z[:])
+                one_over_z_of[u // 2] = one_over_z
 
-        def move_weights(s):
-            place = weights_parked[s % 2]
-            nc.sync.dma_start(out=place[0:P, :], in_=weight_of[s][:].rearrange("p o c -> p (o c)"))
-            moved = table.tile([P, COLS + 1, PLACES], F32, bufs=2, offset=24960)
-            for move, first, last, to in moved_weight_runs():
+        def move_weights(u):
+            place = weights_parked[u % 2]
+            nc.sync.dma_start(out=place[0:P, :], in_=weight_of[u][:].rearrange("p o c -> p (o c)"))
+            moved = table.tile([P, HALF_COLS + 1, PLACES], F32, bufs=2, offset=12800)
+            for move, first, last, to in moved_weight_runs(u % 2):
                 nc.sync.dma_start(
                     out=moved[:, to : to + last - first, :].rearrange("p o c -> p (o c)"),
                     in_=place[move : move + P, first * PLACES : last * PLACES],
                 )
-            moved_weight_of[s] = moved
+            moved_weight_of[u] = moved
 
         weighted_of, acc_of, acc_cols_of, fin_of = {}, {}, {}, {}
-        units = [(s, half, i) for s in range(len(STAGES)) for half in range(2) for i in range(COLS)]
+        units = [(u, half, col) for u in range(HALF_STAGES) for half in range(2) for col in MIX_ORDER[u % 2]]
 
         def cells(col, half):
             found = []
@@ -522,9 +514,8 @@ def tile_dwarfattention_pa_t_kernel(
             return found
 
         def weigh(number, by_vector):
-            s, half, i = units[number]
-            col = MIX_ORDER[i]
-            weighted = phase.tile([P, MIX_PLACES + 2, HD], F32, bufs=4, offset=0)
+            u, half, col = units[number]
+            weighted = phase.tile([P, MIX_PLACES + 2, HD], F32, bufs=8, offset=0)
             split = [found[0] for found in cells(col, half) if found[1] == MIX_PLACES]
             for cell in split:
                 nc.vector.memset(weighted[:, 2 * cell + 1, :], 0.0)
@@ -535,11 +526,11 @@ def tile_dwarfattention_pa_t_kernel(
                 for place in range(max(first, half * MIX_PLACES), min(last, (half + 1) * MIX_PLACES)):
                     c = place - half * MIX_PLACES
                     slot = MIX_PLACES + 1 if c % 2 == 1 and c // 2 in split else c
-                    v_read = v_of[STAGES[s]][:, source + place - first, :]
+                    v_read = v_of[STAGES[u // 2]][:, source + place - first, :]
                     if moved_col is None:
-                        scale = weight_of[s][:, col, place : place + 1]
+                        scale = weight_of[u][:, col % HALF_COLS, place : place + 1]
                     else:
-                        scale = moved_weight_of[s][:, moved_col, place : place + 1]
+                        scale = moved_weight_of[u][:, moved_col, place : place + 1]
                     if c >= MIX_PLACES - by_vector:
                         nc.vector.tensor_scalar_mul(out=weighted[:, slot, :], in0=v_read, scalar1=scale)
                     else:
@@ -547,23 +538,26 @@ def tile_dwarfattention_pa_t_kernel(
             weighted_of[number] = weighted
 
         def sum_weighted(number):
-            s, half, i = units[number]
-            if i == 0:
+            u, half, col = units[number]
+            s = u // 2
+            opens = u % 2 == 0 and col == MIX_ORDER[0][0]
+            closes = u % 2 == 1 and col == MIX_ORDER[1][-1]
+            if opens:
                 for bank in range(MIX_CELLS // 4):
                     acc = psum_acc.tile([P, 4, P], F32, tag="acc")
                     acc_of[s, half, bank] = acc
-            for cell, slot, move in cells(MIX_ORDER[i], half):
+            for cell, slot, move in cells(col, half):
                 nc.tensor.matmul(
                     acc_of[s, half, cell // 4][:, cell % 4, :],
                     lhsT=weighted_of[number][:, slot : slot + 2, :].rearrange("p c d -> p (c d)"),
                     rhs=ident_twice[:, P - move : 2 * P - move],
-                    start=(i == 0 and cell % 4 == 0),
-                    stop=(i == COLS - 1 and cell % 4 == 3),
+                    start=(opens and cell % 4 == 0),
+                    stop=(closes and cell % 4 == 3),
                     is_transpose=True,
                 )
 
         def mix_out(s, half):
-            acc_cols = phase.tile([P, MIX_CELLS, P], F32, offset=20480)
+            acc_cols = phase.tile([P, MIX_CELLS, P], F32, offset=36864)
             for bank in range(MIX_CELLS // 4):
                 nc.scalar.copy(out=acc_cols[:, 4 * bank : 4 * bank + 4, :], in_=acc_of[s, half, bank][:])
             acc_cols_of[s, half] = acc_cols
@@ -582,13 +576,14 @@ def tile_dwarfattention_pa_t_kernel(
                 result = qkv.tile([P, PLACES, HD], F32, tag="q")
                 result_of[s] = result
             for bank in range(MIX_CELLS // 4):
-                place = half * MIX_PLACES + 8 * bank
-                nc.vector.tensor_tensor(
-                    out=result_of[s][:, place : place + 8, :],
-                    in0=fin_of[s, half, bank][:].rearrange("p k (c d) -> p (k c) d", d=HD),
-                    in1=one_over_z_of[s][:, place : place + 8].unsqueeze(2).to_broadcast([P, 8, HD]),
-                    op=ALU.mult,
-                )
+                for i in range(8):
+                    place = half * MIX_PLACES + 8 * bank + i
+                    nc.scalar.activation(
+                        out=result_of[s][:, place, :],
+                        in_=fin_of[s, half, bank][:].rearrange("p k (c d) -> p (k c) d", d=HD)[:, i, :],
+                        func=ACT.Copy,
+                        scale=one_over_z_of[s][:, place : place + 1],
+                    )
 
         def store(s, half):
             b, h = STAGES[s]
@@ -598,75 +593,53 @@ def tile_dwarfattention_pa_t_kernel(
                 in_=result_of[s][:, places, :],
             )
 
+        chunks = [(b, j) for b in range(B) for j in range(CHUNKS)]
+
+        def project(i, part):
+            if 0 <= i < len(chunks):
+                if part == 0:
+                    transpose_x(*chunks[i])
+                    if i + 2 < len(chunks):
+                        load_x(*chunks[i + 2])
+                elif part == 1:
+                    quantise_x(*chunks[i])
+                    multiply(*chunks[i])
+                else:
+                    keep(*chunks[i])
+
         with tc.manual_schedule():
-            transpose_x(0, 0)
-            for j in range(CHUNKS):
-                if j + 2 < CHUNKS:
-                    load_x(0, j + 2)
-                if j + 1 < CHUNKS:
-                    transpose_x(0, j + 1)
-                quantise_x(0, j)
-                multiply(0, j)
-                keep(0, j)
-            park_k(0)
-            move_k(0)
-            load_x(1, 0)
-            load_x(1, 1)
+            project(0, 0)
+            for i in range(CHUNKS + HEAD):
+                project(i + 1, 0)
+                project(i, 1)
+                project(i, 2)
+                if i == CHUNKS - 1:
+                    park_k(0)
+                    move_k(0)
             gains_of_slots(0)
 
-            dot_steps = len(STAGES) * STEPS
+            dot_steps = HALF_STAGES * STEPS
             last_unit = len(units) - 1
             first_mix = STEPS + LAG
-            end = first_mix + len(units) // 2 + 5
+            end = first_mix + len(units) // UNITS_A_STEP + 5
             mix_done = {}
             for t in range(end):
-                s, step = divmod(t, STEPS)
-                for other in range(1, len(STAGES)):
-                    if t == K_PARK_STEP[other]:
-                        park_k(other)
+                u, step = divmod(t, STEPS)
+                for s in range(1, len(STAGES)):
+                    if t == K_PARK_STEP[s]:
+                        park_k(s)
                 if t < dot_steps:
                     move_k(t)
-                    products(s, step)
+                    products(u, step)
                 if 1 <= t <= dot_steps:
                     sum_products((t - 1) // STEPS, (t - 1) % STEPS)
-                if t < 3 * CHUNKS:
-                    j, turn = divmod(t, 3)
-                    if turn == 0:
-                        transpose_x(1, j)
-                        if j + 2 < CHUNKS:
-                            load_x(1, j + 2)
-                    elif turn == 1:
-                        quantise_x(1, j)
-                        multiply(1, j)
-                    else:
-                        keep(1, j)
-                done = s - 1
-                if 0 <= done < len(STAGES):
-                    if step == 0:
-                        dots_out(done)
-                    elif step == 1:
-                        dots_back(done)
-                    elif step == 2:
-                        dots_masked(done)
-                        scores(done)
-                    elif step == 4:
-                        shares(done)
-                        if done + 1 < len(STAGES):
-                            gains_of_slots(done + 1)
-                    elif step == 5:
-                        positive_weights(done)
-                    elif step == 6:
-                        weights(done)
-                        move_weights(done)
-                first = 2 * (t - first_mix)
-                for number in (first - 2, first - 1):
-                    if 0 <= number <= last_unit:
-                        sum_weighted(number)
-                for number in (first, first + 1):
-                    if 0 <= number <= last_unit:
-                        weigh(number, 0 if t < dot_steps else 9)
-                        if units[number][2] == COLS - 1:
-                            mix_done[units[number][:2]] = t
+                i, part = divmod(t, 2)
+                if part == 0:
+                    if i > 0:
+                        project(CHUNKS + HEAD + i - 1, 2)
+                    project(CHUNKS + HEAD + i + 1, 0)
+                else:
+                    project(CHUNKS + HEAD + i, 1)
                 for stage_half, when in mix_done.items():
                     if t == when + 2:
                         mix_out(*stage_half)
@@ -674,6 +647,32 @@ def tile_dwarfattention_pa_t_kernel(
                         mix_back(*stage_half)
                     elif t == when + 4:
                         finish(*stage_half)
+                done = u - 1
+                if 0 <= done < HALF_STAGES:
+                    if step == 0:
+                        dots_out(done)
+                    elif step == 1:
+                        dots_back(done)
+                    elif step == 2:
+                        mask_dots(done)
+                        scores(done)
+                    elif step == 3:
+                        shares(done)
+                        if done + 1 < HALF_STAGES:
+                            gains_of_slots(done + 1)
+                        positive_weights(done)
+                    elif step == 4:
+                        weights(done)
+                        move_weights(done)
+                first = UNITS_A_STEP * (t - first_mix)
+                for number in range(first - UNITS_A_STEP, first):
+                    if 0 <= number <= last_unit:
+                        sum_weighted(number)
+                for number in range(first, first + UNITS_A_STEP):
+                    if 0 <= number <= last_unit:
+                        weigh(number, 0 if t < dot_steps else 9)
+                        if units[number][0] % 2 == 1 and units[number][2] == MIX_ORDER[1][-1]:
+                            mix_done[units[number][0] // 2, units[number][1]] = t
                 if t == dot_steps + 4:
                     for done in range(2):
                         for half in range(2):

@@ -24,40 +24,66 @@ PASSES = D // K_PASS
 PLACES = N // P
 CHUNK = 4
 CHUNKS = PLACES // CHUNK
+STAGES = tuple((b, h) for b in range(B) for h in range(H))
 
-OFFSETS = tuple(1 << i for i in range(S + 1)) + tuple(3 << j for j in range(S)) + (0,)
+SPLIT = 6
+NEAR = 2 * SPLIT
+OFFSETS = (
+    tuple(1 << i for i in range(SPLIT))
+    + tuple(3 << j for j in range(SPLIT))
+    + tuple(1 << i for i in range(SPLIT, S + 1))
+    + (0,)
+    + tuple(3 << j for j in range(SPLIT, S))
+)
 COLS = len(OFFSETS)
-ZERO_COL = COLS - 1
-GROUP = S + 1
-TAUS = (1, 2, 3, 0)
-GROUP_COL = (0, 1, GROUP, ZERO_COL)
-HALF_COLS = COLS // 2
-HALF_SLOTS = 2 * GROUP
+ZERO = OFFSETS.index(0)
+CLASS = 64
+IN_CLASS = N // CLASS
+ROWED = tuple(c for c in range(COLS) if OFFSETS[c] % PLACES == 0)
+SHIFTED = tuple(c for c in range(COLS) if OFFSETS[c] % PLACES != 0)
+NEAR_SLOTS = 3 * SPLIT
+SLOTS = 2 * COLS
+NEAR_TAPS = ((1, 0, SPLIT, 0), (3, 0, SPLIT, SPLIT), (2, 0, SPLIT - 1, NEAR + 1))
+FAR_TAPS = (
+    (1, SPLIT, S, NEAR_SLOTS),
+    (3, SPLIT, S, NEAR_SLOTS + ZERO - NEAR + 1),
+    (2, SPLIT - 1, S, NEAR_SLOTS + COLS - NEAR),
+    (0, 0, S, SLOTS - S - 1),
+)
+LOCAL = SLOTS - 1
+FAR_ZERO = NEAR_SLOTS + ZERO - NEAR
+
+
+def slot_of(col):
+    return col if col < NEAR else NEAR_SLOTS + col - NEAR
+
 
 QUAD = P // PLACES
-QUADS = COLS // QUAD
-GROUP_QUADS = QUADS // 2
+QUADS = NEAR // QUAD
 STEP_D = 8
-QUARTER_D = HD // 4
-PIECES = QUARTER_D // STEP_D
-STEPS = 4 * PIECES
-K_BUFFERS = 16
-UNITS_A_STEP = 2 * HALF_COLS // STEPS
-MIX_PLACES = PLACES // 2
-MIX_CELLS = MIX_PLACES // 2
-PAD = 32
-ROW = HD * PLACES
-K_PLACE = (PAD, 2 * PAD + P, PAD, 2 * PAD + P)
-K_PARK_STEP = (0, 2, 2 * STEPS + 2, 4 * STEPS + 2)
-WEIGHT_ROW = HALF_COLS * PLACES
-MOST = max(OFFSETS) // PLACES
-WEIGHT_PLACE = tuple((2 * (PAD + P)) * ROW + i * (P + MOST) * WEIGHT_ROW for i in range(2))
-MASKED_COLS = tuple(col for col in range(COLS) if OFFSETS[col] > PAD * PLACES)
-EXTRA_COL = HALF_COLS
-HEAD = 2
-LAG = 6
-STAGES = tuple((b, h) for b in range(B) for h in range(H))
-HALF_STAGES = 2 * len(STAGES)
+STEPS = HD // STEP_D
+WINDOW = 4 * PLACES
+BACK = WINDOW - PLACES
+K_BUFFERS = 4
+K_AHEAD = 3
+HALF = PLACES // 2
+CELLS = HALF // 2
+
+S_ROW = 2 * IN_CLASS * HALF
+S_AT = 0
+W_ROW = P * HALF
+W_AT = max(OFFSETS) // PLACES * W_ROW
+K_AT = W_AT + P * W_ROW
+PARK_AT = K_AT + H * HD * N
+PARK_ROW = len(SHIFTED) * PLACES
+PARK_PAD = 2
+SHIFTED_RUN = SPLIT - 1
+EXTRA = len(SHIFTED)
+
+FAR_RUNS = ((NEAR, 2), (NEAR + 2, 2), (NEAR + 4, 2), (ZERO, 1), (ZERO + 1, 2), (ZERO + 3, 2), (ZERO + 5, 1))
+
+LAG = 2
+UNITS_A_STAGE = 2 * len(SHIFTED)
 
 FLOPS = 2 * B * N * D * 3 * H * HD + B * H * N * (4 * S + 1) * 4 * HD
 
@@ -69,34 +95,8 @@ def parts(o):
     return ((rest, PLACES, move, 0), (0, rest, move + 1, PLACES - rest))
 
 
-def moves_of(col):
-    return tuple(part[2] for part in parts(OFFSETS[col]) if part[2] > 0)
-
-
-MIX_ORDER = (tuple(range(2, HALF_COLS)) + (0, 1), (ZERO_COL,) + tuple(range(HALF_COLS, ZERO_COL)))
-
-
-def moved_weight_col(col, part):
-    first, last, move, source = part
-    if move == 0:
-        return None
-    return EXTRA_COL if first == 0 and len(parts(OFFSETS[col])) == 2 and parts(OFFSETS[col])[0][2] > 0 else col % HALF_COLS
-
-
-def moved_weight_runs(group):
-    wanted = []
-    for col in range(group * HALF_COLS, (group + 1) * HALF_COLS):
-        for part in parts(OFFSETS[col]):
-            to = moved_weight_col(col, part)
-            if to is not None:
-                wanted.append((part[2], col % HALF_COLS, to))
-    runs = []
-    for move, col, to in wanted:
-        if runs and runs[-1][0] == move and runs[-1][2] == col and runs[-1][3] + col - runs[-1][1] == to:
-            runs[-1] = (move, runs[-1][1], col + 1, runs[-1][3])
-        else:
-            runs.append((move, col, col + 1, to))
-    return runs
+MIX_ORDER = (1, 0) + SHIFTED[2:]
+HALVES = (1, 0)
 
 
 def tile_dwarfattention_pa_t_kernel(
@@ -105,25 +105,33 @@ def tile_dwarfattention_pa_t_kernel(
     nc = tc.nc
     with ExitStack() as ctx:
         const = ctx.enter_context(tc.tile_pool(name="const", bufs=1))
-        qkv = ctx.enter_context(tc.tile_pool(name="qkv", bufs=4))
-        prods = ctx.enter_context(tc.tile_pool(name="prods", bufs=3))
+        qkv = ctx.enter_context(tc.tile_pool(name="qkv", bufs=2))
+        prods = ctx.enter_context(tc.tile_pool(name="prods", bufs=2))
+        windows = ctx.enter_context(tc.tile_pool(name="windows", bufs=K_BUFFERS))
         table = ctx.enter_context(tc.tile_pool(name="table", bufs=1))
         phase = ctx.enter_context(tc.tile_pool(name="phase", bufs=1))
-        psum_x = ctx.enter_context(tc.psum_pool(name="psum_x", bufs=2))
-        psum_dots = ctx.enter_context(tc.psum_pool(name="psum_dots", bufs=2))
+        psum_x = ctx.enter_context(tc.psum_pool(name="psum_x", bufs=3))
+        psum_dots = ctx.enter_context(tc.psum_pool(name="psum_dots", bufs=1))
         psum_acc = ctx.enter_context(tc.psum_pool(name="psum_acc", bufs=4))
+
+        flat = out.rearrange("b n f -> (b n f)")
+
+        def rows_of(at, count, width):
+            return flat[at : at + count * width].rearrange("(r w) -> r w", w=width)
 
         x_rows_of, grouped_of, codes_of, qkv_ps_of = {}, {}, {}, {}
 
-        def load_x(b, j):
+        def load_x(i):
+            b, j = chunks[i]
             x_rows = phase.tile([P, CHUNK, D], BF16, bufs=2, offset=0, align_bytes=64)
             nc.sync.dma_start(
                 out=x_rows[:], in_=x[b].rearrange("(p c) d -> p c d", c=PLACES)[:, j * CHUNK : (j + 1) * CHUNK, :]
             )
-            x_rows_of[b, j] = x_rows
+            x_rows_of[i] = x_rows
 
-        load_x(0, 0)
-        load_x(0, 1)
+        chunks = [(b, j) for b in range(B) for j in range(CHUNKS)]
+        load_x(0)
+        load_x(1)
 
         ident_twice = const.tile([P, 2 * P], F32)
         make_identity(nc, ident_twice[:, 0:P])
@@ -143,19 +151,19 @@ def tile_dwarfattention_pa_t_kernel(
                 out=w_scales[32 * quadrant : 32 * quadrant + 4, :, :].bitcast(I32),
                 in_=W_qkv_scales[:, 4 * quadrant : 4 * quadrant + 4, :].rearrange("g r n -> r g n").bitcast(I32),
             )
-        bias_bf16 = const.tile([P, 3 * P], BF16)
+        bias_bf16 = phase.tile([P, 3 * P], BF16, offset=63488)
         nc.sync.dma_start(out=bias_bf16[:], in_=b_qkv.partition_broadcast(P))
-        bias = const.tile([P, 3, H, HD], F32)
-        nc.vector.tensor_copy(out=bias[:].rearrange("p r h d -> p (r h d)"), in_=bias_bf16[:])
+        bias = const.tile([P, 3, P], F32)
+        nc.vector.tensor_copy(out=bias[:].rearrange("p r f -> p (r f)"), in_=bias_bf16[:])
 
-        pos_bias_all = const.tile([P, 4 * S * H], BF16)
+        pos_bias_all = phase.tile([P, 4 * S * H], BF16, offset=64512)
         nc.sync.dma_start(out=pos_bias_all[:], in_=pos_bias.rearrange("r h -> (r h)").partition_broadcast(P))
-        bias_plus_1 = const.tile([P, len(TAUS) * GROUP, H], F32)
+        bias_plus_1 = const.tile([P, SLOTS, H], F32)
         nc.vector.memset(bias_plus_1[:], 1.0)
-        for group, tau in enumerate(TAUS):
+        for tau, first, last, at in NEAR_TAPS + FAR_TAPS:
             nc.vector.tensor_scalar_add(
-                out=bias_plus_1[:, group * GROUP : group * GROUP + S, :],
-                in0=pos_bias_all[:].rearrange("p (j t h) -> p t j h", t=4, h=H)[:, tau],
+                out=bias_plus_1[:, at : at + last - first, :],
+                in0=pos_bias_all[:].rearrange("p (j t h) -> p t j h", t=4, h=H)[:, tau, first:last],
                 scalar1=1.0,
             )
 
@@ -175,63 +183,47 @@ def tile_dwarfattention_pa_t_kernel(
         gains_in = const.tile([P, B, H, PLACES, S], BF16)
         for b, h in STAGES:
             nc.sync.dma_start(out=gains_in[:, b, h, :, :], in_=gains[b, h].rearrange("(p c) j -> p c j", c=PLACES))
-        slot_gain = const.tile([P, HALF_SLOTS, PLACES], F32)
+        slot_gain = const.tile([P, SLOTS, PLACES], F32)
         nc.gpsimd.memset(slot_gain[:], 0.0)
+        u1 = const.tile([P, SLOTS - NEAR_SLOTS, PLACES], F32)
+        nc.gpsimd.memset(u1[:], 0.0)
 
         token = const.tile([P, PLACES], F32)
         nc.gpsimd.iota(
             token[:], pattern=[[1, PLACES]], base=0, channel_multiplier=PLACES, allow_small_or_imprecise_dtypes=True
         )
-        reached = const.tile([P, len(MASKED_COLS), PLACES], F32)
-        for i, col in enumerate(MASKED_COLS):
-            nc.vector.tensor_single_scalar(out=reached[:, i, :], in_=token[:], scalar=float(OFFSETS[col]), op=ALU.is_ge)
+        reached = const.tile([P, COLS, PLACES], BF16)
+        for col in range(COLS):
+            nc.vector.tensor_single_scalar(out=reached[:, col, :], in_=token[:], scalar=float(OFFSETS[col]), op=ALU.is_ge)
 
-        k_moved = []
-        for i in range(K_BUFFERS):
-            moved = const.tile([P, QUARTER_D, PLACES], F32, name="k_moved_%d" % i)
-            nc.gpsimd.memset(moved[:], 0.0)
-            k_moved.append(moved)
+        q_split = const.tile([P, CHUNK, 2 * P], F32)
+        nc.gpsimd.memset(q_split[:], 0.0)
 
-        parked = out.rearrange("b (r t) f -> (b r) (t f)", t=16)
-        flat = out.rearrange("b n f -> (b n f)")
-        weights_parked = [
-            flat[at : at + (P + MOST) * WEIGHT_ROW].rearrange("(r w) -> r w", w=WEIGHT_ROW) for at in WEIGHT_PLACE
-        ]
-        for place in weights_parked:
-            for part in range(0, WEIGHT_ROW, QUARTER_D * PLACES):
-                width = min(QUARTER_D * PLACES, WEIGHT_ROW - part)
-                nc.sync.dma_start(
-                    out=place[P : P + MOST, part : part + width],
-                    in_=k_moved[0][0:MOST].rearrange("p d c -> p (d c)")[:, 0:width],
-                )
-        for place in K_PLACE[0:2]:
-            for part in range(0, ROW, QUARTER_D * PLACES):
-                nc.sync.dma_start(
-                    out=parked[place - PAD : place, part : part + QUARTER_D * PLACES],
-                    in_=k_moved[0][0:PAD].rearrange("p d c -> p (d c)"),
-                )
+        bias_col = const.tile([P, 2], F32)
+        bias_t = psum_x.tile([P, 2, P], F32, tag="xt")
+        for part in range(2):
+            nc.tensor.transpose(bias_t[:, part, :], bias[:, part, :], ident)
+        nc.scalar.copy(out=bias_col[:], in_=bias_t[:, :, 0])
 
-        def load_moved(dst, place, move, columns):
-            first = 0 if move <= PAD else move
-            while first < P:
-                rows = P - first
-                while rows & (rows - 1):
-                    rows = rows & (rows - 1)
-                nc.sync.dma_start(
-                    out=dst[first : first + rows], in_=parked[place + first - move : place + first - move + rows, columns]
-                )
-                first += rows
+        def zeros_tile():
+            zeros = phase.tile([P, W_ROW // 4], F32, offset=45056)
+            nc.gpsimd.memset(zeros[:], 0.0)
+            return zeros
 
-        q_of, k_of, v_of = {}, {}, {}
+        zeros = zeros_tile()
+        nc.sync.dma_start(out=rows_of(K_AT - 512, 1, 512), in_=zeros[0:1, :])
+        nc.sync.dma_start(out=rows_of(PARK_AT + P * PARK_ROW, PARK_PAD, PARK_ROW), in_=zeros[0:PARK_PAD, 0:PARK_ROW])
 
-        def transpose_x(b, j):
+        q_of, v_of, v_tile_of, k_t_of, k_chunk_of, s_ps_of, s_of = {}, {}, {}, {}, {}, {}, {}
+
+        def transpose_x(i):
             grouped = phase.tile([P, PASSES, CHUNK * P * PACK], BF16, bufs=2, offset=16384, align_bytes=64)
             for g in range(PASSES):
                 grouped_words = grouped[:, g, :].bitcast(F32).rearrange("p (n u) -> p n u", u=2)
                 for half in range(2):
                     xt = psum_x.tile([P, 2, 2 * P], F32, tag="xt")
                     for c in range(2):
-                        words = x_rows_of[b, j][:, 2 * half + c, :].bitcast(F32)
+                        words = x_rows_of[i][:, 2 * half + c, :].bitcast(F32)
                         for u in range(2):
                             nc.tensor.transpose(
                                 xt[:, u, c * P : (c + 1) * P],
@@ -242,20 +234,33 @@ def tile_dwarfattention_pa_t_kernel(
                         out=grouped_words[:, half * 2 * P : (half + 1) * 2 * P, :],
                         in_=xt[:].rearrange("p u n -> p n u"),
                     )
-            grouped_of[b, j] = grouped
+            grouped_of[i] = grouped
 
-        def quantise_x(b, j):
+        def quantise_x(i):
             x_codes = phase.tile([P, PASSES, CHUNK * P], U32, bufs=2, offset=32768, align_bytes=64)
             x_scales = phase.tile([P, PASSES, CHUNK * P], U8, bufs=2, offset=40960, align_bytes=64)
             for g in range(PASSES):
                 nc.vector.quantize_mx(
-                    out=x_codes[:, g, :].bitcast(FP8X4), scales=x_scales[:, g, :], in_=grouped_of[b, j][:, g, :]
+                    out=x_codes[:, g, :].bitcast(FP8X4), scales=x_scales[:, g, :], in_=grouped_of[i][:, g, :]
                 )
-            codes_of[b, j] = x_codes, x_scales
+            codes_of[i] = x_codes, x_scales
 
-        def multiply(b, j):
-            x_codes, x_scales = codes_of[b, j]
-            for part in range(3):
+        def multiply(i):
+            x_codes, x_scales = codes_of[i]
+            for part in (0, 1):
+                qkv_ps = psum_acc.tile([P, CHUNK, P], F32, tag="acc")
+                for g in range(PASSES):
+                    nc.tensor.matmul_mx(
+                        out=qkv_ps[:].rearrange("p c n -> p (c n)"),
+                        lhsT=w_words[:, g, part * 2 * P : (part + 1) * 2 * P].bitcast(FP4X4),
+                        lhsT_scale=w_scales[:, g, part * P : (part + 1) * P],
+                        rhs=x_codes[:, g, :].bitcast(FP8X4),
+                        rhs_scale=x_scales[:, g, :],
+                        start=(g == 0),
+                        stop=(g == PASSES - 1),
+                    )
+                qkv_ps_of[i, part, "columns"] = qkv_ps
+            for part in (0, 2):
                 qkv_ps = psum_acc.tile([P, CHUNK, P], F32, tag="acc")
                 for c in range(CHUNK):
                     tokens = slice(c * P, (c + 1) * P)
@@ -269,281 +274,351 @@ def tile_dwarfattention_pa_t_kernel(
                             start=(g == 0),
                             stop=(g == PASSES - 1),
                         )
-                qkv_ps_of[b, j, part] = qkv_ps
+                qkv_ps_of[i, part, "rows"] = qkv_ps
 
-        def keep(b, j):
+        def keep_rows(i):
+            b, j = chunks[i]
             if j == 0:
                 for h in range(H):
-                    q = qkv.tile([P, HD, PLACES], F32, tag="q")
-                    k = qkv.tile([P, HD, PLACES], F32)
-                    v = qkv.tile([P, PLACES, HD], F32)
-                    q_of[b, h], k_of[b, h], v_of[b, h] = q, k, v
+                    q = qkv.tile([P, HD, PLACES], F32, tag="q", bufs=4)
+                    q_of[b, h] = q
+                v = qkv.tile([P, H, PLACES, HD], F32)
+                v_of[b] = v
             places = slice(j * CHUNK, (j + 1) * CHUNK)
-            for part, kept in enumerate((q_of, k_of, v_of)):
-                for h in range(H):
-                    in_ps = qkv_ps_of[b, j, part][:, :, h * HD : (h + 1) * HD]
-                    if part < 2:
-                        nc.vector.tensor_tensor(
-                            out=kept[b, h][:, :, places],
-                            in0=in_ps.rearrange("p c d -> p d c"),
-                            in1=bias[:, part, h, :].unsqueeze(2).to_broadcast([P, HD, CHUNK]),
-                            op=ALU.add,
-                        )
-                    else:
-                        nc.vector.tensor_tensor(
-                            out=kept[b, h][:, places, :],
-                            in0=in_ps,
-                            in1=bias[:, part, h, :].unsqueeze(1).to_broadcast([P, CHUNK, HD]),
-                            op=ALU.add,
-                        )
+            for h in range(H):
+                features = slice(h * HD, (h + 1) * HD)
+                nc.vector.tensor_tensor(
+                    out=q_of[b, h][:, :, places],
+                    in0=qkv_ps_of[i, 0, "rows"][:, :, features].rearrange("p c d -> p d c"),
+                    in1=bias[:, 0, features].unsqueeze(2).to_broadcast([P, HD, CHUNK]),
+                    op=ALU.add,
+                )
+            for h in range(H):
+                features = slice(h * HD, (h + 1) * HD)
+                nc.vector.tensor_tensor(
+                    out=v_of[b][:, h, places, :],
+                    in0=qkv_ps_of[i, 2, "rows"][:, :, features],
+                    in1=bias[:, 2, features].unsqueeze(1).to_broadcast([P, CHUNK, HD]),
+                    op=ALU.add,
+                )
 
-        prod_of, dots_ps_of, k_buf_of = {}, {}, {}
+        def keep_columns(i, by_vector):
+            b, j = chunks[i]
+            q_ps, k_ps = qkv_ps_of[i, 0, "columns"], qkv_ps_of[i, 1, "columns"]
+            for h in range(H):
+                mine = slice(h * HD, (h + 1) * HD)
+                nc.scalar.activation(
+                    out=q_split[mine, :, h * P : (h + 1) * P],
+                    in_=q_ps[mine, :, :],
+                    func=ACT.Identity,
+                    bias=bias_col[mine, 0:1],
+                )
+            k_chunk = phase.tile([P, CHUNK, P], F32, bufs=2, offset=43008)
+            nc.scalar.activation(out=k_chunk[:], in_=k_ps[:, :, ::-1], func=ACT.Identity, bias=bias_col[:, 1:2])
+            k_chunk_of[i] = k_chunk
+            if j == 0:
+                k_t = phase.tile([P, P, PLACES], F32, offset=47104)
+                k_t_of[b] = k_t
+            k_out = k_t_of[b][:, :, j * CHUNK : (j + 1) * CHUNK]
+            k_in = k_ps[:].rearrange("p c n -> p n c")
+            if by_vector:
+                nc.vector.tensor_scalar_add(out=k_out, in0=k_in, scalar1=bias_col[:, 1:2])
+            else:
+                nc.scalar.activation(out=k_out, in_=k_in, func=ACT.Identity, bias=bias_col[:, 1:2])
 
-        def columns_of(u):
-            return range(u % 2 * HALF_COLS, (u % 2 + 1) * HALF_COLS)
-
-        def k_item_steps():
-            items, last_use = [], {}
-            for u in range(HALF_STAGES):
-                for step in range(STEPS):
-                    for col in columns_of(u):
-                        for move in moves_of(col):
-                            item = (u, step // PIECES, move)
-                            if item not in last_use:
-                                items.append(item)
-                            last_use[item] = u * STEPS + step
-            return items, last_use
-
-        k_items, k_last_use = k_item_steps()
-        k_free, k_busy, k_parked = list(k_moved), {}, []
-
-        def park_k(s):
-            nc.sync.dma_start(
-                out=parked[K_PLACE[s] : K_PLACE[s] + P, :], in_=k_of[STAGES[s]][:].rearrange("p d c -> p (d c)")
-            )
-            k_parked.append(s)
-
-        def move_k(t):
-            for item in list(k_busy):
-                if k_last_use[item] < t:
-                    k_free.append(k_busy.pop(item))
-            while k_free and k_items:
-                item = k_items.pop(0)
-                if item[0] // 2 not in k_parked:
-                    k_items.insert(0, item)
-                    return
-                moved = k_free.pop(0)
-                u, quarter, move = item
-                d_columns = slice(quarter * QUARTER_D * PLACES, (quarter + 1) * QUARTER_D * PLACES)
-                load_moved(moved[:].rearrange("p d c -> p (d c)"), K_PLACE[u // 2], move, d_columns)
-                k_busy[item] = moved
-                k_buf_of[item] = moved
-
-        def products(u, step):
-            quarter, piece = divmod(step, PIECES)
-            stage = STAGES[u // 2]
-            d0 = step * STEP_D
-            prod = prods.tile([P, STEP_D, GROUP_QUADS, QUAD, PLACES], F32)
-            for i, col in enumerate(columns_of(u)):
-                for first, last, move, source in parts(OFFSETS[col]):
-                    if move == 0:
-                        k_read = k_of[stage][:, d0 : d0 + STEP_D, :]
-                    else:
-                        k_read = k_buf_of[u, quarter, move][:, piece * STEP_D : (piece + 1) * STEP_D, :]
-                    nc.vector.tensor_tensor(
-                        out=prod[:, :, i // QUAD, i % QUAD, first:last],
-                        in0=q_of[stage][:, d0 : d0 + STEP_D, first:last],
-                        in1=k_read[:, :, source : source + last - first],
-                        op=ALU.mult,
-                    )
-            prod_of[u, step] = prod
-
-        def sum_products(u, step):
-            if step == 0:
-                dots_ps = psum_dots.tile([P, GROUP_QUADS, P], F32)
-                dots_ps_of[u] = dots_ps
-            for d in range(STEP_D):
-                for quad in range(GROUP_QUADS):
+        def far_dots(i):
+            s_ps = psum_x.tile([P, CHUNK, 2, IN_CLASS], F32, tag="xt")
+            for c in range(CHUNK):
+                for odd in range(2):
                     nc.tensor.matmul(
-                        dots_ps_of[u][:, quad, :],
-                        lhsT=prod_of[u, step][:, d, quad, :, :].rearrange("p i c -> p (i c)"),
+                        out=s_ps[:, c, odd, :],
+                        lhsT=q_split[:, c, odd : 2 * P : 2],
+                        rhs=k_chunk_of[i][:, c, 1 - odd : P : 2],
+                        start=True,
+                        stop=True,
+                    )
+            s_ps_of[i] = s_ps
+
+        def far_dots_out(i, by_vector):
+            b, j = chunks[i]
+            group, place = divmod(j * CHUNK, HALF)
+            if place == 0:
+                s_rows = phase.tile([P, 2, IN_CLASS, HALF], F32, bufs=2, offset=63488)
+                s_of[b, group] = s_rows
+            out_view = s_of[b, group][:, :, :, place : place + CHUNK]
+            in_view = s_ps_of[i][:].rearrange("p c s k -> p s k c")
+            if by_vector:
+                nc.vector.tensor_copy(out=out_view, in_=in_view)
+            else:
+                nc.scalar.copy(out=out_view, in_=in_view)
+
+        dots_of = {}
+
+        def far_dots_back(b, group):
+            if group == 0:
+                for h in range(H):
+                    dots = table.tile([P, COLS, PLACES], F32, bufs=4)
+                    dots_of[2 * b + h] = dots
+            nc.sync.dma_start(out=rows_of(S_AT, P, S_ROW), in_=s_of[b, group][:].rearrange("p s k c -> p (s k c)"))
+            for odd in range(2):
+                for h in range(H):
+                    at = S_AT + h * IN_CLASS * S_ROW + odd * S_ROW // 2 + (IN_CLASS - 1) * HALF
+                    rows = rows_of(at, IN_CLASS, S_ROW - HALF)
+                    for col, count in FAR_RUNS:
+                        start = OFFSETS[col] // CLASS * HALF
+                        step = HALF if count == 1 else start
+                        nc.sync.dma_start(
+                            out=dots_of[2 * b + h][odd:P:2, col : col + count, group * HALF : (group + 1) * HALF],
+                            in_=rows[:, start : start + count * step].rearrange("r (g k) -> r g k", k=step)[:, :, 0:HALF],
+                        )
+
+        prod_of, dots_ps_of, window_of = {}, {}, {}
+
+        def park_k(b, h):
+            nc.sync.dma_start(
+                out=rows_of(K_AT + h * HD * N, HD, N),
+                in_=k_t_of[b][h * HD : (h + 1) * HD].rearrange("p a c -> p (a c)"),
+            )
+
+        def load_window(t):
+            s, step = divmod(t, STEPS)
+            window = windows.tile([P, STEP_D, WINDOW], F32)
+            at = K_AT + (s % H * HD + step * STEP_D) * N - BACK
+            for r in range(WINDOW // PLACES):
+                nc.sync.dma_start(
+                    out=window[r : P : WINDOW // PLACES],
+                    in_=flat[at + r * PLACES : at + r * PLACES + STEP_D * N].rearrange(
+                        "(d a t) -> a d t", d=STEP_D, t=WINDOW
+                    ),
+                )
+            window_of[t] = window
+
+        def products(t, columns):
+            s, step = divmod(t, STEPS)
+            d0 = step * STEP_D
+            if columns[0] == 0:
+                prod = prods.tile([P, STEP_D, QUADS, QUAD, PLACES], F32)
+                prod_of[t] = prod
+            for i in columns:
+                first = BACK - OFFSETS[i]
+                nc.vector.tensor_tensor(
+                    out=prod_of[t][:, :, i // QUAD, i % QUAD, :],
+                    in0=q_of[STAGES[s]][:, d0 : d0 + STEP_D, :],
+                    in1=window_of[t][:, :, first : first + PLACES],
+                    op=ALU.mult,
+                )
+
+        def sum_products(t):
+            s, step = divmod(t, STEPS)
+            if step == 0:
+                dots_ps = psum_dots.tile([P, QUADS, P], F32)
+                dots_ps_of[s] = dots_ps
+            for d in range(STEP_D):
+                for quad in range(QUADS):
+                    nc.tensor.matmul(
+                        dots_ps_of[s][:, quad, :],
+                        lhsT=prod_of[t][:, d, quad, :, :].rearrange("p i c -> p (i c)"),
                         rhs=ident,
                         start=(step == 0 and d == 0 and quad == 0),
-                        stop=(step == STEPS - 1 and d == STEP_D - 1 and quad == GROUP_QUADS - 1),
+                        stop=(step == STEPS - 1 and d == STEP_D - 1 and quad == QUADS - 1),
                         is_transpose=True,
                     )
 
-        turned_of, dots_of, u1_of, exp_u_of, positive_of = {}, {}, {}, {}, {}
-        weight_of, moved_weight_of = {}, {}
-        z_of, one_over_z_of = {}, {}
+        turned_of, weight_of, moved_weight_of, z_of, one_over_z_of = {}, {}, {}, {}, {}
 
-        def dots_out(u):
-            turned = table.tile([P, GROUP_QUADS, P], F32, offset=0)
-            nc.scalar.copy(out=turned[:], in_=dots_ps_of[u][:])
-            turned_of[u] = turned
+        def dots_out(s):
+            turned = table.tile([P, QUADS, P], F32)
+            nc.scalar.copy(out=turned[:], in_=dots_ps_of[s][:])
+            turned_of[s] = turned
 
-        def dots_back(u):
-            back = psum_x.tile([P, GROUP_QUADS, P], F32, tag="xt")
-            for quad in range(GROUP_QUADS):
-                nc.tensor.transpose(back[:, quad, :], turned_of[u][:, quad, :], ident)
-            dots = table.tile([P, HALF_COLS, PLACES], F32, offset=6144)
-            nc.scalar.copy(out=dots[:], in_=back[:].rearrange("p q (i c) -> p (q i) c", i=QUAD))
-            dots_of[u] = dots
+        def dots_back(s):
+            back = psum_x.tile([P, QUADS, P], F32, tag="xt")
+            for quad in range(QUADS):
+                nc.tensor.transpose(back[:, quad, :], turned_of[s][:, quad, :], ident)
+            nc.scalar.copy(
+                out=dots_of[s][:, 0:NEAR, :], in_=back[:].rearrange("p q (i c) -> p (q i) c", c=PLACES)
+            )
 
-        def mask_dots(u):
-            for i, col in enumerate(MASKED_COLS):
-                if col in columns_of(u):
-                    dot = dots_of[u][:, col % HALF_COLS, :]
-                    nc.vector.tensor_tensor(out=dot, in0=dot, in1=reached[:, i, :], op=ALU.mult)
-
-        def scores(u):
-            h = STAGES[u // 2][1]
-            u1 = table.tile([P, HALF_SLOTS, PLACES], F32, offset=3072)
-            for i in range(2):
-                group = u % 2 * 2 + i
-                col = GROUP_COL[group] % HALF_COLS
-                slots = min(GROUP, HALF_COLS - col) if TAUS[group] > 0 else GROUP
-                if TAUS[group] > 0:
-                    dots_read = dots_of[u][:, col : col + slots, :]
-                else:
-                    dots_read = dots_of[u][:, col : col + 1, :].to_broadcast([P, slots, PLACES])
-                at = group * GROUP
+        def scores(s, near):
+            h = STAGES[s][1]
+            dots = dots_of[s]
+            cols = slice(0, NEAR) if near else slice(NEAR, COLS)
+            nc.vector.tensor_tensor(out=dots[:, cols, :], in0=dots[:, cols, :], in1=reached[:, cols, :], op=ALU.mult)
+            if near:
+                reads = ((0, NEAR, dots[:, cols, :]), (NEAR + 1, SPLIT - 1, dots[:, 1:SPLIT, :]))
+                slots = slice(0, NEAR_SLOTS)
+            else:
+                at = NEAR_SLOTS + COLS - NEAR
+                reads = (
+                    (NEAR_SLOTS, COLS - NEAR, dots[:, cols, :]),
+                    (at, SPLIT, dots[:, NEAR : NEAR + SPLIT, :]),
+                    (at + SPLIT, S + 1, dots[:, ZERO : ZERO + 1, :].to_broadcast([P, S + 1, PLACES])),
+                )
+                slots = slice(NEAR_SLOTS, SLOTS)
+                weight = table.tile([P, SLOTS, PLACES], F32, bufs=2)
+                weight_of[s] = weight
+                z = table.tile([P, 4, PLACES], F32, bufs=2)
+                z_of[s] = z
+            for at, count, dots_read in reads:
                 nc.vector.tensor_tensor(
-                    out=u1[:, i * GROUP : i * GROUP + slots, :],
+                    out=u1[:, at - slots.start : at - slots.start + count, :],
                     in0=dots_read,
-                    in1=bias_plus_1[:, at : at + slots, h : h + 1].to_broadcast([P, slots, PLACES]),
+                    in1=bias_plus_1[:, at : at + count, h : h + 1].to_broadcast([P, count, PLACES]),
                     op=ALU.add,
                 )
-            used = GROUP + slots
-            exp_u = table.tile([P, HALF_SLOTS, PLACES], F32, offset=0)
-            nc.scalar.activation(out=exp_u[:, 0:used, :], in_=u1[:, 0:used, :], func=ACT.Exp, bias=minus_one_col[:, 0:1])
-            u1_of[u], exp_u_of[u] = u1, exp_u
+            nc.scalar.activation(
+                out=weight_of[s][:, slots, :],
+                in_=u1[:, 0 : slots.stop - slots.start, :],
+                func=ACT.Exp,
+                bias=minus_one_col[:, 0:1],
+            )
 
-        def gains_of_slots(u):
-            b, h = STAGES[u // 2]
-            for i in range(2):
-                tau = TAUS[u % 2 * 2 + i]
+        def gains_of_slots(s, near):
+            b, h = STAGES[s]
+            for tau, first, last, at in NEAR_TAPS if near else FAR_TAPS:
                 nc.gpsimd.tensor_scalar(
-                    out=slot_gain[:, i * GROUP : i * GROUP + S, :],
-                    in0=gains_in[:, b, h, :, :].rearrange("p c j -> p j c"),
-                    scalar1=abs(D4[tau]),
+                    out=slot_gain[:, at : at + last - first, :],
+                    in0=gains_in[:, b, h, :, first:last].rearrange("p c j -> p j c"),
+                    scalar1=D4[tau],
                     scalar2=0.0,
                     op0=ALU.mult,
                     op1=ALU.add,
                 )
-                if tau == 0:
-                    nc.gpsimd.tensor_copy(
-                        out=slot_gain[:, HALF_SLOTS - 1, :], in_=local_gain[:, h : h + 1].to_broadcast([P, PLACES])
-                    )
+            if not near:
+                nc.gpsimd.tensor_copy(out=slot_gain[:, LOCAL, :], in_=local_gain[:, h : h + 1].to_broadcast([P, PLACES]))
 
-        def shares(u):
-            used = HALF_SLOTS - 1 if u % 2 == 0 else HALF_SLOTS
-            u1, exp_u = u1_of[u][:, 0:used, :], exp_u_of[u][:, 0:used, :]
+        def shares(s, near):
+            slots = slice(0, NEAR_SLOTS) if near else slice(NEAR_SLOTS, SLOTS)
+            share, u1_read = weight_of[s][:, slots, :], u1[:, 0 : slots.stop - slots.start, :]
             nc.vector.scalar_tensor_tensor(
-                out=exp_u.rearrange("p s c -> p (s c)"),
-                in0=exp_u.rearrange("p s c -> p (s c)"),
+                out=share.rearrange("p s c -> p (s c)"),
+                in0=share.rearrange("p s c -> p (s c)"),
                 scalar=1.0,
-                in1=u1.rearrange("p s c -> p (s c)"),
+                in1=u1_read.rearrange("p s c -> p (s c)"),
                 op0=ALU.min,
                 op1=ALU.max,
             )
-            nc.vector.tensor_tensor(out=exp_u, in0=exp_u, in1=slot_gain[:, 0:used, :], op=ALU.mult)
+            nc.vector.tensor_tensor(out=share, in0=share, in1=slot_gain[:, slots, :], op=ALU.mult)
 
-        def positive_weights(u):
-            share = exp_u_of[u]
-            positive = table.tile([P, HALF_COLS, PLACES], F32, offset=7680)
-            if u % 2 == 0:
-                nc.vector.tensor_tensor(
-                    out=positive[:], in0=share[:, 0:GROUP, :], in1=share[:, GROUP - 1 : 2 * GROUP - 1, :], op=ALU.add
-                )
-            else:
-                nc.vector.tensor_copy(out=positive[:, 0:S, :], in_=share[:, 0:S, :])
+        def weights(s, near):
+            weight = weight_of[s]
+            at, more = (0, NEAR) if near else (NEAR_SLOTS, NEAR_SLOTS + COLS - NEAR)
+            nc.vector.tensor_tensor(
+                out=weight[:, at : at + SPLIT, :],
+                in0=weight[:, at : at + SPLIT, :],
+                in1=weight[:, more : more + SPLIT, :],
+                op=ALU.add,
+            )
+            if not near:
                 nc.vector.tensor_reduce(
-                    out=positive[:, S, :],
-                    in_=share[:, GROUP:, :].rearrange("p s c -> p c s"),
+                    out=weight[:, FAR_ZERO, :],
+                    in_=weight[:, more + SPLIT : SLOTS, :].rearrange("p s c -> p c s"),
                     axis=AXIS.X,
                     op=ALU.add,
                 )
-            positive_of[u] = positive
 
-        def weights(u):
-            positive = positive_of[u]
-            weight = table.tile([P, HALF_COLS, PLACES], F32, bufs=2, offset=9216)
-            weight_of[u] = weight
-            if u % 2 == 0:
-                nc.scalar.copy(out=weight[:], in_=positive[:])
+        def add_to_z(s, near):
+            weight, z = weight_of[s], z_of[s]
+            if near:
+                runs = (slice(0, SPLIT), slice(SPLIT, NEAR))
             else:
-                nc.scalar.activation(out=weight[:, 0:S, :], in_=positive[:, 0:S, :], func=ACT.Copy, scale=-1.0)
-                nc.scalar.copy(out=weight[:, S, :], in_=positive[:, S, :])
-            z = table.tile([P, PLACES], F32, bufs=2, offset=12288)
-            nc.vector.tensor_reduce(out=z[:], in_=positive[:].rearrange("p o c -> p c o"), axis=AXIS.X, op=ALU.add)
-            if u % 2 == 0:
-                z_of[u // 2] = z
-            else:
-                one_over_z = table.tile([P, PLACES], F32, bufs=2, offset=12544)
+                runs = (slice(NEAR_SLOTS, FAR_ZERO + 1), slice(FAR_ZERO + 1, NEAR_SLOTS + COLS - NEAR))
+            at = 2 * near
+            for i, slots in enumerate(runs):
+                nc.vector.tensor_reduce(
+                    out=z[:, at + i, :], in_=weight[:, slots, :].rearrange("p o c -> p c o"), axis=AXIS.X, op=ALU.add
+                )
+            nc.vector.tensor_tensor(out=z[:, at, :], in0=z[:, at, :], in1=z[:, at + 1, :], op=ALU.subtract)
+            if near:
+                one_over_z = table.tile([P, PLACES], F32, bufs=2)
                 nc.vector.scalar_tensor_tensor(
-                    out=one_over_z[:], in0=z[:], scalar=1e-06, in1=z_of[u // 2][:], op0=ALU.add, op1=ALU.add
+                    out=one_over_z[:], in0=z[:, 0, :], scalar=1e-06, in1=z[:, 2, :], op0=ALU.add, op1=ALU.add
                 )
                 nc.vector.reciprocal(out=one_over_z[:], in_=one_over_z[:])
-                one_over_z_of[u // 2] = one_over_z
+                one_over_z_of[s] = one_over_z
 
-        def move_weights(u):
-            place = weights_parked[u % 2]
-            nc.sync.dma_start(out=place[0:P, :], in_=weight_of[u][:].rearrange("p o c -> p (o c)"))
-            moved = table.tile([P, HALF_COLS + 1, PLACES], F32, bufs=2, offset=12800)
-            for move, first, last, to in moved_weight_runs(u % 2):
+        def move_weights(s):
+            weight = weight_of[s]
+            for run in range(2):
+                columns = slice(run * SHIFTED_RUN * PLACES, (run + 1) * SHIFTED_RUN * PLACES)
                 nc.sync.dma_start(
-                    out=moved[:, to : to + last - first, :].rearrange("p o c -> p (o c)"),
-                    in_=place[move : move + P, first * PLACES : last * PLACES],
+                    out=rows_of(PARK_AT, P, PARK_ROW)[:, columns],
+                    in_=weight[:, run * SPLIT : run * SPLIT + SHIFTED_RUN, :].rearrange("p o c -> p (o c)"),
                 )
-            moved_weight_of[u] = moved
+            moved = table.tile([P, len(SHIFTED) + 1, PLACES], F32, bufs=2)
+            nc.sync.dma_start(
+                out=moved[:, 0 : len(SHIFTED), :].rearrange("p o c -> p (o c)"), in_=rows_of(PARK_AT + PARK_ROW, P, PARK_ROW)
+            )
+            nc.sync.dma_start(
+                out=moved[:, EXTRA, :],
+                in_=rows_of(PARK_AT + 2 * PARK_ROW, P, PARK_ROW)[:, (EXTRA - 1) * PLACES : EXTRA * PLACES],
+            )
+            moved_weight_of[s] = moved
 
-        weighted_of, acc_of, acc_cols_of, fin_of = {}, {}, {}, {}
-        units = [(u, half, col) for u in range(HALF_STAGES) for half in range(2) for col in MIX_ORDER[u % 2]]
+        matrix_of = {}
+
+        def clear_matrix():
+            zeros = zeros_tile()
+            for part in range(4):
+                nc.sync.dma_start(
+                    out=rows_of(W_AT, P, W_ROW)[:, part * W_ROW // 4 : (part + 1) * W_ROW // 4], in_=zeros[:]
+                )
+
+        def write_matrix(s, half, columns):
+            for col in columns:
+                at = W_AT - OFFSETS[col] // PLACES * W_ROW
+                nc.sync.dma_start(
+                    out=rows_of(at, P, W_ROW + HALF)[:, 0:HALF],
+                    in_=weight_of[s][:, slot_of(col), half * HALF : (half + 1) * HALF],
+                )
+
+        def read_matrix(s, half):
+            matrix = phase.tile([P, P, HALF], F32, bufs=2, offset=63488)
+            nc.sync.dma_start(out=matrix[:].rearrange("p q c -> p (q c)"), in_=rows_of(W_AT, P, W_ROW))
+            matrix_of[s, half] = matrix
+
+        weighted_of, acc_of, acc_cols_of, fin_of, result_of = {}, {}, {}, {}, {}
+        units = [(s, half, col) for s in range(len(STAGES)) for half in HALVES for col in MIX_ORDER]
 
         def cells(col, half):
             found = []
-            for cell in range(MIX_CELLS):
-                place = half * MIX_PLACES + 2 * cell
+            for cell in range(CELLS):
+                place = half * HALF + 2 * cell
                 moves = [[part[2] for part in parts(OFFSETS[col]) if part[0] <= p < part[1]][0] for p in (place, place + 1)]
-                if moves[0] == moves[1]:
-                    found.append((cell, 2 * cell, moves[0]))
-                else:
-                    found.append((cell, 2 * cell, moves[0]))
-                    found.append((cell, MIX_PLACES, moves[1]))
+                found.append((cell, 2 * cell, moves[0]))
+                if moves[0] != moves[1]:
+                    found.append((cell, HALF, moves[1]))
             return found
 
         def weigh(number, by_vector):
-            u, half, col = units[number]
-            weighted = phase.tile([P, MIX_PLACES + 2, HD], F32, bufs=8, offset=0)
-            split = [found[0] for found in cells(col, half) if found[1] == MIX_PLACES]
+            s, half, col = units[number]
+            b, h = STAGES[s]
+            weighted = phase.tile([P, HALF + 2, HD], F32, bufs=8, offset=0)
+            split = [found[0] for found in cells(col, half) if found[1] == HALF]
             for cell in split:
                 nc.vector.memset(weighted[:, 2 * cell + 1, :], 0.0)
-                nc.vector.memset(weighted[:, MIX_PLACES, :], 0.0)
-            for part in parts(OFFSETS[col]):
-                first, last, move, source = part
-                moved_col = moved_weight_col(col, part)
-                for place in range(max(first, half * MIX_PLACES), min(last, (half + 1) * MIX_PLACES)):
-                    c = place - half * MIX_PLACES
-                    slot = MIX_PLACES + 1 if c % 2 == 1 and c // 2 in split else c
-                    v_read = v_of[STAGES[u // 2]][:, source + place - first, :]
-                    if moved_col is None:
-                        scale = weight_of[u][:, col % HALF_COLS, place : place + 1]
+                nc.vector.memset(weighted[:, HALF, :], 0.0)
+            for first, last, move, source in parts(OFFSETS[col]):
+                for place in range(max(first, half * HALF), min(last, (half + 1) * HALF)):
+                    c = place - half * HALF
+                    slot = HALF + 1 if c % 2 == 1 and c // 2 in split else c
+                    v_read = v_of[b][:, h, source + place - first, :]
+                    if move == 0:
+                        scale = weight_of[s][:, col, place : place + 1]
                     else:
-                        scale = moved_weight_of[u][:, moved_col, place : place + 1]
-                    if c >= MIX_PLACES - by_vector:
+                        moved_col = SHIFTED.index(col) if move == 1 else EXTRA
+                        scale = moved_weight_of[s][:, moved_col, place : place + 1]
+                    if c >= HALF - by_vector:
                         nc.vector.tensor_scalar_mul(out=weighted[:, slot, :], in0=v_read, scalar1=scale)
                     else:
                         nc.scalar.activation(out=weighted[:, slot, :], in_=v_read, func=ACT.Copy, scale=scale)
             weighted_of[number] = weighted
 
         def sum_weighted(number):
-            u, half, col = units[number]
-            s = u // 2
-            opens = u % 2 == 0 and col == MIX_ORDER[0][0]
-            closes = u % 2 == 1 and col == MIX_ORDER[1][-1]
+            s, half, col = units[number]
+            opens, closes = col == MIX_ORDER[0], col == MIX_ORDER[-1]
             if opens:
-                for bank in range(MIX_CELLS // 4):
+                for bank in range(CELLS // 4):
                     acc = psum_acc.tile([P, 4, P], F32, tag="acc")
                     acc_of[s, half, bank] = acc
             for cell, slot, move in cells(col, half):
@@ -557,126 +632,171 @@ def tile_dwarfattention_pa_t_kernel(
                 )
 
         def mix_out(s, half):
-            acc_cols = phase.tile([P, MIX_CELLS, P], F32, offset=36864)
-            for bank in range(MIX_CELLS // 4):
+            acc_cols = phase.tile([P, CELLS, P], F32, bufs=2, offset=36864)
+            for bank in range(CELLS // 4):
                 nc.scalar.copy(out=acc_cols[:, 4 * bank : 4 * bank + 4, :], in_=acc_of[s, half, bank][:])
             acc_cols_of[s, half] = acc_cols
 
         def mix_back(s, half):
-            for bank in range(MIX_CELLS // 4):
+            b, h = STAGES[s]
+            for bank in range(CELLS // 4):
                 fin = psum_x.tile([P, 4, P], F32, tag="xt")
+                for i in range(8):
+                    c = 8 * bank + i
+                    nc.tensor.matmul(
+                        fin[:, i // 2, i % 2 * HD : (i % 2 + 1) * HD],
+                        lhsT=matrix_of[s, half][:, :, c],
+                        rhs=v_of[b][:, h, half * HALF + c, :],
+                        start=(i == 0),
+                        stop=False,
+                    )
                 for cell in range(4):
-                    nc.tensor.transpose(fin[:, cell, :], acc_cols_of[s, half][:, 4 * bank + cell, :], ident)
+                    nc.tensor.matmul(
+                        fin[:, cell, :],
+                        lhsT=acc_cols_of[s, half][:, 4 * bank + cell, :],
+                        rhs=ident,
+                        start=False,
+                        stop=(cell == 3),
+                        is_transpose=True,
+                    )
                 fin_of[s, half, bank] = fin
 
-        result_of = {}
-
         def finish(s, half):
-            if half == 0:
-                result = qkv.tile([P, PLACES, HD], F32, tag="q")
+            if half == HALVES[0]:
+                result = qkv.tile([P, PLACES, HD], F32, tag="q", bufs=4)
                 result_of[s] = result
-            for bank in range(MIX_CELLS // 4):
-                for i in range(8):
-                    place = half * MIX_PLACES + 8 * bank + i
-                    nc.scalar.activation(
-                        out=result_of[s][:, place, :],
-                        in_=fin_of[s, half, bank][:].rearrange("p k (c d) -> p (k c) d", d=HD)[:, i, :],
-                        func=ACT.Copy,
-                        scale=one_over_z_of[s][:, place : place + 1],
-                    )
+            for bank in range(CELLS // 4):
+                places = slice(half * HALF + 8 * bank, half * HALF + 8 * bank + 8)
+                nc.vector.tensor_tensor(
+                    out=result_of[s][:, places, :],
+                    in0=fin_of[s, half, bank][:].rearrange("p k (c d) -> p (k c) d", d=HD),
+                    in1=one_over_z_of[s][:, places].unsqueeze(2).to_broadcast([P, 8, HD]),
+                    op=ALU.mult,
+                )
 
         def store(s, half):
             b, h = STAGES[s]
-            places = slice(half * MIX_PLACES, (half + 1) * MIX_PLACES)
+            places = slice(half * HALF, (half + 1) * HALF)
             nc.sync.dma_start(
                 out=out[b].rearrange("(p c) f -> p c f", c=PLACES)[:, places, h * HD : (h + 1) * HD],
                 in_=result_of[s][:, places, :],
             )
 
-        chunks = [(b, j) for b in range(B) for j in range(CHUNKS)]
+        last_chunk = len(chunks) - 1
 
-        def project(i, part):
-            if 0 <= i < len(chunks):
-                if part == 0:
-                    transpose_x(*chunks[i])
-                    if i + 2 < len(chunks):
-                        load_x(*chunks[i + 2])
-                elif part == 1:
-                    quantise_x(*chunks[i])
-                    multiply(*chunks[i])
-                else:
-                    keep(*chunks[i])
+        def project(i, by_vector):
+            if 0 <= i - 1 <= last_chunk:
+                keep_columns(i - 1, by_vector)
+                keep_rows(i - 1)
+            if i <= last_chunk:
+                quantise_x(i)
+            if i + 1 <= last_chunk:
+                transpose_x(i + 1)
+                if i + 3 <= last_chunk:
+                    load_x(i + 3)
+            if 0 <= i - 1 <= last_chunk:
+                far_dots(i - 1)
+                far_dots_out(i - 1, by_vector)
+            if i <= last_chunk:
+                multiply(i)
+
+        dot_steps = len(STAGES) * STEPS
+        last_unit = len(units) - 1
+        end = dot_steps + LAG + STEPS + 6
+        near_rowed = tuple(col for col in ROWED if col < NEAR)
+        far_rowed = tuple(col for col in ROWED if col >= NEAR)
 
         with tc.manual_schedule():
-            project(0, 0)
-            for i in range(CHUNKS + HEAD):
-                project(i + 1, 0)
-                project(i, 1)
-                project(i, 2)
-                if i == CHUNKS - 1:
-                    park_k(0)
-                    move_k(0)
-            gains_of_slots(0)
+            transpose_x(0)
+            load_x(2)
+            for i in range(CHUNKS):
+                project(i, True)
+                if i == CHUNKS // 2:
+                    far_dots_back(0, 0)
+            gains_of_slots(0, True)
+            gains_of_slots(0, False)
 
-            dot_steps = HALF_STAGES * STEPS
-            last_unit = len(units) - 1
-            first_mix = STEPS + LAG
-            end = first_mix + len(units) // UNITS_A_STEP + 5
             mix_done = {}
+            weighed, summed = 0, 0
             for t in range(end):
-                u, step = divmod(t, STEPS)
-                for s in range(1, len(STAGES)):
-                    if t == K_PARK_STEP[s]:
-                        park_k(s)
+                s, step = divmod(t, STEPS)
+                before = s - 1
+                mixing = 0 <= before < len(STAGES)
+                project(CHUNKS + t, t == 0)
+                if t == 0:
+                    park_k(0, 0)
+                    park_k(0, 1)
+                    for ahead in range(K_AHEAD):
+                        load_window(ahead)
+                    far_dots_back(0, 1)
+                elif t == CHUNKS // 2:
+                    far_dots_back(1, 0)
+                elif t == CHUNKS:
+                    far_dots_back(1, 1)
+                    clear_matrix()
+                elif t == STEPS + 1:
+                    park_k(1, 0)
+                elif t == 2 * STEPS - 2:
+                    park_k(1, 1)
+                if t + K_AHEAD < dot_steps:
+                    load_window(t + K_AHEAD)
                 if t < dot_steps:
-                    move_k(t)
-                    products(u, step)
+                    products(t, range(0, NEAR // 2))
+                if mixing and step == 1:
+                    shares(before, True)
+                    weights(before, True)
+                    move_weights(before)
+                if t < dot_steps:
+                    products(t, range(NEAR // 2, NEAR))
                 if 1 <= t <= dot_steps:
-                    sum_products((t - 1) // STEPS, (t - 1) % STEPS)
-                i, part = divmod(t, 2)
-                if part == 0:
-                    if i > 0:
-                        project(CHUNKS + HEAD + i - 1, 2)
-                    project(CHUNKS + HEAD + i + 1, 0)
-                else:
-                    project(CHUNKS + HEAD + i, 1)
-                for stage_half, when in mix_done.items():
+                    sum_products(t - 1)
+                if mixing and step == 0:
+                    dots_out(before)
+                    dots_back(before)
+                    scores(before, True)
+                elif mixing and step == 1:
+                    add_to_z(before, True)
+                    if s < len(STAGES):
+                        gains_of_slots(s, True)
+                if s < len(STAGES):
+                    if step == 5:
+                        scores(s, False)
+                    elif step == 6:
+                        shares(s, False)
+                        if s + 1 < len(STAGES):
+                            gains_of_slots(s + 1, False)
+                        weights(s, False)
+                        add_to_z(s, False)
+                    elif step == 7 and s > 0:
+                        write_matrix(s, HALVES[0], far_rowed)
+                if mixing:
+                    if step == 1 and before > 0:
+                        write_matrix(before, HALVES[0], near_rowed)
+                        read_matrix(before, HALVES[0])
+                    elif step == 3 and before == 0:
+                        write_matrix(before, HALVES[0], ROWED)
+                        read_matrix(before, HALVES[0])
+                    elif step == 5:
+                        write_matrix(before, HALVES[1], ROWED)
+                        read_matrix(before, HALVES[1])
+                for (stage, half), when in mix_done.items():
                     if t == when + 2:
-                        mix_out(*stage_half)
+                        mix_out(stage, half)
                     elif t == when + 3:
-                        mix_back(*stage_half)
-                    elif t == when + 4:
-                        finish(*stage_half)
-                done = u - 1
-                if 0 <= done < HALF_STAGES:
-                    if step == 0:
-                        dots_out(done)
-                    elif step == 1:
-                        dots_back(done)
-                    elif step == 2:
-                        mask_dots(done)
-                        scores(done)
-                    elif step == 3:
-                        shares(done)
-                        if done + 1 < HALF_STAGES:
-                            gains_of_slots(done + 1)
-                        positive_weights(done)
-                    elif step == 4:
-                        weights(done)
-                        move_weights(done)
-                first = UNITS_A_STEP * (t - first_mix)
-                for number in range(first - UNITS_A_STEP, first):
-                    if 0 <= number <= last_unit:
-                        sum_weighted(number)
-                for number in range(first, first + UNITS_A_STEP):
-                    if 0 <= number <= last_unit:
-                        weigh(number, 0 if t < dot_steps else 9)
-                        if units[number][0] % 2 == 1 and units[number][2] == MIX_ORDER[1][-1]:
-                            mix_done[units[number][0] // 2, units[number][1]] = t
-                if t == dot_steps + 4:
-                    for done in range(2):
-                        for half in range(2):
+                        mix_back(stage, half)
+                        finish(stage, half)
+                for number in range(summed, weighed):
+                    sum_weighted(number)
+                summed = weighed
+                wanted = min(last_unit + 1, max(0, (t + 1 - STEPS - LAG) * UNITS_A_STAGE // STEPS))
+                for number in range(weighed, wanted):
+                    weigh(number, 0 if t < dot_steps else 9)
+                    if units[number][2] == MIX_ORDER[-1]:
+                        mix_done[units[number][0], units[number][1]] = t
+                weighed = max(weighed, wanted)
+                if t == dot_steps + STEPS - 1:
+                    for done in range(3):
+                        for half in HALVES:
                             store(done, half)
-            for done in range(2, 4):
-                for half in range(2):
-                    store(done, half)
+            for half in HALVES:
+                store(3, half)

@@ -60,12 +60,10 @@ def slot_of(col):
 
 QUAD = P // PLACES
 QUADS = NEAR // QUAD
-STEP_D = 8
-STEPS = HD // STEP_D
+STEP_D = 16
+STEPS = HD // STEP_D * QUADS
 WINDOW = 4 * PLACES
 BACK = WINDOW - PLACES
-K_BUFFERS = 4
-K_AHEAD = 3
 HALF = PLACES // 2
 CELLS = HALF // 2
 
@@ -80,10 +78,10 @@ PARK_PAD = 2
 SHIFTED_RUN = SPLIT - 1
 EXTRA = len(SHIFTED)
 
+HEAD = 1
+
 FAR_RUNS = ((NEAR, 2), (NEAR + 2, 2), (NEAR + 4, 2), (ZERO, 1), (ZERO + 1, 2), (ZERO + 3, 2), (ZERO + 5, 1))
 
-LAG = 2
-UNITS_A_STAGE = 2 * len(SHIFTED)
 
 FLOPS = 2 * B * N * D * 3 * H * HD + B * H * N * (4 * S + 1) * 4 * HD
 
@@ -106,8 +104,8 @@ def tile_dwarfattention_pa_t_kernel(
     with ExitStack() as ctx:
         const = ctx.enter_context(tc.tile_pool(name="const", bufs=1))
         qkv = ctx.enter_context(tc.tile_pool(name="qkv", bufs=2))
-        prods = ctx.enter_context(tc.tile_pool(name="prods", bufs=2))
-        windows = ctx.enter_context(tc.tile_pool(name="windows", bufs=K_BUFFERS))
+        prods = ctx.enter_context(tc.tile_pool(name="prods", bufs=3))
+        windows = ctx.enter_context(tc.tile_pool(name="windows", bufs=2))
         table = ctx.enter_context(tc.tile_pool(name="table", bufs=1))
         phase = ctx.enter_context(tc.tile_pool(name="phase", bufs=1))
         psum_x = ctx.enter_context(tc.psum_pool(name="psum_x", bufs=3))
@@ -196,14 +194,19 @@ def tile_dwarfattention_pa_t_kernel(
         for col in range(COLS):
             nc.vector.tensor_single_scalar(out=reached[:, col, :], in_=token[:], scalar=float(OFFSETS[col]), op=ALU.is_ge)
 
-        q_split = const.tile([P, CHUNK, 2 * P], F32)
-        nc.gpsimd.memset(q_split[:], 0.0)
+        q_splits = []
+        for i in range(2):
+            q_split = const.tile([P, CHUNK, 2 * P], F32, name="q_split_%d" % i)
+            nc.gpsimd.memset(q_split[:], 0.0)
+            q_splits.append(q_split)
 
         bias_col = const.tile([P, 2], F32)
-        bias_t = psum_x.tile([P, 2, P], F32, tag="xt")
-        for part in range(2):
-            nc.tensor.transpose(bias_t[:, part, :], bias[:, part, :], ident)
-        nc.scalar.copy(out=bias_col[:], in_=bias_t[:, :, 0])
+
+        def turn_bias():
+            bias_t = psum_x.tile([P, 2, P], F32, tag="xt")
+            for part in range(2):
+                nc.tensor.transpose(bias_t[:, part, :], bias[:, part, :], ident)
+            nc.scalar.copy(out=bias_col[:], in_=bias_t[:, :, 0])
 
         def zeros_tile():
             zeros = phase.tile([P, W_ROW // 4], F32, offset=45056)
@@ -211,7 +214,8 @@ def tile_dwarfattention_pa_t_kernel(
             return zeros
 
         zeros = zeros_tile()
-        nc.sync.dma_start(out=rows_of(K_AT - 512, 1, 512), in_=zeros[0:1, :])
+        for part in range(4):
+            nc.sync.dma_start(out=rows_of(W_AT + part * P * W_ROW // 4, P, W_ROW // 4), in_=zeros[:])
         nc.sync.dma_start(out=rows_of(PARK_AT + P * PARK_ROW, PARK_PAD, PARK_ROW), in_=zeros[0:PARK_PAD, 0:PARK_ROW])
 
         q_of, v_of, v_tile_of, k_t_of, k_chunk_of, s_ps_of, s_of = {}, {}, {}, {}, {}, {}, {}
@@ -308,7 +312,7 @@ def tile_dwarfattention_pa_t_kernel(
             for h in range(H):
                 mine = slice(h * HD, (h + 1) * HD)
                 nc.scalar.activation(
-                    out=q_split[mine, :, h * P : (h + 1) * P],
+                    out=q_splits[i % 2][mine, :, h * P : (h + 1) * P],
                     in_=q_ps[mine, :, :],
                     func=ACT.Identity,
                     bias=bias_col[mine, 0:1],
@@ -332,7 +336,7 @@ def tile_dwarfattention_pa_t_kernel(
                 for odd in range(2):
                     nc.tensor.matmul(
                         out=s_ps[:, c, odd, :],
-                        lhsT=q_split[:, c, odd : 2 * P : 2],
+                        lhsT=q_splits[i % 2][:, c, odd : 2 * P : 2],
                         rhs=k_chunk_of[i][:, c, 1 - odd : P : 2],
                         start=True,
                         stop=True,
@@ -354,23 +358,23 @@ def tile_dwarfattention_pa_t_kernel(
 
         dots_of = {}
 
-        def far_dots_back(b, group):
-            if group == 0:
-                for h in range(H):
+        def store_far_dots(b, group):
+            nc.sync.dma_start(out=rows_of(S_AT, P, S_ROW), in_=s_of[b, group][:].rearrange("p s k c -> p (s k c)"))
+
+        def fetch_far_dots(b, group, odd):
+            for h in range(H):
+                if group == 0 and odd == 0:
                     dots = table.tile([P, COLS, PLACES], F32, bufs=4)
                     dots_of[2 * b + h] = dots
-            nc.sync.dma_start(out=rows_of(S_AT, P, S_ROW), in_=s_of[b, group][:].rearrange("p s k c -> p (s k c)"))
-            for odd in range(2):
-                for h in range(H):
-                    at = S_AT + h * IN_CLASS * S_ROW + odd * S_ROW // 2 + (IN_CLASS - 1) * HALF
-                    rows = rows_of(at, IN_CLASS, S_ROW - HALF)
-                    for col, count in FAR_RUNS:
-                        start = OFFSETS[col] // CLASS * HALF
-                        step = HALF if count == 1 else start
-                        nc.sync.dma_start(
-                            out=dots_of[2 * b + h][odd:P:2, col : col + count, group * HALF : (group + 1) * HALF],
-                            in_=rows[:, start : start + count * step].rearrange("r (g k) -> r g k", k=step)[:, :, 0:HALF],
-                        )
+                at = S_AT + h * IN_CLASS * S_ROW + odd * S_ROW // 2 + (IN_CLASS - 1) * HALF
+                rows = rows_of(at, IN_CLASS, S_ROW - HALF)
+                for col, count in FAR_RUNS:
+                    start = OFFSETS[col] // CLASS * HALF
+                    step = HALF if count == 1 else start
+                    nc.sync.dma_start(
+                        out=dots_of[2 * b + h][odd:P:2, col : col + count, group * HALF : (group + 1) * HALF],
+                        in_=rows[:, start : start + count * step].rearrange("r (g k) -> r g k", k=step)[:, :, 0:HALF],
+                    )
 
         prod_of, dots_ps_of, window_of = {}, {}, {}
 
@@ -380,10 +384,10 @@ def tile_dwarfattention_pa_t_kernel(
                 in_=k_t_of[b][h * HD : (h + 1) * HD].rearrange("p a c -> p (a c)"),
             )
 
-        def load_window(t):
-            s, step = divmod(t, STEPS)
+        def load_window(n):
+            s, group = divmod(n, HD // STEP_D)
             window = windows.tile([P, STEP_D, WINDOW], F32)
-            at = K_AT + (s % H * HD + step * STEP_D) * N - BACK
+            at = K_AT + (s % H * HD + group * STEP_D) * N - BACK
             for r in range(WINDOW // PLACES):
                 nc.sync.dma_start(
                     out=window[r : P : WINDOW // PLACES],
@@ -391,38 +395,37 @@ def tile_dwarfattention_pa_t_kernel(
                         "(d a t) -> a d t", d=STEP_D, t=WINDOW
                     ),
                 )
-            window_of[t] = window
+            window_of[n] = window
 
-        def products(t, columns):
+        def products(t):
             s, step = divmod(t, STEPS)
-            d0 = step * STEP_D
-            if columns[0] == 0:
-                prod = prods.tile([P, STEP_D, QUADS, QUAD, PLACES], F32)
-                prod_of[t] = prod
-            for i in columns:
-                first = BACK - OFFSETS[i]
+            group, quad = divmod(step, QUADS)
+            prod = prods.tile([P, STEP_D, QUAD, PLACES], F32)
+            for i in range(QUAD):
+                first = BACK - OFFSETS[quad * QUAD + i]
                 nc.vector.tensor_tensor(
-                    out=prod_of[t][:, :, i // QUAD, i % QUAD, :],
-                    in0=q_of[STAGES[s]][:, d0 : d0 + STEP_D, :],
-                    in1=window_of[t][:, :, first : first + PLACES],
+                    out=prod[:, :, i, :],
+                    in0=q_of[STAGES[s]][:, group * STEP_D : (group + 1) * STEP_D, :],
+                    in1=window_of[t // QUADS][:, :, first : first + PLACES],
                     op=ALU.mult,
                 )
+            prod_of[t] = prod
 
         def sum_products(t):
             s, step = divmod(t, STEPS)
+            quad = step % QUADS
             if step == 0:
                 dots_ps = psum_dots.tile([P, QUADS, P], F32)
                 dots_ps_of[s] = dots_ps
             for d in range(STEP_D):
-                for quad in range(QUADS):
-                    nc.tensor.matmul(
-                        dots_ps_of[s][:, quad, :],
-                        lhsT=prod_of[t][:, d, quad, :, :].rearrange("p i c -> p (i c)"),
-                        rhs=ident,
-                        start=(step == 0 and d == 0 and quad == 0),
-                        stop=(step == STEPS - 1 and d == STEP_D - 1 and quad == QUADS - 1),
-                        is_transpose=True,
-                    )
+                nc.tensor.matmul(
+                    dots_ps_of[s][:, quad, :],
+                    lhsT=prod_of[t][:, d, :, :].rearrange("p i c -> p (i c)"),
+                    rhs=ident,
+                    start=(step == 0 and d == 0),
+                    stop=(step == STEPS - 1 and d == STEP_D - 1),
+                    is_transpose=True,
+                )
 
         turned_of, weight_of, moved_weight_of, z_of, one_over_z_of = {}, {}, {}, {}, {}
 
@@ -466,6 +469,9 @@ def tile_dwarfattention_pa_t_kernel(
                     in1=bias_plus_1[:, at : at + count, h : h + 1].to_broadcast([P, count, PLACES]),
                     op=ALU.add,
                 )
+
+        def exponentials(s, near):
+            slots = slice(0, NEAR_SLOTS) if near else slice(NEAR_SLOTS, SLOTS)
             nc.scalar.activation(
                 out=weight_of[s][:, slots, :],
                 in_=u1[:, 0 : slots.stop - slots.start, :],
@@ -537,14 +543,15 @@ def tile_dwarfattention_pa_t_kernel(
                 nc.vector.reciprocal(out=one_over_z[:], in_=one_over_z[:])
                 one_over_z_of[s] = one_over_z
 
-        def move_weights(s):
-            weight = weight_of[s]
+        def park_weights(s):
             for run in range(2):
                 columns = slice(run * SHIFTED_RUN * PLACES, (run + 1) * SHIFTED_RUN * PLACES)
                 nc.sync.dma_start(
                     out=rows_of(PARK_AT, P, PARK_ROW)[:, columns],
-                    in_=weight[:, run * SPLIT : run * SPLIT + SHIFTED_RUN, :].rearrange("p o c -> p (o c)"),
+                    in_=weight_of[s][:, run * SPLIT : run * SPLIT + SHIFTED_RUN, :].rearrange("p o c -> p (o c)"),
                 )
+
+        def move_weights(s):
             moved = table.tile([P, len(SHIFTED) + 1, PLACES], F32, bufs=2)
             nc.sync.dma_start(
                 out=moved[:, 0 : len(SHIFTED), :].rearrange("p o c -> p (o c)"), in_=rows_of(PARK_AT + PARK_ROW, P, PARK_ROW)
@@ -557,12 +564,10 @@ def tile_dwarfattention_pa_t_kernel(
 
         matrix_of = {}
 
-        def clear_matrix():
+        def clear_matrix(rows):
             zeros = zeros_tile()
-            for part in range(4):
-                nc.sync.dma_start(
-                    out=rows_of(W_AT, P, W_ROW)[:, part * W_ROW // 4 : (part + 1) * W_ROW // 4], in_=zeros[:]
-                )
+            for part in range(0, rows, 32):
+                nc.sync.dma_start(out=rows_of(W_AT + part * W_ROW, P, W_ROW // 4), in_=zeros[:])
 
         def write_matrix(s, half, columns):
             for col in columns:
@@ -578,7 +583,6 @@ def tile_dwarfattention_pa_t_kernel(
             matrix_of[s, half] = matrix
 
         weighted_of, acc_of, acc_cols_of, fin_of, result_of = {}, {}, {}, {}, {}
-        units = [(s, half, col) for s in range(len(STAGES)) for half in HALVES for col in MIX_ORDER]
 
         def cells(col, half):
             found = []
@@ -590,9 +594,9 @@ def tile_dwarfattention_pa_t_kernel(
                     found.append((cell, HALF, moves[1]))
             return found
 
-        def weigh(number, by_vector):
-            s, half, col = units[number]
+        def weigh(s, half, k, by_vector):
             b, h = STAGES[s]
+            col = MIX_ORDER[k]
             weighted = phase.tile([P, HALF + 2, HD], F32, bufs=8, offset=0)
             split = [found[0] for found in cells(col, half) if found[1] == HALF]
             for cell in split:
@@ -612,11 +616,11 @@ def tile_dwarfattention_pa_t_kernel(
                         nc.vector.tensor_scalar_mul(out=weighted[:, slot, :], in0=v_read, scalar1=scale)
                     else:
                         nc.scalar.activation(out=weighted[:, slot, :], in_=v_read, func=ACT.Copy, scale=scale)
-            weighted_of[number] = weighted
+            weighted_of[s, half, k] = weighted
 
-        def sum_weighted(number):
-            s, half, col = units[number]
-            opens, closes = col == MIX_ORDER[0], col == MIX_ORDER[-1]
+        def sum_weighted(s, half, k):
+            col = MIX_ORDER[k]
+            opens, closes = k == 0, k == len(MIX_ORDER) - 1
             if opens:
                 for bank in range(CELLS // 4):
                     acc = psum_acc.tile([P, 4, P], F32, tag="acc")
@@ -624,7 +628,7 @@ def tile_dwarfattention_pa_t_kernel(
             for cell, slot, move in cells(col, half):
                 nc.tensor.matmul(
                     acc_of[s, half, cell // 4][:, cell % 4, :],
-                    lhsT=weighted_of[number][:, slot : slot + 2, :].rearrange("p c d -> p (c d)"),
+                    lhsT=weighted_of[s, half, k][:, slot : slot + 2, :].rearrange("p c d -> p (c d)"),
                     rhs=ident_twice[:, P - move : 2 * P - move],
                     start=(opens and cell % 4 == 0),
                     stop=(closes and cell % 4 == 3),
@@ -637,29 +641,30 @@ def tile_dwarfattention_pa_t_kernel(
                 nc.scalar.copy(out=acc_cols[:, 4 * bank : 4 * bank + 4, :], in_=acc_of[s, half, bank][:])
             acc_cols_of[s, half] = acc_cols
 
-        def mix_back(s, half):
+        def mix_far(s, half, i):
             b, h = STAGES[s]
-            for bank in range(CELLS // 4):
+            bank, place = divmod(i, 8)
+            if place == 0:
                 fin = psum_x.tile([P, 4, P], F32, tag="xt")
-                for i in range(8):
-                    c = 8 * bank + i
-                    nc.tensor.matmul(
-                        fin[:, i // 2, i % 2 * HD : (i % 2 + 1) * HD],
-                        lhsT=matrix_of[s, half][:, :, c],
-                        rhs=v_of[b][:, h, half * HALF + c, :],
-                        start=(i == 0),
-                        stop=False,
-                    )
-                for cell in range(4):
-                    nc.tensor.matmul(
-                        fin[:, cell, :],
-                        lhsT=acc_cols_of[s, half][:, 4 * bank + cell, :],
-                        rhs=ident,
-                        start=False,
-                        stop=(cell == 3),
-                        is_transpose=True,
-                    )
                 fin_of[s, half, bank] = fin
+            nc.tensor.matmul(
+                fin_of[s, half, bank][:, place // 2, place % 2 * HD : (place % 2 + 1) * HD],
+                lhsT=matrix_of[s, half][:, :, i],
+                rhs=v_of[b][:, h, half * HALF + i, :],
+                start=(place == 0),
+                stop=False,
+            )
+
+        def mix_back(s, half):
+            for cell in range(CELLS):
+                nc.tensor.matmul(
+                    fin_of[s, half, cell // 4][:, cell % 4, :],
+                    lhsT=acc_cols_of[s, half][:, cell, :],
+                    rhs=ident,
+                    start=False,
+                    stop=(cell % 4 == 3),
+                    is_transpose=True,
+                )
 
         def finish(s, half):
             if half == HALVES[0]:
@@ -683,117 +688,171 @@ def tile_dwarfattention_pa_t_kernel(
             )
 
         last_chunk = len(chunks) - 1
-
-        def project(i, by_vector):
-            if 0 <= i - 1 <= last_chunk:
-                keep_columns(i - 1, by_vector)
-                keep_rows(i - 1)
-            if i <= last_chunk:
-                quantise_x(i)
-            if i + 1 <= last_chunk:
-                transpose_x(i + 1)
-                if i + 3 <= last_chunk:
-                    load_x(i + 3)
-            if 0 <= i - 1 <= last_chunk:
-                far_dots(i - 1)
-                far_dots_out(i - 1, by_vector)
-            if i <= last_chunk:
-                multiply(i)
-
-        dot_steps = len(STAGES) * STEPS
-        last_unit = len(units) - 1
-        end = dot_steps + LAG + STEPS + 6
         near_rowed = tuple(col for col in ROWED if col < NEAR)
         far_rowed = tuple(col for col in ROWED if col >= NEAR)
+        dot_steps = len(STAGES) * STEPS
+
+        units_at, plan = {}, {}
+
+        def plan_at(t, *work):
+            plan.setdefault(t, []).append(work)
+
+        for s in range(len(STAGES)):
+            start, last = STEPS * (s + 1), s == len(STAGES) - 1
+            units = [(half, k) for half in HALVES for k in range(len(MIX_ORDER))]
+            for n, (half, k) in enumerate(units):
+                t = start + ((1 + n * 8 // len(units)) if last else (3 + n * 9 // len(units)))
+                units_at.setdefault(t, []).append((s, half, k))
+                if k == len(MIX_ORDER) - 1:
+                    mixed = t + (3 if last else 2)
+                    far_from, far_steps = ((9, 3) if half == HALVES[0] else (13, 3)) if s == 0 else ((7, 3) if half == HALVES[0] else (10, 3))
+                    for i in range(HALF):
+                        plan_at(start + far_from + i * far_steps // HALF, mix_far, s, half, i)
+                    done = max(mixed + 1, start + far_from + far_steps)
+                    plan_at(mixed, mix_out, s, half)
+                    plan_at(done, mix_back, s, half)
+                    plan_at(done, finish, s, half)
+        end = max(plan) + 1
+
+        def project(i, part, early):
+            if part == 0:
+                if i + 2 <= last_chunk:
+                    transpose_x(i + 2)
+                    if i + 4 <= last_chunk:
+                        load_x(i + 4)
+                if early and i > 0:
+                    keep_rows(i - 1)
+                if 0 <= i - 1 <= last_chunk:
+                    far_dots(i - 1)
+                    far_dots_out(i - 1, early)
+            elif part == 1:
+                if not early and i - 1 <= last_chunk:
+                    keep_rows(i - 1)
+                if i + 1 <= last_chunk:
+                    quantise_x(i + 1)
+            elif i <= last_chunk:
+                multiply(i)
+                keep_columns(i, early)
 
         with tc.manual_schedule():
             transpose_x(0)
             load_x(2)
-            for i in range(CHUNKS):
-                project(i, True)
+            transpose_x(1)
+            load_x(3)
+            quantise_x(0)
+            turn_bias()
+            for i in range(CHUNKS + HEAD):
+                for part in range(3):
+                    project(i, part, True)
                 if i == CHUNKS // 2:
-                    far_dots_back(0, 0)
+                    store_far_dots(0, 0)
+                elif i == CHUNKS // 2 + 1:
+                    for odd in range(2):
+                        fetch_far_dots(0, 0, odd)
+                elif i == CHUNKS - 1:
+                    park_k(0, 0)
+                    park_k(0, 1)
+                    load_window(0)
+                elif i == CHUNKS:
+                    store_far_dots(0, 1)
             gains_of_slots(0, True)
             gains_of_slots(0, False)
 
-            mix_done = {}
-            weighed, summed = 0, 0
+            next_chunk = CHUNKS + HEAD
             for t in range(end):
                 s, step = divmod(t, STEPS)
                 before = s - 1
                 mixing = 0 <= before < len(STAGES)
-                project(CHUNKS + t, t == 0)
-                if t == 0:
-                    park_k(0, 0)
-                    park_k(0, 1)
-                    for ahead in range(K_AHEAD):
-                        load_window(ahead)
-                    far_dots_back(0, 1)
-                elif t == CHUNKS // 2:
-                    far_dots_back(1, 0)
-                elif t == CHUNKS:
-                    far_dots_back(1, 1)
-                    clear_matrix()
-                elif t == STEPS + 1:
+                projecting = t % 3 != 2 and next_chunk <= last_chunk + 1
+                if projecting:
+                    project(next_chunk, 0, False)
+                if t < dot_steps and step % QUADS == 0 and t // QUADS + 1 < dot_steps // QUADS:
+                    load_window(t // QUADS + 1)
+                if t == 1:
+                    for odd in range(2):
+                        fetch_far_dots(0, 1, odd)
+                elif t == 5:
+                    store_far_dots(1, 0)
+                elif t == 5 + 1:
+                    for odd in range(2):
+                        fetch_far_dots(1, 0, odd)
+                elif t == STEPS:
+                    store_far_dots(1, 1)
+                elif t == STEPS + 2:
+                    for odd in range(2):
+                        fetch_far_dots(1, 1, odd)
+                elif t == STEPS + 3:
+                    clear_matrix(32)
+                elif t == STEPS + 5:
                     park_k(1, 0)
                 elif t == 2 * STEPS - 2:
                     park_k(1, 1)
-                if t + K_AHEAD < dot_steps:
-                    load_window(t + K_AHEAD)
                 if t < dot_steps:
-                    products(t, range(0, NEAR // 2))
-                if mixing and step == 1:
+                    products(t)
+                if projecting:
+                    project(next_chunk, 1, False)
+                if mixing and step == 1 and t < dot_steps:
+                    scores(before, True)
+                elif mixing and step == 1 + 1 and t < dot_steps:
                     shares(before, True)
                     weights(before, True)
-                    move_weights(before)
-                if t < dot_steps:
-                    products(t, range(NEAR // 2, NEAR))
-                if 1 <= t <= dot_steps:
-                    sum_products(t - 1)
-                if mixing and step == 0:
-                    dots_out(before)
-                    dots_back(before)
-                    scores(before, True)
-                elif mixing and step == 1:
+                    park_weights(before)
                     add_to_z(before, True)
                     if s < len(STAGES):
                         gains_of_slots(s, True)
+                if 1 <= t <= dot_steps:
+                    sum_products(t - 1)
+                if projecting:
+                    project(next_chunk, 2, False)
+                    next_chunk += 1
+                if t == dot_steps:
+                    dots_out(before)
+                    dots_back(before)
+                    scores(before, True)
+                    exponentials(before, True)
+                    shares(before, True)
+                    weights(before, True)
+                    park_weights(before)
                 if s < len(STAGES):
-                    if step == 5:
+                    if step == 7:
                         scores(s, False)
-                    elif step == 6:
+                    elif step == 8:
                         shares(s, False)
                         if s + 1 < len(STAGES):
                             gains_of_slots(s + 1, False)
                         weights(s, False)
                         add_to_z(s, False)
-                    elif step == 7 and s > 0:
+                    elif step == 10 and s > 1:
                         write_matrix(s, HALVES[0], far_rowed)
                 if mixing:
-                    if step == 1 and before > 0:
-                        write_matrix(before, HALVES[0], near_rowed)
+                    late = 3 if before == 0 else -1 if t >= dot_steps else 0
+                    if step == 0 and before == 1:
+                        write_matrix(before, HALVES[0], far_rowed)
+                    if step == 4:
+                        move_weights(before)
+                    if step == 2 + late:
+                        write_matrix(before, HALVES[0], ROWED if before == 0 else near_rowed)
+                    elif step == 4 + late:
                         read_matrix(before, HALVES[0])
-                    elif step == 3 and before == 0:
-                        write_matrix(before, HALVES[0], ROWED)
-                        read_matrix(before, HALVES[0])
-                    elif step == 5:
+                    elif step == 6 + late:
                         write_matrix(before, HALVES[1], ROWED)
+                    elif step == 8 + late:
                         read_matrix(before, HALVES[1])
-                for (stage, half), when in mix_done.items():
-                    if t == when + 2:
-                        mix_out(stage, half)
-                    elif t == when + 3:
-                        mix_back(stage, half)
-                        finish(stage, half)
-                for number in range(summed, weighed):
-                    sum_weighted(number)
-                summed = weighed
-                wanted = min(last_unit + 1, max(0, (t + 1 - STEPS - LAG) * UNITS_A_STAGE // STEPS))
-                for number in range(weighed, wanted):
-                    weigh(number, 0 if t < dot_steps else 9)
-                    if units[number][2] == MIX_ORDER[-1]:
-                        mix_done[units[number][0], units[number][1]] = t
-                weighed = max(weighed, wanted)
+                for work in plan.get(t, ()):
+                    work[0](*work[1:])
+                for unit in units_at.get(t - 1, ()):
+                    sum_weighted(*unit)
+                for unit in units_at.get(t, ()):
+                    weigh(*unit, 0 if t < dot_steps else 8)
+                if mixing and step == 0 and t < dot_steps:
+                    dots_out(before)
+                    dots_back(before)
+                elif mixing and step == 1 and t < dot_steps:
+                    exponentials(before, True)
+                elif s < len(STAGES) and step == 7:
+                    exponentials(s, False)
+                if t == dot_steps + 2:
+                    add_to_z(before, True)
                 if t == dot_steps + STEPS - 1:
                     for done in range(3):
                         for half in HALVES:

@@ -196,7 +196,7 @@ def tile_dwarfattention_pa_t_kernel(
 
         q_splits = []
         for i in range(2):
-            q_split = const.tile([P, CHUNK, 2 * P], F32, name="q_split_%d" % i)
+            q_split = const.tile([P, CHUNK, 2, H * IN_CLASS], F32, name="q_split_%d" % i)
             nc.gpsimd.memset(q_split[:], 0.0)
             q_splits.append(q_split)
 
@@ -312,13 +312,15 @@ def tile_dwarfattention_pa_t_kernel(
             for h in range(H):
                 mine = slice(h * HD, (h + 1) * HD)
                 nc.scalar.activation(
-                    out=q_splits[i % 2][mine, :, h * P : (h + 1) * P],
-                    in_=q_ps[mine, :, :],
+                    out=q_splits[i % 2][mine, :, :, h * IN_CLASS : (h + 1) * IN_CLASS],
+                    in_=q_ps[mine, :, :].rearrange("p c (k s) -> p c s k", s=2),
                     func=ACT.Identity,
                     bias=bias_col[mine, 0:1],
                 )
-            k_chunk = phase.tile([P, CHUNK, P], F32, bufs=2, offset=43008)
-            nc.scalar.activation(out=k_chunk[:], in_=k_ps[:, :, ::-1], func=ACT.Identity, bias=bias_col[:, 1:2])
+            k_chunk = phase.tile([P, CHUNK, 2, IN_CLASS], F32, bufs=2, offset=43008)
+            nc.scalar.activation(
+                out=k_chunk[:], in_=k_ps[:, :, ::-1].rearrange("p c (k s) -> p c s k", s=2), func=ACT.Identity, bias=bias_col[:, 1:2]
+            )
             k_chunk_of[i] = k_chunk
             if j == 0:
                 k_t = phase.tile([P, P, PLACES], F32, offset=47104)
@@ -336,8 +338,8 @@ def tile_dwarfattention_pa_t_kernel(
                 for odd in range(2):
                     nc.tensor.matmul(
                         out=s_ps[:, c, odd, :],
-                        lhsT=q_splits[i % 2][:, c, odd : 2 * P : 2],
-                        rhs=k_chunk_of[i][:, c, 1 - odd : P : 2],
+                        lhsT=q_splits[i % 2][:, c, odd, :],
+                        rhs=k_chunk_of[i][:, c, 1 - odd, :],
                         start=True,
                         stop=True,
                     )
@@ -562,7 +564,7 @@ def tile_dwarfattention_pa_t_kernel(
             )
             moved_weight_of[s] = moved
 
-        matrix_of = {}
+        loaded_of, matrix_of = {}, {}
 
         def clear_matrix(rows):
             zeros = zeros_tile()
@@ -578,8 +580,16 @@ def tile_dwarfattention_pa_t_kernel(
                 )
 
         def read_matrix(s, half):
-            matrix = phase.tile([P, P, HALF], F32, bufs=2, offset=63488)
-            nc.sync.dma_start(out=matrix[:].rearrange("p q c -> p (q c)"), in_=rows_of(W_AT, P, W_ROW))
+            loaded = phase.tile([P, P, HALF], F32, offset=35840)
+            nc.sync.dma_start(out=loaded[:].rearrange("p q c -> p (q c)"), in_=rows_of(W_AT, P, W_ROW))
+            loaded_of[s, half] = loaded
+
+        def turn_matrix(s, half):
+            matrix = phase.tile([P, HALF, P], F32, bufs=2, offset=63488)
+            nc.scalar.copy(
+                out=matrix[:].rearrange("p (g k) q -> p g q k", k=4),
+                in_=loaded_of[s, half][:].rearrange("p q (g k) -> p g q k", k=4),
+            )
             matrix_of[s, half] = matrix
 
         weighted_of, acc_of, acc_cols_of, fin_of, result_of = {}, {}, {}, {}, {}
@@ -597,7 +607,7 @@ def tile_dwarfattention_pa_t_kernel(
         def weigh(s, half, k, by_vector):
             b, h = STAGES[s]
             col = MIX_ORDER[k]
-            weighted = phase.tile([P, HALF + 2, HD], F32, bufs=8, offset=0)
+            weighted = phase.tile([P, HALF + 2, HD], F32, bufs=6, offset=0)
             split = [found[0] for found in cells(col, half) if found[1] == HALF]
             for cell in split:
                 nc.vector.memset(weighted[:, 2 * cell + 1, :], 0.0)
@@ -636,7 +646,7 @@ def tile_dwarfattention_pa_t_kernel(
                 )
 
         def mix_out(s, half):
-            acc_cols = phase.tile([P, CELLS, P], F32, bufs=2, offset=36864)
+            acc_cols = phase.tile([P, CELLS, P], F32, bufs=2, offset=27648)
             for bank in range(CELLS // 4):
                 nc.scalar.copy(out=acc_cols[:, 4 * bank : 4 * bank + 4, :], in_=acc_of[s, half, bank][:])
             acc_cols_of[s, half] = acc_cols
@@ -649,7 +659,7 @@ def tile_dwarfattention_pa_t_kernel(
                 fin_of[s, half, bank] = fin
             nc.tensor.matmul(
                 fin_of[s, half, bank][:, place // 2, place % 2 * HD : (place % 2 + 1) * HD],
-                lhsT=matrix_of[s, half][:, :, i],
+                lhsT=matrix_of[s, half][:, i, :],
                 rhs=v_of[b][:, h, half * HALF + i, :],
                 start=(place == 0),
                 stop=False,
@@ -699,13 +709,21 @@ def tile_dwarfattention_pa_t_kernel(
 
         for s in range(len(STAGES)):
             start, last = STEPS * (s + 1), s == len(STAGES) - 1
+            first = (5, 5, 7, 9, 9, 11, 13) if s == 0 else (-2, 1, 2, 3, 3, 4, 6) if last else (0 if s == 1 else -2, 2, 4, 6, 6, 8, 10)
+            plan_at(start + first[0], write_matrix, s, HALVES[0], far_rowed)
+            plan_at(start + first[1], write_matrix, s, HALVES[0], near_rowed)
+            plan_at(start + first[2], read_matrix, s, HALVES[0])
+            plan_at(start + first[3], turn_matrix, s, HALVES[0])
+            plan_at(start + first[4], write_matrix, s, HALVES[1], ROWED)
+            plan_at(start + first[5], read_matrix, s, HALVES[1])
+            plan_at(start + first[6], turn_matrix, s, HALVES[1])
             units = [(half, k) for half in HALVES for k in range(len(MIX_ORDER))]
             for n, (half, k) in enumerate(units):
                 t = start + ((1 + n * 8 // len(units)) if last else (3 + n * 9 // len(units)))
                 units_at.setdefault(t, []).append((s, half, k))
                 if k == len(MIX_ORDER) - 1:
                     mixed = t + (3 if last else 2)
-                    far_from, far_steps = ((9, 3) if half == HALVES[0] else (13, 3)) if s == 0 else ((7, 3) if half == HALVES[0] else (10, 3))
+                    far_from, far_steps = ((10, 3) if half == HALVES[0] else (14, 3)) if s == 0 else ((4, 4) if half == HALVES[0] else (8, 4)) if last else ((8, 3) if half == HALVES[0] else (11, 3))
                     for i in range(HALF):
                         plan_at(start + far_from + i * far_steps // HALF, mix_far, s, half, i)
                     done = max(mixed + 1, start + far_from + far_steps)
@@ -822,22 +840,9 @@ def tile_dwarfattention_pa_t_kernel(
                             gains_of_slots(s + 1, False)
                         weights(s, False)
                         add_to_z(s, False)
-                    elif step == 10 and s > 1:
-                        write_matrix(s, HALVES[0], far_rowed)
                 if mixing:
-                    late = 3 if before == 0 else -1 if t >= dot_steps else 0
-                    if step == 0 and before == 1:
-                        write_matrix(before, HALVES[0], far_rowed)
                     if step == 4:
                         move_weights(before)
-                    if step == 2 + late:
-                        write_matrix(before, HALVES[0], ROWED if before == 0 else near_rowed)
-                    elif step == 4 + late:
-                        read_matrix(before, HALVES[0])
-                    elif step == 6 + late:
-                        write_matrix(before, HALVES[1], ROWED)
-                    elif step == 8 + late:
-                        read_matrix(before, HALVES[1])
                 for work in plan.get(t, ()):
                     work[0](*work[1:])
                 for unit in units_at.get(t - 1, ()):

@@ -117,7 +117,7 @@ def tile_dwarfattention_pa_t_kernel(
         def rows_of(at, count, width):
             return flat[at : at + count * width].rearrange("(r w) -> r w", w=width)
 
-        x_rows_of, grouped_of, codes_of, qkv_ps_of = {}, {}, {}, {}
+        x_rows_of, x_sorted_of, grouped_of, codes_of, qkv_ps_of = {}, {}, {}, {}, {}
 
         def load_x(i):
             b, j = chunks[i]
@@ -220,20 +220,31 @@ def tile_dwarfattention_pa_t_kernel(
 
         q_of, v_of, v_tile_of, k_t_of, k_chunk_of, s_ps_of, s_of = {}, {}, {}, {}, {}, {}, {}
 
+        def sort_x(i):
+            x_sorted = prods.tile([P, CHUNK, PASSES, 2, P], I32, tag="prod")
+            nc.gpsimd.tensor_copy(
+                out=x_sorted[:].rearrange("p c g u k -> p (c g) u k"),
+                in_=x_rows_of[i][:].rearrange("p c d -> p (c d)").bitcast(I32).rearrange("p (m k u) -> p m u k", k=P, u=2),
+            )
+            x_sorted_of[i] = x_sorted
+
         def transpose_x(i):
             grouped = phase.tile([P, PASSES, CHUNK * P * PACK], BF16, bufs=2, offset=16384, align_bytes=64)
             for g in range(PASSES):
                 grouped_words = grouped[:, g, :].bitcast(F32).rearrange("p (n u) -> p n u", u=2)
                 for half in range(2):
-                    xt = psum_x.tile([P, 2, 2 * P], F32, tag="xt")
+                    if i in x_sorted_of and g == half == 0:
+                        xt = psum_dots.tile([P, 2, 2 * P], F32, tag="dots_ps")
+                    else:
+                        xt = psum_x.tile([P, 2, 2 * P], F32, tag="xt")
                     for c in range(2):
-                        words = x_rows_of[i][:, 2 * half + c, :].bitcast(F32)
+                        place = 2 * half + c
                         for u in range(2):
-                            nc.tensor.transpose(
-                                xt[:, u, c * P : (c + 1) * P],
-                                words[:, g * 2 * P + u : (g + 1) * 2 * P : 2],
-                                ident,
-                            )
+                            if i in x_sorted_of:
+                                words = x_sorted_of[i][:, place, g, u, :].bitcast(F32)
+                            else:
+                                words = x_rows_of[i][:, place, :].bitcast(F32)[:, g * 2 * P + u : (g + 1) * 2 * P : 2]
+                            nc.tensor.transpose(xt[:, u, c * P : (c + 1) * P], words, ident)
                     nc.scalar.copy(
                         out=grouped_words[:, half * 2 * P : (half + 1) * 2 * P, :],
                         in_=xt[:].rearrange("p u n -> p n u"),
@@ -399,25 +410,25 @@ def tile_dwarfattention_pa_t_kernel(
                 )
             window_of[n] = window
 
-        def products(t):
+        def product(t, i):
             s, step = divmod(t, STEPS)
             group, quad = divmod(step, QUADS)
-            prod = prods.tile([P, STEP_D, QUAD, PLACES], F32)
-            for i in range(QUAD):
-                first = BACK - OFFSETS[quad * QUAD + i]
-                nc.vector.tensor_tensor(
-                    out=prod[:, :, i, :],
-                    in0=q_of[STAGES[s]][:, group * STEP_D : (group + 1) * STEP_D, :],
-                    in1=window_of[t // QUADS][:, :, first : first + PLACES],
-                    op=ALU.mult,
-                )
-            prod_of[t] = prod
+            if i == 0:
+                prod = prods.tile([P, STEP_D, QUAD, PLACES], F32)
+                prod_of[t] = prod
+            first = BACK - OFFSETS[quad * QUAD + i]
+            nc.vector.tensor_tensor(
+                out=prod_of[t][:, :, i, :],
+                in0=q_of[STAGES[s]][:, group * STEP_D : (group + 1) * STEP_D, :],
+                in1=window_of[t // QUADS][:, :, first : first + PLACES],
+                op=ALU.mult,
+            )
 
         def sum_products(t):
             s, step = divmod(t, STEPS)
             quad = step % QUADS
             if step == 0:
-                dots_ps = psum_dots.tile([P, QUADS, P], F32)
+                dots_ps = psum_dots.tile([P, QUADS, P], F32, tag="dots_ps")
                 dots_ps_of[s] = dots_ps
             for d in range(STEP_D):
                 nc.tensor.matmul(
@@ -444,11 +455,15 @@ def tile_dwarfattention_pa_t_kernel(
                 out=dots_of[s][:, 0:NEAR, :], in_=back[:].rearrange("p q (i c) -> p (q i) c", c=PLACES)
             )
 
+        def mask_dots(s, near):
+            cols = slice(0, NEAR) if near else slice(NEAR, COLS)
+            dots = dots_of[s][:, cols, :]
+            nc.vector.tensor_tensor(out=dots, in0=dots, in1=reached[:, cols, :], op=ALU.mult)
+
         def scores(s, near):
             h = STAGES[s][1]
             dots = dots_of[s]
             cols = slice(0, NEAR) if near else slice(NEAR, COLS)
-            nc.vector.tensor_tensor(out=dots[:, cols, :], in0=dots[:, cols, :], in1=reached[:, cols, :], op=ALU.mult)
             if near:
                 reads = ((0, NEAR, dots[:, cols, :]), (NEAR + 1, SPLIT - 1, dots[:, 1:SPLIT, :]))
                 slots = slice(0, NEAR_SLOTS)
@@ -495,7 +510,7 @@ def tile_dwarfattention_pa_t_kernel(
             if not near:
                 nc.gpsimd.tensor_copy(out=slot_gain[:, LOCAL, :], in_=local_gain[:, h : h + 1].to_broadcast([P, PLACES]))
 
-        def shares(s, near):
+        def features(s, near):
             slots = slice(0, NEAR_SLOTS) if near else slice(NEAR_SLOTS, SLOTS)
             share, u1_read = weight_of[s][:, slots, :], u1[:, 0 : slots.stop - slots.start, :]
             nc.vector.scalar_tensor_tensor(
@@ -506,6 +521,10 @@ def tile_dwarfattention_pa_t_kernel(
                 op0=ALU.min,
                 op1=ALU.max,
             )
+
+        def shares(s, near):
+            slots = slice(0, NEAR_SLOTS) if near else slice(NEAR_SLOTS, SLOTS)
+            share = weight_of[s][:, slots, :]
             nc.vector.tensor_tensor(out=share, in0=share, in1=slot_gain[:, slots, :], op=ALU.mult)
 
         def weights(s, near):
@@ -536,14 +555,20 @@ def tile_dwarfattention_pa_t_kernel(
                 nc.vector.tensor_reduce(
                     out=z[:, at + i, :], in_=weight[:, slots, :].rearrange("p o c -> p c o"), axis=AXIS.X, op=ALU.add
                 )
+
+        def subtract_in_z(s, near):
+            z, at = z_of[s], 2 * near
             nc.vector.tensor_tensor(out=z[:, at, :], in0=z[:, at, :], in1=z[:, at + 1, :], op=ALU.subtract)
-            if near:
-                one_over_z = table.tile([P, PLACES], F32, bufs=2)
-                nc.vector.scalar_tensor_tensor(
-                    out=one_over_z[:], in0=z[:, 0, :], scalar=1e-06, in1=z[:, 2, :], op0=ALU.add, op1=ALU.add
-                )
-                nc.vector.reciprocal(out=one_over_z[:], in_=one_over_z[:])
-                one_over_z_of[s] = one_over_z
+
+        def add_up_z(s):
+            one_over_z = table.tile([P, PLACES], F32, bufs=2)
+            nc.vector.scalar_tensor_tensor(
+                out=one_over_z[:], in0=z_of[s][:, 0, :], scalar=1e-06, in1=z_of[s][:, 2, :], op0=ALU.add, op1=ALU.add
+            )
+            one_over_z_of[s] = one_over_z
+
+        def invert_z(s):
+            nc.vector.reciprocal(out=one_over_z_of[s][:], in_=one_over_z_of[s][:])
 
         def park_weights(s):
             for run in range(2):
@@ -586,10 +611,12 @@ def tile_dwarfattention_pa_t_kernel(
 
         def turn_matrix(s, half):
             matrix = phase.tile([P, HALF, P], F32, bufs=2, offset=63488)
-            nc.scalar.copy(
-                out=matrix[:].rearrange("p (g k) q -> p g q k", k=4),
-                in_=loaded_of[s, half][:].rearrange("p q (g k) -> p g q k", k=4),
-            )
+            turned_view = matrix[:].rearrange("p (g k) q -> p g q k", k=4)
+            loaded_view = loaded_of[s, half][:].rearrange("p q (g k) -> p g q k", k=4)
+            if s == len(STAGES) - 1:
+                nc.vector.tensor_copy(out=turned_view, in_=loaded_view)
+            else:
+                nc.scalar.copy(out=turned_view, in_=loaded_view)
             matrix_of[s, half] = matrix
 
         weighted_of, acc_of, acc_cols_of, fin_of, result_of = {}, {}, {}, {}, {}
@@ -702,35 +729,70 @@ def tile_dwarfattention_pa_t_kernel(
         far_rowed = tuple(col for col in ROWED if col >= NEAR)
         dot_steps = len(STAGES) * STEPS
 
-        units_at, plan = {}, {}
+        between, beside, units_at = {}, {}, {}
+
+        def vector_job(t, *work):
+            between.setdefault(t, []).append(work)
 
         def plan_at(t, *work):
-            plan.setdefault(t, []).append(work)
+            beside.setdefault(t, []).append(work)
 
         for s in range(len(STAGES)):
-            start, last = STEPS * (s + 1), s == len(STAGES) - 1
-            first = (5, 5, 7, 9, 9, 11, 13) if s == 0 else (-2, 1, 2, 3, 3, 4, 6) if last else (0 if s == 1 else -2, 2, 4, 6, 6, 8, 10)
-            plan_at(start + first[0], write_matrix, s, HALVES[0], far_rowed)
-            plan_at(start + first[1], write_matrix, s, HALVES[0], near_rowed)
-            plan_at(start + first[2], read_matrix, s, HALVES[0])
-            plan_at(start + first[3], turn_matrix, s, HALVES[0])
-            plan_at(start + first[4], write_matrix, s, HALVES[1], ROWED)
-            plan_at(start + first[5], read_matrix, s, HALVES[1])
-            plan_at(start + first[6], turn_matrix, s, HALVES[1])
+            begin, start, last = STEPS * s, STEPS * (s + 1), s == len(STAGES) - 1
+            f = begin + 5
+            vector_job(f, mask_dots, s, False)
+            vector_job(f, scores, s, False)
+            plan_at(f, exponentials, s, False)
+            for work in (features, shares, weights, add_to_z):
+                vector_job(f + 1, work, s, False)
+            vector_job(f + 2, subtract_in_z, s, False)
+            if not last:
+                plan_at(f + 2, gains_of_slots, s + 1, False)
+            if not last:
+                plan_at(start, dots_out, s)
+                plan_at(start, dots_back, s)
+                n = start + 2
+                for work in (mask_dots, scores):
+                    vector_job(n, work, s, True)
+                plan_at(n, exponentials, s, True)
+                for work in (features, shares, weights):
+                    vector_job(n + 1, work, s, True)
+                plan_at(n + 1, park_weights, s)
+                plan_at(n + 1, gains_of_slots, s + 1, True)
+                for work in (add_to_z, subtract_in_z):
+                    vector_job(n + 2, work, s, True)
+                for work in (add_up_z, invert_z):
+                    vector_job(n + 2, work, s)
+            far_at, near_at, read_at, turn_at, write_at, read_too_at, turn_too_at = (
+                (6, 6, 8, 10, 9, 11, 13) if s == 0 else (-2, 1, 2, 3, 3, 4, 6) if last else (0 if s == 1 else -2, 3, 5, 7, 7, 9, 11)
+            )
+            plan_at(start + far_at, write_matrix, s, HALVES[0], far_rowed)
+            plan_at(start + near_at, write_matrix, s, HALVES[0], near_rowed)
+            plan_at(start + (2 if last else 5), move_weights, s)
+            plan_at(start + read_at, read_matrix, s, HALVES[0])
+            plan_at(start + turn_at, turn_matrix, s, HALVES[0])
+            plan_at(start + write_at, write_matrix, s, HALVES[1], ROWED)
+            plan_at(start + read_too_at, read_matrix, s, HALVES[1])
+            plan_at(start + turn_too_at, turn_matrix, s, HALVES[1])
             units = [(half, k) for half in HALVES for k in range(len(MIX_ORDER))]
             for n, (half, k) in enumerate(units):
-                t = start + ((1 + n * 8 // len(units)) if last else (3 + n * 9 // len(units)))
+                if last:
+                    t = start + 2 + n * 8 // len(units)
+                elif s < len(STAGES) - 2 or n < 14:
+                    t = start + 4 + n * 8 // len(units)
+                else:
+                    t = start + STEPS + (n - 14) // 2
                 units_at.setdefault(t, []).append((s, half, k))
                 if k == len(MIX_ORDER) - 1:
                     mixed = t + (3 if last else 2)
-                    far_from, far_steps = ((10, 3) if half == HALVES[0] else (14, 3)) if s == 0 else ((4, 4) if half == HALVES[0] else (8, 4)) if last else ((8, 3) if half == HALVES[0] else (11, 3))
+                    far_from, far_steps = ((11, 3) if half == HALVES[0] else (15, 3)) if s == 0 else ((4, 4) if half == HALVES[0] else (9, 4)) if last else ((9, 2) if half == HALVES[0] else (13, 2)) if s == 2 else ((9, 2) if half == HALVES[0] else (12, 3))
                     for i in range(HALF):
                         plan_at(start + far_from + i * far_steps // HALF, mix_far, s, half, i)
                     done = max(mixed + 1, start + far_from + far_steps)
                     plan_at(mixed, mix_out, s, half)
                     plan_at(done, mix_back, s, half)
-                    plan_at(done, finish, s, half)
-        end = max(plan) + 1
+                    vector_job(done + 1, finish, s, half)
+        end = max(max(beside), max(between)) + 1
 
         def project(i, part, early):
             if part == 0:
@@ -738,6 +800,8 @@ def tile_dwarfattention_pa_t_kernel(
                     transpose_x(i + 2)
                     if i + 4 <= last_chunk:
                         load_x(i + 4)
+                        if early and i + 4 <= 10:
+                            sort_x(i + 4)
                 if early and i > 0:
                     keep_rows(i - 1)
                 if 0 <= i - 1 <= last_chunk:
@@ -753,10 +817,17 @@ def tile_dwarfattention_pa_t_kernel(
                 keep_columns(i, early)
 
         with tc.manual_schedule():
+            for i in range(2):
+                if 10 > 0:
+                    sort_x(i)
             transpose_x(0)
             load_x(2)
+            if 10 > 0:
+                sort_x(2)
             transpose_x(1)
             load_x(3)
+            if 10 > 0:
+                sort_x(3)
             quantise_x(0)
             turn_bias()
             for i in range(CHUNKS + HEAD):
@@ -778,86 +849,75 @@ def tile_dwarfattention_pa_t_kernel(
 
             next_chunk = CHUNKS + HEAD
             for t in range(end):
-                s, step = divmod(t, STEPS)
-                before = s - 1
-                mixing = 0 <= before < len(STAGES)
-                projecting = t % 3 != 2 and next_chunk <= last_chunk + 1
+                projecting = t % 2 == 0 and next_chunk <= last_chunk + 1
                 if projecting:
                     project(next_chunk, 0, False)
-                if t < dot_steps and step % QUADS == 0 and t // QUADS + 1 < dot_steps // QUADS:
+                if t < dot_steps and t % QUADS == 0 and t // QUADS + 1 < dot_steps // QUADS:
                     load_window(t // QUADS + 1)
                 if t == 1:
                     for odd in range(2):
                         fetch_far_dots(0, 1, odd)
-                elif t == 5:
+                elif t == 6:
                     store_far_dots(1, 0)
-                elif t == 5 + 1:
+                elif t == 6 + 1:
                     for odd in range(2):
                         fetch_far_dots(1, 0, odd)
-                elif t == STEPS:
-                    store_far_dots(1, 1)
                 elif t == STEPS + 2:
+                    store_far_dots(1, 1)
+                elif t == STEPS + 2 + 2:
                     for odd in range(2):
                         fetch_far_dots(1, 1, odd)
-                elif t == STEPS + 3:
+                elif t == STEPS + 2 + 3:
                     clear_matrix(32)
-                elif t == STEPS + 5:
+                elif t == STEPS + 7:
                     park_k(1, 0)
                 elif t == 2 * STEPS - 2:
                     park_k(1, 1)
+                jobs = between.get(t, [])
                 if t < dot_steps:
-                    products(t)
+                    for i in range(QUAD):
+                        product(t, i)
+                        for work in jobs[i : i + 1] if i < QUAD - 1 else jobs[i:]:
+                            work[0](*work[1:])
+                elif t > dot_steps:
+                    for work in jobs:
+                        work[0](*work[1:])
                 if projecting:
                     project(next_chunk, 1, False)
-                if mixing and step == 1 and t < dot_steps:
-                    scores(before, True)
-                elif mixing and step == 1 + 1 and t < dot_steps:
-                    shares(before, True)
-                    weights(before, True)
-                    park_weights(before)
-                    add_to_z(before, True)
-                    if s < len(STAGES):
-                        gains_of_slots(s, True)
                 if 1 <= t <= dot_steps:
                     sum_products(t - 1)
                 if projecting:
                     project(next_chunk, 2, False)
                     next_chunk += 1
                 if t == dot_steps:
-                    dots_out(before)
-                    dots_back(before)
-                    scores(before, True)
-                    exponentials(before, True)
-                    shares(before, True)
-                    weights(before, True)
-                    park_weights(before)
-                if s < len(STAGES):
-                    if step == 7:
-                        scores(s, False)
-                    elif step == 8:
-                        shares(s, False)
-                        if s + 1 < len(STAGES):
-                            gains_of_slots(s + 1, False)
-                        weights(s, False)
-                        add_to_z(s, False)
-                if mixing:
-                    if step == 4:
-                        move_weights(before)
-                for work in plan.get(t, ()):
-                    work[0](*work[1:])
-                for unit in units_at.get(t - 1, ()):
-                    sum_weighted(*unit)
+                    for work in jobs:
+                        work[0](*work[1:])
+                    s = len(STAGES) - 1
+                    dots_out(s)
+                    dots_back(s)
+                    mask_dots(s, True)
+                    scores(s, True)
+                    exponentials(s, True)
+                    features(s, True)
+                    shares(s, True)
+                    weights(s, True)
+                    park_weights(s)
+                elif t == dot_steps + 2:
+                    add_to_z(s, True)
+                    subtract_in_z(s, True)
+                    add_up_z(s)
+                    invert_z(s)
+                late = [work for work in beside.get(t, ()) if work[0] in (exponentials, dots_out, dots_back)]
+                for work in beside.get(t, ()):
+                    if work not in late:
+                        work[0](*work[1:])
+                for when in range(dot_steps - 3, dot_steps) if t == dot_steps else () if dot_steps - 3 < t < dot_steps else (t - 1,):
+                    for unit in units_at.get(when, ()):
+                        sum_weighted(*unit)
                 for unit in units_at.get(t, ()):
-                    weigh(*unit, 0 if t < dot_steps else 8)
-                if mixing and step == 0 and t < dot_steps:
-                    dots_out(before)
-                    dots_back(before)
-                elif mixing and step == 1 and t < dot_steps:
-                    exponentials(before, True)
-                elif s < len(STAGES) and step == 7:
-                    exponentials(s, False)
-                if t == dot_steps + 2:
-                    add_to_z(before, True)
+                    weigh(*unit, 0 if t < dot_steps else 6)
+                for work in late:
+                    work[0](*work[1:])
                 if t == dot_steps + STEPS - 1:
                     for done in range(3):
                         for half in HALVES:

@@ -428,7 +428,7 @@ def tile_dwarfattention_pa_t_kernel(
             s, step = divmod(t, STEPS)
             quad = step % QUADS
             if step == 0:
-                dots_ps = psum_dots.tile([P, QUADS, P], F32, tag="dots_ps")
+                dots_ps = psum_dots.tile([P, QUADS + 1, P], F32, tag="dots_ps")
                 dots_ps_of[s] = dots_ps
             for d in range(STEP_D):
                 nc.tensor.matmul(
@@ -440,11 +440,26 @@ def tile_dwarfattention_pa_t_kernel(
                     is_transpose=True,
                 )
 
+        def wake(s, count):
+            if s < len(STAGES):
+                target, alone = dots_ps_of[s], False
+            else:
+                idle = psum_dots.tile([P, QUADS + 1, P], F32, tag="dots_ps")
+                target, alone = idle, True
+            for i in range(count):
+                nc.tensor.matmul(
+                    out=target[:, QUADS, 0:HD],
+                    lhsT=ident,
+                    rhs=ident_twice[:, 0:HD],
+                    start=(alone and i == 0),
+                    stop=(alone and i == count - 1),
+                )
+
         turned_of, weight_of, moved_weight_of, z_of, one_over_z_of = {}, {}, {}, {}, {}
 
         def dots_out(s):
             turned = table.tile([P, QUADS, P], F32)
-            nc.scalar.copy(out=turned[:], in_=dots_ps_of[s][:])
+            nc.scalar.copy(out=turned[:], in_=dots_ps_of[s][:, 0:QUADS, :])
             turned_of[s] = turned
 
         def dots_back(s):
@@ -692,29 +707,28 @@ def tile_dwarfattention_pa_t_kernel(
                 stop=False,
             )
 
-        def mix_back(s, half):
-            for cell in range(CELLS):
+        def mix_back(s, half, bank):
+            for cell in range(4):
                 nc.tensor.matmul(
-                    fin_of[s, half, cell // 4][:, cell % 4, :],
-                    lhsT=acc_cols_of[s, half][:, cell, :],
+                    fin_of[s, half, bank][:, cell, :],
+                    lhsT=acc_cols_of[s, half][:, 4 * bank + cell, :],
                     rhs=ident,
                     start=False,
-                    stop=(cell % 4 == 3),
+                    stop=(cell == 3),
                     is_transpose=True,
                 )
 
-        def finish(s, half):
-            if half == HALVES[0]:
+        def finish(s, half, bank):
+            if s not in result_of:
                 result = qkv.tile([P, PLACES, HD], F32, tag="q", bufs=4)
                 result_of[s] = result
-            for bank in range(CELLS // 4):
-                places = slice(half * HALF + 8 * bank, half * HALF + 8 * bank + 8)
-                nc.vector.tensor_tensor(
-                    out=result_of[s][:, places, :],
-                    in0=fin_of[s, half, bank][:].rearrange("p k (c d) -> p (k c) d", d=HD),
-                    in1=one_over_z_of[s][:, places].unsqueeze(2).to_broadcast([P, 8, HD]),
-                    op=ALU.mult,
-                )
+            places = slice(half * HALF + 8 * bank, half * HALF + 8 * bank + 8)
+            nc.vector.tensor_tensor(
+                out=result_of[s][:, places, :],
+                in0=fin_of[s, half, bank][:].rearrange("p k (c d) -> p (k c) d", d=HD),
+                in1=one_over_z_of[s][:, places].unsqueeze(2).to_broadcast([P, 8, HD]),
+                op=ALU.mult,
+            )
 
         def store(s, half):
             b, h = STAGES[s]
@@ -785,14 +799,16 @@ def tile_dwarfattention_pa_t_kernel(
                 units_at.setdefault(t, []).append((s, half, k))
                 if k == len(MIX_ORDER) - 1:
                     mixed = t + (3 if last else 2)
-                    far_from, far_steps = ((11, 3) if half == HALVES[0] else (15, 3)) if s == 0 else ((4, 4) if half == HALVES[0] else (9, 4)) if last else ((9, 2) if half == HALVES[0] else (13, 2)) if s == 2 else ((9, 2) if half == HALVES[0] else (12, 3))
-                    for i in range(HALF):
-                        plan_at(start + far_from + i * far_steps // HALF, mix_far, s, half, i)
-                    done = max(mixed + 1, start + far_from + far_steps)
                     plan_at(mixed, mix_out, s, half)
-                    plan_at(done, mix_back, s, half)
-                    vector_job(done + 1, finish, s, half)
+                    for bank in range(2):
+                        far_from, far_steps = (((4, 2), (6, 2), (9, 2), (11, 2)) if last else ((11, 2), (13, 2), (15, 3), (18, 3)) if s == 0 else ((9, 1), (10, 1), (13, 1), (14, 1)) if s == 2 else ((9, 3), (12, 3), (15, 3), (18, 3)))[(half != HALVES[0]) * 2 + bank]
+                        for i in range(8):
+                            plan_at(start + far_from + i * far_steps // 8, mix_far, s, half, 8 * bank + i)
+                        done = max(mixed + 1, start + far_from + far_steps)
+                        plan_at(done, mix_back, s, half, bank)
+                        vector_job(done + 1, finish, s, half, bank)
         end = max(max(beside), max(between)) + 1
+        wakes = {STEPS * s + n: 6 for s in (1, 2, 3) for n in (4, 6)}
 
         def project(i, part, early):
             if part == 0:
@@ -820,6 +836,7 @@ def tile_dwarfattention_pa_t_kernel(
             for i in range(2):
                 if 10 > 0:
                     sort_x(i)
+            wake(len(STAGES), 6)
             transpose_x(0)
             load_x(2)
             if 10 > 0:
@@ -886,6 +903,8 @@ def tile_dwarfattention_pa_t_kernel(
                     project(next_chunk, 1, False)
                 if 1 <= t <= dot_steps:
                     sum_products(t - 1)
+                if t in wakes:
+                    wake(t // STEPS, wakes[t])
                 if projecting:
                     project(next_chunk, 2, False)
                     next_chunk += 1

@@ -68,10 +68,12 @@ HALF = PLACES // 2
 CELLS = HALF // 2
 
 S_ROW = 2 * IN_CLASS * HALF
+S_PITCH = S_ROW + HALF
 S_AT = 0
 W_ROW = P * HALF
 W_AT = max(OFFSETS) // PLACES * W_ROW
 K_AT = W_AT + P * W_ROW
+W_TOO_AT = K_AT + HD * N
 PARK_AT = K_AT + H * HD * N
 PARK_ROW = len(SHIFTED) * PLACES
 PARK_PAD = 2
@@ -214,8 +216,8 @@ def tile_dwarfattention_pa_t_kernel(
             return zeros
 
         zeros = zeros_tile()
-        for part in range(4):
-            nc.sync.dma_start(out=rows_of(W_AT + part * P * W_ROW // 4, P, W_ROW // 4), in_=zeros[:])
+        for at in range(0, K_AT, P * W_ROW // 4):
+            nc.sync.dma_start(out=rows_of(at, P, W_ROW // 4), in_=zeros[:])
         nc.sync.dma_start(out=rows_of(PARK_AT + P * PARK_ROW, PARK_PAD, PARK_ROW), in_=zeros[0:PARK_PAD, 0:PARK_ROW])
 
         q_of, v_of, v_tile_of, k_t_of, k_chunk_of, s_ps_of, s_of = {}, {}, {}, {}, {}, {}, {}
@@ -372,20 +374,21 @@ def tile_dwarfattention_pa_t_kernel(
         dots_of = {}
 
         def store_far_dots(b, group):
-            nc.sync.dma_start(out=rows_of(S_AT, P, S_ROW), in_=s_of[b, group][:].rearrange("p s k c -> p (s k c)"))
+            nc.sync.dma_start(
+                out=rows_of(S_AT, P, S_PITCH)[:, 0:S_ROW], in_=s_of[b, group][:].rearrange("p s k c -> p (s k c)")
+            )
 
-        def fetch_far_dots(b, group, odd):
+        def fetch_far_dots(b, group):
             for h in range(H):
-                if group == 0 and odd == 0:
+                if group == 0:
                     dots = table.tile([P, COLS, PLACES], F32, bufs=4)
                     dots_of[2 * b + h] = dots
-                at = S_AT + h * IN_CLASS * S_ROW + odd * S_ROW // 2 + (IN_CLASS - 1) * HALF
-                rows = rows_of(at, IN_CLASS, S_ROW - HALF)
+                rows = rows_of(S_AT + h * IN_CLASS * S_PITCH + (IN_CLASS - 1) * HALF, P, S_ROW // 2)
                 for col, count in FAR_RUNS:
                     start = OFFSETS[col] // CLASS * HALF
                     step = HALF if count == 1 else start
                     nc.sync.dma_start(
-                        out=dots_of[2 * b + h][odd:P:2, col : col + count, group * HALF : (group + 1) * HALF],
+                        out=dots_of[2 * b + h][:, col : col + count, group * HALF : (group + 1) * HALF],
                         in_=rows[:, start : start + count * step].rearrange("r (g k) -> r g k", k=step)[:, :, 0:HALF],
                     )
 
@@ -428,7 +431,7 @@ def tile_dwarfattention_pa_t_kernel(
             s, step = divmod(t, STEPS)
             quad = step % QUADS
             if step == 0:
-                dots_ps = psum_dots.tile([P, QUADS + 1, P], F32, tag="dots_ps")
+                dots_ps = psum_dots.tile([P, QUADS, P], F32, tag="dots_ps")
                 dots_ps_of[s] = dots_ps
             for d in range(STEP_D):
                 nc.tensor.matmul(
@@ -440,26 +443,12 @@ def tile_dwarfattention_pa_t_kernel(
                     is_transpose=True,
                 )
 
-        def wake(s, count):
-            if s < len(STAGES):
-                target, alone = dots_ps_of[s], False
-            else:
-                idle = psum_dots.tile([P, QUADS + 1, P], F32, tag="dots_ps")
-                target, alone = idle, True
-            for i in range(count):
-                nc.tensor.matmul(
-                    out=target[:, QUADS, 0:HD],
-                    lhsT=ident,
-                    rhs=ident_twice[:, 0:HD],
-                    start=(alone and i == 0),
-                    stop=(alone and i == count - 1),
-                )
 
         turned_of, weight_of, moved_weight_of, z_of, one_over_z_of = {}, {}, {}, {}, {}
 
         def dots_out(s):
             turned = table.tile([P, QUADS, P], F32)
-            nc.scalar.copy(out=turned[:], in_=dots_ps_of[s][:, 0:QUADS, :])
+            nc.scalar.copy(out=turned[:], in_=dots_ps_of[s][:])
             turned_of[s] = turned
 
         def dots_back(s):
@@ -606,22 +595,30 @@ def tile_dwarfattention_pa_t_kernel(
 
         loaded_of, matrix_of = {}, {}
 
-        def clear_matrix(rows):
+        def matrix_at(s, half):
+            return W_TOO_AT if s == len(STAGES) - 1 and half == HALVES[1] else W_AT
+
+        def clear_matrix(at, rows):
             zeros = zeros_tile()
             for part in range(0, rows, 32):
-                nc.sync.dma_start(out=rows_of(W_AT + part * W_ROW, P, W_ROW // 4), in_=zeros[:])
+                nc.sync.dma_start(out=rows_of(at + part * W_ROW, P, W_ROW // 4), in_=zeros[:])
 
         def write_matrix(s, half, columns):
             for col in columns:
-                at = W_AT - OFFSETS[col] // PLACES * W_ROW
+                at = matrix_at(s, half) - OFFSETS[col] // PLACES * W_ROW
                 nc.sync.dma_start(
                     out=rows_of(at, P, W_ROW + HALF)[:, 0:HALF],
                     in_=weight_of[s][:, slot_of(col), half * HALF : (half + 1) * HALF],
                 )
 
         def read_matrix(s, half):
-            loaded = phase.tile([P, P, HALF], F32, offset=35840)
-            nc.sync.dma_start(out=loaded[:].rearrange("p q c -> p (q c)"), in_=rows_of(W_AT, P, W_ROW))
+            if matrix_at(s, half) == W_AT:
+                loaded = phase.tile([P, P, HALF], F32, offset=35840)
+            else:
+                loaded = phase.tile([P, P, HALF], F32, tag="loaded_too", offset=47104)
+            nc.sync.dma_start(
+                out=loaded[:].rearrange("p q c -> p (q c)"), in_=rows_of(matrix_at(s, half), P, W_ROW)
+            )
             loaded_of[s, half] = loaded
 
         def turn_matrix(s, half):
@@ -778,14 +775,17 @@ def tile_dwarfattention_pa_t_kernel(
                 for work in (add_up_z, invert_z):
                     vector_job(n + 2, work, s)
             far_at, near_at, read_at, turn_at, write_at, read_too_at, turn_too_at = (
-                (6, 6, 8, 10, 9, 11, 13) if s == 0 else (-2, 1, 2, 3, 3, 4, 6) if last else (0 if s == 1 else -2, 3, 5, 7, 7, 9, 11)
+                (6, 6, 8, 10, 9, 11, 13) if s == 0 else (-2, 1, 2, 3, 1, 2, 5) if last else (0 if s == 1 else -2, 3, 5, 7, 7, 9, 11)
             )
             plan_at(start + far_at, write_matrix, s, HALVES[0], far_rowed)
+            if last:
+                plan_at(start + far_at, clear_matrix, W_TOO_AT, P)
+                plan_at(start + far_at + 1, write_matrix, s, HALVES[1], far_rowed)
             plan_at(start + near_at, write_matrix, s, HALVES[0], near_rowed)
             plan_at(start + (2 if last else 5), move_weights, s)
             plan_at(start + read_at, read_matrix, s, HALVES[0])
             plan_at(start + turn_at, turn_matrix, s, HALVES[0])
-            plan_at(start + write_at, write_matrix, s, HALVES[1], ROWED)
+            plan_at(start + write_at, write_matrix, s, HALVES[1], near_rowed if last else ROWED)
             plan_at(start + read_too_at, read_matrix, s, HALVES[1])
             plan_at(start + turn_too_at, turn_matrix, s, HALVES[1])
             units = [(half, k) for half in HALVES for k in range(len(MIX_ORDER))]
@@ -808,7 +808,6 @@ def tile_dwarfattention_pa_t_kernel(
                         plan_at(done, mix_back, s, half, bank)
                         vector_job(done + 1, finish, s, half, bank)
         end = max(max(beside), max(between)) + 1
-        wakes = {STEPS * s + n: 6 for s in (1, 2, 3) for n in (4, 6)}
 
         def project(i, part, early):
             if part == 0:
@@ -836,7 +835,6 @@ def tile_dwarfattention_pa_t_kernel(
             for i in range(2):
                 if 10 > 0:
                     sort_x(i)
-            wake(len(STAGES), 6)
             transpose_x(0)
             load_x(2)
             if 10 > 0:
@@ -853,8 +851,7 @@ def tile_dwarfattention_pa_t_kernel(
                 if i == CHUNKS // 2:
                     store_far_dots(0, 0)
                 elif i == CHUNKS // 2 + 1:
-                    for odd in range(2):
-                        fetch_far_dots(0, 0, odd)
+                    fetch_far_dots(0, 0)
                 elif i == CHUNKS - 1:
                     park_k(0, 0)
                     park_k(0, 1)
@@ -872,20 +869,17 @@ def tile_dwarfattention_pa_t_kernel(
                 if t < dot_steps and t % QUADS == 0 and t // QUADS + 1 < dot_steps // QUADS:
                     load_window(t // QUADS + 1)
                 if t == 1:
-                    for odd in range(2):
-                        fetch_far_dots(0, 1, odd)
+                    fetch_far_dots(0, 1)
                 elif t == 6:
                     store_far_dots(1, 0)
                 elif t == 6 + 1:
-                    for odd in range(2):
-                        fetch_far_dots(1, 0, odd)
+                    fetch_far_dots(1, 0)
                 elif t == STEPS + 2:
                     store_far_dots(1, 1)
                 elif t == STEPS + 2 + 2:
-                    for odd in range(2):
-                        fetch_far_dots(1, 1, odd)
+                    fetch_far_dots(1, 1)
                 elif t == STEPS + 2 + 3:
-                    clear_matrix(32)
+                    clear_matrix(W_AT, 64)
                 elif t == STEPS + 7:
                     park_k(1, 0)
                 elif t == 2 * STEPS - 2:
@@ -903,8 +897,6 @@ def tile_dwarfattention_pa_t_kernel(
                     project(next_chunk, 1, False)
                 if 1 <= t <= dot_steps:
                     sum_products(t - 1)
-                if t in wakes:
-                    wake(t // STEPS, wakes[t])
                 if projecting:
                     project(next_chunk, 2, False)
                     next_chunk += 1

@@ -41,17 +41,19 @@ CLASS = 64
 IN_CLASS = N // CLASS
 ROWED = tuple(c for c in range(COLS) if OFFSETS[c] % PLACES == 0)
 SHIFTED = tuple(c for c in range(COLS) if OFFSETS[c] % PLACES != 0)
-NEAR_SLOTS = 3 * SPLIT
-SLOTS = 2 * COLS
-NEAR_TAPS = ((1, 0, SPLIT, 0), (3, 0, SPLIT, SPLIT), (2, 0, SPLIT - 1, NEAR + 1))
+NEAR_TAPS = ((1, 0, SPLIT, 0), (3, 0, SPLIT, SPLIT), (2, 0, SPLIT - 1, NEAR))
+NEAR_SLOTS = NEAR + SPLIT - 1
+FAR_ZERO = NEAR_SLOTS + ZERO - NEAR
+FAR_MORE = NEAR_SLOTS + COLS - NEAR
 FAR_TAPS = (
     (1, SPLIT, S, NEAR_SLOTS),
-    (3, SPLIT, S, NEAR_SLOTS + ZERO - NEAR + 1),
-    (2, SPLIT - 1, S, NEAR_SLOTS + COLS - NEAR),
-    (0, 0, S, SLOTS - S - 1),
+    (2, S - 1, S, FAR_ZERO - 1),
+    (3, SPLIT, S, FAR_ZERO + 1),
+    (2, SPLIT - 1, S - 1, FAR_MORE),
+    (0, 0, S, FAR_MORE + SPLIT - 1),
 )
-LOCAL = SLOTS - 1
-FAR_ZERO = NEAR_SLOTS + ZERO - NEAR
+LOCAL = FAR_MORE + SPLIT - 1 + S
+SLOTS = LOCAL + 1
 
 
 def slot_of(col):
@@ -137,6 +139,8 @@ def tile_dwarfattention_pa_t_kernel(
         make_identity(nc, ident_twice[:, 0:P])
         make_identity(nc, ident_twice[:, P : 2 * P])
         ident = ident_twice[:, 0:P]
+        move_by_one = const.tile([P, P], F32)
+        nc.vector.tensor_copy(out=move_by_one[:], in_=ident_twice[:, P - 1 : 2 * P - 1])
         one_col = const.tile([P, 1], F32)
         nc.vector.memset(one_col[:], 1.0)
         minus_one_col = const.tile([P, 1], F32)
@@ -180,13 +184,13 @@ def tile_dwarfattention_pa_t_kernel(
             out=local_gain[:], in0=bypass[:], scalar=0.0, in1=bypass_tail[:], op0=ALU.max, op1=ALU.add
         )
 
-        gains_in = const.tile([P, B, H, PLACES, S], BF16)
+        gains_in = phase.tile([P, B, H, PLACES, S], BF16, offset=65536)
         for b, h in STAGES:
             nc.sync.dma_start(out=gains_in[:, b, h, :, :], in_=gains[b, h].rearrange("(p c) j -> p c j", c=PLACES))
-        slot_gain = const.tile([P, SLOTS, PLACES], F32)
-        nc.gpsimd.memset(slot_gain[:], 0.0)
+        gain = const.tile([P, B, H, S, PLACES], BF16)
+        for b, h in STAGES:
+            nc.vector.tensor_copy(out=gain[:, b, h], in_=gains_in[:, b, h].rearrange("p c j -> p j c"))
         u1 = const.tile([P, SLOTS - NEAR_SLOTS, PLACES], F32)
-        nc.gpsimd.memset(u1[:], 0.0)
 
         token = const.tile([P, PLACES], F32)
         nc.gpsimd.iota(
@@ -216,8 +220,6 @@ def tile_dwarfattention_pa_t_kernel(
             return zeros
 
         zeros = zeros_tile()
-        for at in range(0, K_AT, P * W_ROW // 4):
-            nc.sync.dma_start(out=rows_of(at, P, W_ROW // 4), in_=zeros[:])
         nc.sync.dma_start(out=rows_of(PARK_AT + P * PARK_ROW, PARK_PAD, PARK_ROW), in_=zeros[0:PARK_PAD, 0:PARK_ROW])
 
         q_of, v_of, v_tile_of, k_t_of, k_chunk_of, s_ps_of, s_of = {}, {}, {}, {}, {}, {}, {}
@@ -469,14 +471,13 @@ def tile_dwarfattention_pa_t_kernel(
             dots = dots_of[s]
             cols = slice(0, NEAR) if near else slice(NEAR, COLS)
             if near:
-                reads = ((0, NEAR, dots[:, cols, :]), (NEAR + 1, SPLIT - 1, dots[:, 1:SPLIT, :]))
+                reads = ((0, NEAR, dots[:, cols, :]), (NEAR, SPLIT - 1, dots[:, 1:SPLIT, :]))
                 slots = slice(0, NEAR_SLOTS)
             else:
-                at = NEAR_SLOTS + COLS - NEAR
                 reads = (
                     (NEAR_SLOTS, COLS - NEAR, dots[:, cols, :]),
-                    (at, SPLIT, dots[:, NEAR : NEAR + SPLIT, :]),
-                    (at + SPLIT, S + 1, dots[:, ZERO : ZERO + 1, :].to_broadcast([P, S + 1, PLACES])),
+                    (FAR_MORE, SPLIT - 1, dots[:, NEAR : NEAR + SPLIT - 1, :]),
+                    (FAR_MORE + SPLIT - 1, S + 1, dots[:, ZERO : ZERO + 1, :].to_broadcast([P, S + 1, PLACES])),
                 )
                 slots = slice(NEAR_SLOTS, SLOTS)
                 weight = table.tile([P, SLOTS, PLACES], F32, bufs=2)
@@ -500,20 +501,6 @@ def tile_dwarfattention_pa_t_kernel(
                 bias=minus_one_col[:, 0:1],
             )
 
-        def gains_of_slots(s, near):
-            b, h = STAGES[s]
-            for tau, first, last, at in NEAR_TAPS if near else FAR_TAPS:
-                nc.gpsimd.tensor_scalar(
-                    out=slot_gain[:, at : at + last - first, :],
-                    in0=gains_in[:, b, h, :, first:last].rearrange("p c j -> p j c"),
-                    scalar1=D4[tau],
-                    scalar2=0.0,
-                    op0=ALU.mult,
-                    op1=ALU.add,
-                )
-            if not near:
-                nc.gpsimd.tensor_copy(out=slot_gain[:, LOCAL, :], in_=local_gain[:, h : h + 1].to_broadcast([P, PLACES]))
-
         def features(s, near):
             slots = slice(0, NEAR_SLOTS) if near else slice(NEAR_SLOTS, SLOTS)
             share, u1_read = weight_of[s][:, slots, :], u1[:, 0 : slots.stop - slots.start, :]
@@ -527,23 +514,34 @@ def tile_dwarfattention_pa_t_kernel(
             )
 
         def shares(s, near):
-            slots = slice(0, NEAR_SLOTS) if near else slice(NEAR_SLOTS, SLOTS)
-            share = weight_of[s][:, slots, :]
-            nc.vector.tensor_tensor(out=share, in0=share, in1=slot_gain[:, slots, :], op=ALU.mult)
+            b, h = STAGES[s]
+            weight = weight_of[s]
+            for tau, first, last, at in NEAR_TAPS if near else FAR_TAPS:
+                share = weight[:, at : at + last - first, :].rearrange("p s c -> p (s c)")
+                nc.vector.scalar_tensor_tensor(
+                    out=share,
+                    in0=share,
+                    scalar=D4[tau],
+                    in1=gain[:, b, h, first:last, :].rearrange("p s c -> p (s c)"),
+                    op0=ALU.mult,
+                    op1=ALU.mult,
+                )
+            if not near:
+                nc.vector.tensor_scalar_mul(out=weight[:, LOCAL, :], in0=weight[:, LOCAL, :], scalar1=local_gain[:, h : h + 1])
 
         def weights(s, near):
             weight = weight_of[s]
-            at, more = (0, NEAR) if near else (NEAR_SLOTS, NEAR_SLOTS + COLS - NEAR)
+            at, more = (1, NEAR) if near else (NEAR_SLOTS, FAR_MORE)
             nc.vector.tensor_tensor(
-                out=weight[:, at : at + SPLIT, :],
-                in0=weight[:, at : at + SPLIT, :],
-                in1=weight[:, more : more + SPLIT, :],
+                out=weight[:, at : at + SPLIT - 1, :],
+                in0=weight[:, at : at + SPLIT - 1, :],
+                in1=weight[:, more : more + SPLIT - 1, :],
                 op=ALU.add,
             )
             if not near:
                 nc.vector.tensor_reduce(
                     out=weight[:, FAR_ZERO, :],
-                    in_=weight[:, more + SPLIT : SLOTS, :].rearrange("p s c -> p c s"),
+                    in_=weight[:, FAR_MORE + SPLIT - 1 : SLOTS, :].rearrange("p s c -> p c s"),
                     axis=AXIS.X,
                     op=ALU.add,
                 )
@@ -553,7 +551,7 @@ def tile_dwarfattention_pa_t_kernel(
             if near:
                 runs = (slice(0, SPLIT), slice(SPLIT, NEAR))
             else:
-                runs = (slice(NEAR_SLOTS, FAR_ZERO + 1), slice(FAR_ZERO + 1, NEAR_SLOTS + COLS - NEAR))
+                runs = (slice(NEAR_SLOTS, FAR_ZERO + 1), slice(FAR_ZERO + 1, FAR_MORE))
             at = 2 * near
             for i, slots in enumerate(runs):
                 nc.vector.tensor_reduce(
@@ -598,8 +596,7 @@ def tile_dwarfattention_pa_t_kernel(
         def matrix_at(s, half):
             return W_TOO_AT if s == len(STAGES) - 1 and half == HALVES[1] else W_AT
 
-        def clear_matrix(at, rows):
-            zeros = zeros_tile()
+        def clear_matrix(at, rows, zeros):
             for part in range(0, rows, 32):
                 nc.sync.dma_start(out=rows_of(at + part * W_ROW, P, W_ROW // 4), in_=zeros[:])
 
@@ -678,7 +675,7 @@ def tile_dwarfattention_pa_t_kernel(
                 nc.tensor.matmul(
                     acc_of[s, half, cell // 4][:, cell % 4, :],
                     lhsT=weighted_of[s, half, k][:, slot : slot + 2, :].rearrange("p c d -> p (c d)"),
-                    rhs=ident_twice[:, P - move : 2 * P - move],
+                    rhs=move_by_one[:] if move == 1 else ident_twice[:, P - move : 2 * P - move],
                     start=(opens and cell % 4 == 0),
                     stop=(closes and cell % 4 == 3),
                     is_transpose=True,
@@ -748,6 +745,9 @@ def tile_dwarfattention_pa_t_kernel(
         def plan_at(t, *work):
             beside.setdefault(t, []).append(work)
 
+        def clear_late():
+            clear_matrix(W_TOO_AT, P, zeros_tile())
+
         for s in range(len(STAGES)):
             begin, start, last = STEPS * s, STEPS * (s + 1), s == len(STAGES) - 1
             f = begin + 5
@@ -758,8 +758,6 @@ def tile_dwarfattention_pa_t_kernel(
                 vector_job(f + 1, work, s, False)
             vector_job(f + 2, subtract_in_z, s, False)
             if not last:
-                plan_at(f + 2, gains_of_slots, s + 1, False)
-            if not last:
                 plan_at(start, dots_out, s)
                 plan_at(start, dots_back, s)
                 n = start + 2
@@ -769,7 +767,6 @@ def tile_dwarfattention_pa_t_kernel(
                 for work in (features, shares, weights):
                     vector_job(n + 1, work, s, True)
                 plan_at(n + 1, park_weights, s)
-                plan_at(n + 1, gains_of_slots, s + 1, True)
                 for work in (add_to_z, subtract_in_z):
                     vector_job(n + 2, work, s, True)
                 for work in (add_up_z, invert_z):
@@ -779,7 +776,7 @@ def tile_dwarfattention_pa_t_kernel(
             )
             plan_at(start + far_at, write_matrix, s, HALVES[0], far_rowed)
             if last:
-                plan_at(start + far_at, clear_matrix, W_TOO_AT, P)
+                plan_at(start + far_at, clear_late)
                 plan_at(start + far_at + 1, write_matrix, s, HALVES[1], far_rowed)
             plan_at(start + near_at, write_matrix, s, HALVES[0], near_rowed)
             plan_at(start + (2 if last else 5), move_weights, s)
@@ -848,7 +845,9 @@ def tile_dwarfattention_pa_t_kernel(
             for i in range(CHUNKS + HEAD):
                 for part in range(3):
                     project(i, part, True)
-                if i == CHUNKS // 2:
+                if i == 0:
+                    clear_matrix(0, K_AT // W_ROW, zeros)
+                elif i == CHUNKS // 2:
                     store_far_dots(0, 0)
                 elif i == CHUNKS // 2 + 1:
                     fetch_far_dots(0, 0)
@@ -858,8 +857,6 @@ def tile_dwarfattention_pa_t_kernel(
                     load_window(0)
                 elif i == CHUNKS:
                     store_far_dots(0, 1)
-            gains_of_slots(0, True)
-            gains_of_slots(0, False)
 
             next_chunk = CHUNKS + HEAD
             for t in range(end):
@@ -879,7 +876,7 @@ def tile_dwarfattention_pa_t_kernel(
                 elif t == STEPS + 2 + 2:
                     fetch_far_dots(1, 1)
                 elif t == STEPS + 2 + 3:
-                    clear_matrix(W_AT, 64)
+                    clear_matrix(W_AT, 64, zeros_tile())
                 elif t == STEPS + 7:
                     park_k(1, 0)
                 elif t == 2 * STEPS - 2:

@@ -69,14 +69,14 @@ BACK = WINDOW - PLACES
 HALF = PLACES // 2
 CELLS = HALF // 2
 
-S_ROW = 2 * IN_CLASS * HALF
-S_PITCH = S_ROW + HALF
-S_AT = 0
+S_BLOCK = (IN_CLASS + max(OFFSETS) // CLASS) * HALF
+S_PITCH = 2 * S_BLOCK + HALF
 W_ROW = P * HALF
 W_AT = max(OFFSETS) // PLACES * W_ROW
-K_AT = W_AT + P * W_ROW
-W_TOO_AT = K_AT + HD * N
-PARK_AT = K_AT + H * HD * N
+K_PITCH = N + BACK
+K_AT = P * S_PITCH
+W_TOO_AT = K_AT + HD * K_PITCH
+PARK_AT = K_AT + H * HD * K_PITCH
 PARK_ROW = len(SHIFTED) * PLACES
 PARK_PAD = 2
 SHIFTED_RUN = SPLIT - 1
@@ -109,7 +109,7 @@ def tile_dwarfattention_pa_t_kernel(
         const = ctx.enter_context(tc.tile_pool(name="const", bufs=1))
         qkv = ctx.enter_context(tc.tile_pool(name="qkv", bufs=2))
         prods = ctx.enter_context(tc.tile_pool(name="prods", bufs=3))
-        windows = ctx.enter_context(tc.tile_pool(name="windows", bufs=2))
+        windows = ctx.enter_context(tc.tile_pool(name="windows", bufs=3))
         table = ctx.enter_context(tc.tile_pool(name="table", bufs=1))
         phase = ctx.enter_context(tc.tile_pool(name="phase", bufs=1))
         psum_x = ctx.enter_context(tc.psum_pool(name="psum_x", bufs=3))
@@ -121,7 +121,7 @@ def tile_dwarfattention_pa_t_kernel(
         def rows_of(at, count, width):
             return flat[at : at + count * width].rearrange("(r w) -> r w", w=width)
 
-        x_rows_of, x_sorted_of, grouped_of, codes_of, qkv_ps_of = {}, {}, {}, {}, {}
+        x_rows_of, grouped_of, codes_of, qkv_ps_of = {}, {}, {}, {}
 
         def load_x(i):
             b, j = chunks[i]
@@ -192,14 +192,6 @@ def tile_dwarfattention_pa_t_kernel(
             nc.vector.tensor_copy(out=gain[:, b, h], in_=gains_in[:, b, h].rearrange("p c j -> p j c"))
         u1 = const.tile([P, SLOTS - NEAR_SLOTS, PLACES], F32)
 
-        token = const.tile([P, PLACES], F32)
-        nc.gpsimd.iota(
-            token[:], pattern=[[1, PLACES]], base=0, channel_multiplier=PLACES, allow_small_or_imprecise_dtypes=True
-        )
-        reached = const.tile([P, COLS, PLACES], BF16)
-        for col in range(COLS):
-            nc.vector.tensor_single_scalar(out=reached[:, col, :], in_=token[:], scalar=float(OFFSETS[col]), op=ALU.is_ge)
-
         q_splits = []
         for i in range(2):
             q_split = const.tile([P, CHUNK, 2, H * IN_CLASS], F32, name="q_split_%d" % i)
@@ -207,12 +199,14 @@ def tile_dwarfattention_pa_t_kernel(
             q_splits.append(q_split)
 
         bias_col = const.tile([P, 2], F32)
+        warm_exp = const.tile([P, 1], F32)
 
         def turn_bias():
             bias_t = psum_x.tile([P, 2, P], F32, tag="xt")
             for part in range(2):
                 nc.tensor.transpose(bias_t[:, part, :], bias[:, part, :], ident)
             nc.scalar.copy(out=bias_col[:], in_=bias_t[:, :, 0])
+            nc.scalar.activation(out=warm_exp[:], in_=one_col[:], func=ACT.Exp)
 
         def zeros_tile():
             zeros = phase.tile([P, W_ROW // 4], F32, offset=45056)
@@ -220,40 +214,30 @@ def tile_dwarfattention_pa_t_kernel(
             return zeros
 
         zeros = zeros_tile()
+        nc.sync.dma_start(out=rows_of(K_AT, P, K_PITCH)[:, 0:BACK], in_=zeros[:, 0:BACK])
         nc.sync.dma_start(out=rows_of(PARK_AT + P * PARK_ROW, PARK_PAD, PARK_ROW), in_=zeros[0:PARK_PAD, 0:PARK_ROW])
 
         q_of, v_of, v_tile_of, k_t_of, k_chunk_of, s_ps_of, s_of = {}, {}, {}, {}, {}, {}, {}
 
-        def sort_x(i):
-            x_sorted = prods.tile([P, CHUNK, PASSES, 2, P], I32, tag="prod")
-            nc.gpsimd.tensor_copy(
-                out=x_sorted[:].rearrange("p c g u k -> p (c g) u k"),
-                in_=x_rows_of[i][:].rearrange("p c d -> p (c d)").bitcast(I32).rearrange("p (m k u) -> p m u k", k=P, u=2),
-            )
-            x_sorted_of[i] = x_sorted
-
-        def transpose_x(i):
-            grouped = phase.tile([P, PASSES, CHUNK * P * PACK], BF16, bufs=2, offset=16384, align_bytes=64)
-            for g in range(PASSES):
-                grouped_words = grouped[:, g, :].bitcast(F32).rearrange("p (n u) -> p n u", u=2)
-                for half in range(2):
-                    if i in x_sorted_of and g == half == 0:
-                        xt = psum_dots.tile([P, 2, 2 * P], F32, tag="dots_ps")
-                    else:
-                        xt = psum_x.tile([P, 2, 2 * P], F32, tag="xt")
-                    for c in range(2):
-                        place = 2 * half + c
-                        for u in range(2):
-                            if i in x_sorted_of:
-                                words = x_sorted_of[i][:, place, g, u, :].bitcast(F32)
-                            else:
-                                words = x_rows_of[i][:, place, :].bitcast(F32)[:, g * 2 * P + u : (g + 1) * 2 * P : 2]
-                            nc.tensor.transpose(xt[:, u, c * P : (c + 1) * P], words, ident)
-                    nc.scalar.copy(
-                        out=grouped_words[:, half * 2 * P : (half + 1) * 2 * P, :],
-                        in_=xt[:].rearrange("p u n -> p n u"),
-                    )
-            grouped_of[i] = grouped
+        def transpose_x(i, g):
+            if g == 0:
+                grouped = phase.tile([P, PASSES, CHUNK * P * PACK], BF16, bufs=2, offset=16384, align_bytes=64)
+                grouped_of[i] = grouped
+            grouped_words = grouped_of[i][:, g, :].bitcast(F32).rearrange("p (n u) -> p n u", u=2)
+            for half in range(2):
+                if i <= CHUNKS + HEAD + 1 and g == half:
+                    xt = psum_dots.tile([P, 2, 2 * P], F32, tag="dots_ps")
+                else:
+                    xt = psum_x.tile([P, 2, 2 * P], F32, tag="xt")
+                for c in range(2):
+                    place = 2 * half + c
+                    for u in range(2):
+                        words = x_rows_of[i][:, place, :].bitcast(F32)[:, g * 2 * P + u : (g + 1) * 2 * P : 2]
+                        nc.tensor.transpose(xt[:, u, c * P : (c + 1) * P], words, ident)
+                nc.scalar.copy(
+                    out=grouped_words[:, half * 2 * P : (half + 1) * 2 * P, :],
+                    in_=xt[:].rearrange("p u n -> p n u"),
+                )
 
         def quantise_x(i):
             x_codes = phase.tile([P, PASSES, CHUNK * P], U32, bufs=2, offset=32768, align_bytes=64)
@@ -377,7 +361,8 @@ def tile_dwarfattention_pa_t_kernel(
 
         def store_far_dots(b, group):
             nc.sync.dma_start(
-                out=rows_of(S_AT, P, S_PITCH)[:, 0:S_ROW], in_=s_of[b, group][:].rearrange("p s k c -> p (s k c)")
+                out=rows_of(0, P, S_PITCH)[:, 0 : 2 * S_BLOCK].rearrange("r (s k) -> r s k", s=2)[:, :, 0 : IN_CLASS * HALF],
+                in_=s_of[b, group][:].rearrange("p s k c -> p s (k c)"),
             )
 
         def fetch_far_dots(b, group):
@@ -385,7 +370,7 @@ def tile_dwarfattention_pa_t_kernel(
                 if group == 0:
                     dots = table.tile([P, COLS, PLACES], F32, bufs=4)
                     dots_of[2 * b + h] = dots
-                rows = rows_of(S_AT + h * IN_CLASS * S_PITCH + (IN_CLASS - 1) * HALF, P, S_ROW // 2)
+                rows = rows_of(h * IN_CLASS * S_PITCH + (IN_CLASS - 1) * HALF, P, S_BLOCK)
                 for col, count in FAR_RUNS:
                     start = OFFSETS[col] // CLASS * HALF
                     step = HALF if count == 1 else start
@@ -398,20 +383,18 @@ def tile_dwarfattention_pa_t_kernel(
 
         def park_k(b, h):
             nc.sync.dma_start(
-                out=rows_of(K_AT + h * HD * N, HD, N),
+                out=rows_of(K_AT + h * HD * K_PITCH, HD, K_PITCH)[:, BACK:K_PITCH],
                 in_=k_t_of[b][h * HD : (h + 1) * HD].rearrange("p a c -> p (a c)"),
             )
 
         def load_window(n):
             s, group = divmod(n, HD // STEP_D)
             window = windows.tile([P, STEP_D, WINDOW], F32)
-            at = K_AT + (s % H * HD + group * STEP_D) * N - BACK
+            rows = rows_of(K_AT + (s % H * HD + group * STEP_D) * K_PITCH, STEP_D, K_PITCH)
             for r in range(WINDOW // PLACES):
                 nc.sync.dma_start(
                     out=window[r : P : WINDOW // PLACES],
-                    in_=flat[at + r * PLACES : at + r * PLACES + STEP_D * N].rearrange(
-                        "(d a t) -> a d t", d=STEP_D, t=WINDOW
-                    ),
+                    in_=rows[:, r * PLACES : r * PLACES + N].rearrange("d (a t) -> a d t", t=WINDOW),
                 )
             window_of[n] = window
 
@@ -460,11 +443,6 @@ def tile_dwarfattention_pa_t_kernel(
             nc.scalar.copy(
                 out=dots_of[s][:, 0:NEAR, :], in_=back[:].rearrange("p q (i c) -> p (q i) c", c=PLACES)
             )
-
-        def mask_dots(s, near):
-            cols = slice(0, NEAR) if near else slice(NEAR, COLS)
-            dots = dots_of[s][:, cols, :]
-            nc.vector.tensor_tensor(out=dots, in0=dots, in1=reached[:, cols, :], op=ALU.mult)
 
         def scores(s, near):
             h = STAGES[s][1]
@@ -751,7 +729,6 @@ def tile_dwarfattention_pa_t_kernel(
         for s in range(len(STAGES)):
             begin, start, last = STEPS * s, STEPS * (s + 1), s == len(STAGES) - 1
             f = begin + 5
-            vector_job(f, mask_dots, s, False)
             vector_job(f, scores, s, False)
             plan_at(f, exponentials, s, False)
             for work in (features, shares, weights, add_to_z):
@@ -761,8 +738,7 @@ def tile_dwarfattention_pa_t_kernel(
                 plan_at(start, dots_out, s)
                 plan_at(start, dots_back, s)
                 n = start + 2
-                for work in (mask_dots, scores):
-                    vector_job(n, work, s, True)
+                vector_job(n, scores, s, True)
                 plan_at(n, exponentials, s, True)
                 for work in (features, shares, weights):
                     vector_job(n + 1, work, s, True)
@@ -809,16 +785,16 @@ def tile_dwarfattention_pa_t_kernel(
         def project(i, part, early):
             if part == 0:
                 if i + 2 <= last_chunk:
-                    transpose_x(i + 2)
-                    if i + 4 <= last_chunk:
-                        load_x(i + 4)
-                        if early and i + 4 <= 10:
-                            sort_x(i + 4)
+                    transpose_x(i + 2, 0)
                 if early and i > 0:
                     keep_rows(i - 1)
                 if 0 <= i - 1 <= last_chunk:
                     far_dots(i - 1)
                     far_dots_out(i - 1, early)
+                if i + 2 <= last_chunk:
+                    transpose_x(i + 2, 1)
+                    if i + 4 <= last_chunk:
+                        load_x(i + 4)
             elif part == 1:
                 if not early and i - 1 <= last_chunk:
                     keep_rows(i - 1)
@@ -829,17 +805,12 @@ def tile_dwarfattention_pa_t_kernel(
                 keep_columns(i, early)
 
         with tc.manual_schedule():
-            for i in range(2):
-                if 10 > 0:
-                    sort_x(i)
-            transpose_x(0)
+            for g in range(PASSES):
+                transpose_x(0, g)
             load_x(2)
-            if 10 > 0:
-                sort_x(2)
-            transpose_x(1)
+            for g in range(PASSES):
+                transpose_x(1, g)
             load_x(3)
-            if 10 > 0:
-                sort_x(3)
             quantise_x(0)
             turn_bias()
             for i in range(CHUNKS + HEAD):
@@ -855,6 +826,7 @@ def tile_dwarfattention_pa_t_kernel(
                     park_k(0, 0)
                     park_k(0, 1)
                     load_window(0)
+                    load_window(1)
                 elif i == CHUNKS:
                     store_far_dots(0, 1)
 
@@ -863,8 +835,8 @@ def tile_dwarfattention_pa_t_kernel(
                 projecting = t % 2 == 0 and next_chunk <= last_chunk + 1
                 if projecting:
                     project(next_chunk, 0, False)
-                if t < dot_steps and t % QUADS == 0 and t // QUADS + 1 < dot_steps // QUADS:
-                    load_window(t // QUADS + 1)
+                if t < dot_steps and t % QUADS == 0 and t // QUADS + 2 < dot_steps // QUADS:
+                    load_window(t // QUADS + 2)
                 if t == 1:
                     fetch_far_dots(0, 1)
                 elif t == 6:
@@ -876,8 +848,8 @@ def tile_dwarfattention_pa_t_kernel(
                 elif t == STEPS + 2 + 2:
                     fetch_far_dots(1, 1)
                 elif t == STEPS + 2 + 3:
-                    clear_matrix(W_AT, 64, zeros_tile())
-                elif t == STEPS + 7:
+                    clear_matrix(W_AT, P, zeros_tile())
+                elif t == STEPS + 3:
                     park_k(1, 0)
                 elif t == 2 * STEPS - 2:
                     park_k(1, 1)
@@ -903,7 +875,6 @@ def tile_dwarfattention_pa_t_kernel(
                     s = len(STAGES) - 1
                     dots_out(s)
                     dots_back(s)
-                    mask_dots(s, True)
                     scores(s, True)
                     exponentials(s, True)
                     features(s, True)

@@ -121,7 +121,7 @@ def tile_dwarfattention_pa_t_kernel(
         def rows_of(at, count, width):
             return flat[at : at + count * width].rearrange("(r w) -> r w", w=width)
 
-        x_rows_of, grouped_of, codes_of, qkv_ps_of = {}, {}, {}, {}
+        x_rows_of, x_sorted_of, grouped_of, codes_of, qkv_ps_of = {}, {}, {}, {}, {}
 
         def load_x(i):
             b, j = chunks[i]
@@ -219,20 +219,31 @@ def tile_dwarfattention_pa_t_kernel(
 
         q_of, v_of, v_tile_of, k_t_of, k_chunk_of, s_ps_of, s_of = {}, {}, {}, {}, {}, {}, {}
 
+        def sort_x(i):
+            x_sorted = prods.tile([P, CHUNK, PASSES, 2, P], I32, tag="prod")
+            nc.vector.tensor_copy(
+                out=x_sorted[:].rearrange("p c g u k -> p (c g) u k"),
+                in_=x_rows_of[i][:].rearrange("p c d -> p (c d)").bitcast(I32).rearrange("p (m k u) -> p m u k", k=P, u=2),
+            )
+            x_sorted_of[i] = x_sorted
+
         def transpose_x(i, g):
             if g == 0:
                 grouped = phase.tile([P, PASSES, CHUNK * P * PACK], BF16, bufs=2, offset=16384, align_bytes=64)
                 grouped_of[i] = grouped
             grouped_words = grouped_of[i][:, g, :].bitcast(F32).rearrange("p (n u) -> p n u", u=2)
             for half in range(2):
-                if i <= CHUNKS + HEAD + 1 and g == half:
+                if i <= CHUNKS + HEAD + 1 and g == half == 0:
                     xt = psum_dots.tile([P, 2, 2 * P], F32, tag="dots_ps")
                 else:
                     xt = psum_x.tile([P, 2, 2 * P], F32, tag="xt")
                 for c in range(2):
                     place = 2 * half + c
                     for u in range(2):
-                        words = x_rows_of[i][:, place, :].bitcast(F32)[:, g * 2 * P + u : (g + 1) * 2 * P : 2]
+                        if i in x_sorted_of:
+                            words = x_sorted_of[i][:, place, g, u, :].bitcast(F32)
+                        else:
+                            words = x_rows_of[i][:, place, :].bitcast(F32)[:, g * 2 * P + u : (g + 1) * 2 * P : 2]
                         nc.tensor.transpose(xt[:, u, c * P : (c + 1) * P], words, ident)
                 nc.scalar.copy(
                     out=grouped_words[:, half * 2 * P : (half + 1) * 2 * P, :],
@@ -332,7 +343,7 @@ def tile_dwarfattention_pa_t_kernel(
                 nc.scalar.activation(out=k_out, in_=k_in, func=ACT.Identity, bias=bias_col[:, 1:2])
 
         def far_dots(i):
-            s_ps = psum_x.tile([P, CHUNK, 2, IN_CLASS], F32, tag="xt")
+            s_ps = psum_acc.tile([P, CHUNK, 2, IN_CLASS], F32, tag="acc")
             for c in range(CHUNK):
                 for odd in range(2):
                     nc.tensor.matmul(
@@ -800,6 +811,8 @@ def tile_dwarfattention_pa_t_kernel(
                     keep_rows(i - 1)
                 if i + 1 <= last_chunk:
                     quantise_x(i + 1)
+                if early and 3 <= i + 3 <= CHUNKS + HEAD + 1:
+                    sort_x(i + 3)
             elif i <= last_chunk:
                 multiply(i)
                 keep_columns(i, early)

@@ -121,14 +121,17 @@ def tile_dwarfattention_pa_t_kernel(
         def rows_of(at, count, width):
             return flat[at : at + count * width].rearrange("(r w) -> r w", w=width)
 
-        x_rows_of, x_sorted_of, grouped_of, codes_of, qkv_ps_of = {}, {}, {}, {}, {}
+        x_rows_of, grouped_of, codes_of, qkv_ps_of = {}, {}, {}, {}
 
         def load_x(i):
             b, j = chunks[i]
             x_rows = phase.tile([P, CHUNK, D], BF16, bufs=2, offset=0, align_bytes=64)
-            nc.sync.dma_start(
-                out=x_rows[:], in_=x[b].rearrange("(p c) d -> p c d", c=PLACES)[:, j * CHUNK : (j + 1) * CHUNK, :]
-            )
+            for c in range(0, CHUNK, 2) if i == 0 else (0,):
+                width = 2 if i == 0 else CHUNK
+                nc.sync.dma_start(
+                    out=x_rows[:, c : c + width, :],
+                    in_=x[b].rearrange("(p c) d -> p c d", c=PLACES)[:, j * CHUNK + c : j * CHUNK + c + width, :],
+                )
             x_rows_of[i] = x_rows
 
         chunks = [(b, j) for b in range(B) for j in range(CHUNKS)]
@@ -219,14 +222,6 @@ def tile_dwarfattention_pa_t_kernel(
 
         q_of, v_of, v_tile_of, k_t_of, k_chunk_of, s_ps_of, s_of = {}, {}, {}, {}, {}, {}, {}
 
-        def sort_x(i):
-            x_sorted = prods.tile([P, CHUNK, PASSES, 2, P], I32, tag="prod")
-            nc.vector.tensor_copy(
-                out=x_sorted[:].rearrange("p c g u k -> p (c g) u k"),
-                in_=x_rows_of[i][:].rearrange("p c d -> p (c d)").bitcast(I32).rearrange("p (m k u) -> p m u k", k=P, u=2),
-            )
-            x_sorted_of[i] = x_sorted
-
         def transpose_x(i, g):
             if g == 0:
                 grouped = phase.tile([P, PASSES, CHUNK * P * PACK], BF16, bufs=2, offset=16384, align_bytes=64)
@@ -240,10 +235,7 @@ def tile_dwarfattention_pa_t_kernel(
                 for c in range(2):
                     place = 2 * half + c
                     for u in range(2):
-                        if i in x_sorted_of:
-                            words = x_sorted_of[i][:, place, g, u, :].bitcast(F32)
-                        else:
-                            words = x_rows_of[i][:, place, :].bitcast(F32)[:, g * 2 * P + u : (g + 1) * 2 * P : 2]
+                        words = x_rows_of[i][:, place, :].bitcast(F32)[:, g * 2 * P + u : (g + 1) * 2 * P : 2]
                         nc.tensor.transpose(xt[:, u, c * P : (c + 1) * P], words, ident)
                 nc.scalar.copy(
                     out=grouped_words[:, half * 2 * P : (half + 1) * 2 * P, :],
@@ -379,14 +371,14 @@ def tile_dwarfattention_pa_t_kernel(
         def fetch_far_dots(b, group):
             for h in range(H):
                 if group == 0:
-                    dots = table.tile([P, COLS, PLACES], F32, bufs=4)
+                    dots = table.tile([P, COLS - NEAR, PLACES], F32, bufs=4)
                     dots_of[2 * b + h] = dots
                 rows = rows_of(h * IN_CLASS * S_PITCH + (IN_CLASS - 1) * HALF, P, S_BLOCK)
                 for col, count in FAR_RUNS:
                     start = OFFSETS[col] // CLASS * HALF
                     step = HALF if count == 1 else start
                     nc.sync.dma_start(
-                        out=dots_of[2 * b + h][:, col : col + count, group * HALF : (group + 1) * HALF],
+                        out=dots_of[2 * b + h][:, col - NEAR : col - NEAR + count, group * HALF : (group + 1) * HALF],
                         in_=rows[:, start : start + count * step].rearrange("r (g k) -> r g k", k=step)[:, :, 0:HALF],
                     )
 
@@ -440,7 +432,7 @@ def tile_dwarfattention_pa_t_kernel(
                 )
 
 
-        turned_of, weight_of, moved_weight_of, z_of, one_over_z_of = {}, {}, {}, {}, {}
+        turned_of, back_of, weight_of, moved_weight_of, z_of, one_over_z_of = {}, {}, {}, {}, {}, {}
 
         def dots_out(s):
             turned = table.tile([P, QUADS, P], F32)
@@ -451,22 +443,20 @@ def tile_dwarfattention_pa_t_kernel(
             back = psum_x.tile([P, QUADS, P], F32, tag="xt")
             for quad in range(QUADS):
                 nc.tensor.transpose(back[:, quad, :], turned_of[s][:, quad, :], ident)
-            nc.scalar.copy(
-                out=dots_of[s][:, 0:NEAR, :], in_=back[:].rearrange("p q (i c) -> p (q i) c", c=PLACES)
-            )
+            back_of[s] = back
 
         def scores(s, near):
             h = STAGES[s][1]
-            dots = dots_of[s]
-            cols = slice(0, NEAR) if near else slice(NEAR, COLS)
             if near:
-                reads = ((0, NEAR, dots[:, cols, :]), (NEAR, SPLIT - 1, dots[:, 1:SPLIT, :]))
+                dots = back_of[s][:].rearrange("p q (i c) -> p (q i) c", c=PLACES)
+                reads = ((0, NEAR, dots), (NEAR, SPLIT - 1, dots[:, 1:SPLIT, :]))
                 slots = slice(0, NEAR_SLOTS)
             else:
+                dots, zero = dots_of[s], ZERO - NEAR
                 reads = (
-                    (NEAR_SLOTS, COLS - NEAR, dots[:, cols, :]),
-                    (FAR_MORE, SPLIT - 1, dots[:, NEAR : NEAR + SPLIT - 1, :]),
-                    (FAR_MORE + SPLIT - 1, S + 1, dots[:, ZERO : ZERO + 1, :].to_broadcast([P, S + 1, PLACES])),
+                    (NEAR_SLOTS, COLS - NEAR, dots[:]),
+                    (FAR_MORE, SPLIT - 1, dots[:, 0 : SPLIT - 1, :]),
+                    (FAR_MORE + SPLIT - 1, S + 1, dots[:, zero : zero + 1, :].to_broadcast([P, S + 1, PLACES])),
                 )
                 slots = slice(NEAR_SLOTS, SLOTS)
                 weight = table.tile([P, SLOTS, PLACES], F32, bufs=2)
@@ -713,12 +703,11 @@ def tile_dwarfattention_pa_t_kernel(
                 op=ALU.mult,
             )
 
-        def store(s, half):
+        def store(s, first, last):
             b, h = STAGES[s]
-            places = slice(half * HALF, (half + 1) * HALF)
             nc.sync.dma_start(
-                out=out[b].rearrange("(p c) f -> p c f", c=PLACES)[:, places, h * HD : (h + 1) * HD],
-                in_=result_of[s][:, places, :],
+                out=out[b].rearrange("(p c) f -> p c f", c=PLACES)[:, first:last, h * HD : (h + 1) * HD],
+                in_=result_of[s][:, first:last, :],
             )
 
         last_chunk = len(chunks) - 1
@@ -775,17 +764,17 @@ def tile_dwarfattention_pa_t_kernel(
             units = [(half, k) for half in HALVES for k in range(len(MIX_ORDER))]
             for n, (half, k) in enumerate(units):
                 if last:
-                    t = start + 2 + n * 8 // len(units)
-                elif s < len(STAGES) - 2 or n < 14:
+                    t = start + 1 + n * 7 // len(units)
+                elif s < len(STAGES) - 2 or n < 16:
                     t = start + 4 + n * 8 // len(units)
                 else:
-                    t = start + STEPS + (n - 14) // 2
+                    t = start + STEPS + (n - 16) // 2
                 units_at.setdefault(t, []).append((s, half, k))
                 if k == len(MIX_ORDER) - 1:
                     mixed = t + (3 if last else 2)
                     plan_at(mixed, mix_out, s, half)
                     for bank in range(2):
-                        far_from, far_steps = (((4, 2), (6, 2), (9, 2), (11, 2)) if last else ((11, 2), (13, 2), (15, 3), (18, 3)) if s == 0 else ((9, 1), (10, 1), (13, 1), (14, 1)) if s == 2 else ((9, 3), (12, 3), (15, 3), (18, 3)))[(half != HALVES[0]) * 2 + bank]
+                        far_from, far_steps = (((4, 2), (6, 2), (9, 2), (11, 2)) if last else ((11, 2), (13, 2), (15, 3), (18, 3)) if s == 0 else ((8, 2), (10, 2), (13, 1), (14, 1)) if s == 2 else ((9, 2), (12, 2), (15, 2), (18, 2)))[(half != HALVES[0]) * 2 + bank]
                         for i in range(8):
                             plan_at(start + far_from + i * far_steps // 8, mix_far, s, half, 8 * bank + i)
                         done = max(mixed + 1, start + far_from + far_steps)
@@ -811,8 +800,6 @@ def tile_dwarfattention_pa_t_kernel(
                     keep_rows(i - 1)
                 if i + 1 <= last_chunk:
                     quantise_x(i + 1)
-                if early and 3 <= i + 3 <= CHUNKS + HEAD + 1:
-                    sort_x(i + 3)
             elif i <= last_chunk:
                 multiply(i)
                 keep_columns(i, early)
@@ -912,7 +899,7 @@ def tile_dwarfattention_pa_t_kernel(
                     work[0](*work[1:])
                 if t == dot_steps + STEPS - 1:
                     for done in range(3):
-                        for half in HALVES:
-                            store(done, half)
+                        store(done, 0, PLACES)
             for half in HALVES:
-                store(3, half)
+                for bank in range(2):
+                    store(3, half * HALF + 8 * bank, half * HALF + 8 * bank + 8)

from contextlib import ExitStack

import concourse.mybir as mybir
from concourse.masks import make_identity

F32 = mybir.dt.float32
BF16 = mybir.dt.bfloat16
U8 = mybir.dt.uint8
U32 = mybir.dt.uint32
I32 = mybir.dt.int32
FP8X4 = mybir.dt.float8_e4m3fn_x4
FP4X4 = mybir.dt.float4_e2m1fn_x4
ALU = mybir.AluOpType
ACT = mybir.ActivationFunctionType
AXIS = mybir.AxisListType

B, N, D, H, HD, S = 2, 4096, 1024, 2, 64, 11
D4 = (0.4829629131445341, 0.8365163037378079, 0.2241438680420134, -0.1294095225512604)

P = 128
PACK = 4
K_PASS = P * PACK
PASSES = D // K_PASS
PLACES = N // P
CHUNK = 4
CHUNKS = PLACES // CHUNK
STAGES = tuple((b, h) for b in range(B) for h in range(H))

SPLIT = 6
NEAR = 2 * SPLIT
OFFSETS = (
    tuple(1 << i for i in range(SPLIT))
    + tuple(3 << j for j in range(SPLIT))
    + tuple(1 << i for i in range(SPLIT, S + 1))
    + (0,)
    + tuple(3 << j for j in range(SPLIT, S))
)
COLS = len(OFFSETS)
ZERO = OFFSETS.index(0)
CLASS = 64
IN_CLASS = N // CLASS
ROWED = tuple(c for c in range(COLS) if OFFSETS[c] % PLACES == 0)
SHIFTED = tuple(c for c in range(COLS) if OFFSETS[c] % PLACES != 0)
NEAR_TAPS = ((1, 0, SPLIT, 0), (3, 0, SPLIT, SPLIT), (2, 0, SPLIT - 1, NEAR))
NEAR_SLOTS = NEAR + SPLIT - 1
FAR_ZERO = NEAR_SLOTS + ZERO - NEAR
FAR_MORE = NEAR_SLOTS + COLS - NEAR
FAR_TAPS = (
    (1, SPLIT, S, NEAR_SLOTS),
    (2, S - 1, S, FAR_ZERO - 1),
    (3, SPLIT, S, FAR_ZERO + 1),
    (2, SPLIT - 1, S - 1, FAR_MORE),
    (0, 0, S, FAR_MORE + SPLIT - 1),
)
LOCAL = FAR_MORE + SPLIT - 1 + S
SLOTS = LOCAL + 1


def slot_of(col):
    return col if col < NEAR else NEAR_SLOTS + col - NEAR


QUAD = P // PLACES
QUADS = NEAR // QUAD
STEP_D = 16
STEPS = HD // STEP_D * QUADS
WINDOW = 4 * PLACES
BACK = WINDOW - PLACES
HALF = PLACES // 2
CELLS = HALF // 2

S_BLOCK = (IN_CLASS + max(OFFSETS) // CLASS) * HALF
S_PITCH = 2 * S_BLOCK + HALF
W_ROW = P * HALF
W_AT = max(OFFSETS) // PLACES * W_ROW
K_PITCH = N + BACK
K_AT = P * S_PITCH
W_TOO_AT = K_AT + HD * K_PITCH
PARK_AT = K_AT + H * HD * K_PITCH
PARK_ROW = len(SHIFTED) * PLACES
PARK_PAD = 2
SHIFTED_RUN = SPLIT - 1
EXTRA = len(SHIFTED)

HEAD = 1

FAR_RUNS = ((NEAR, 2), (NEAR + 2, 2), (NEAR + 4, 2), (ZERO, 1), (ZERO + 1, 2), (ZERO + 3, 2), (ZERO + 5, 1))


FLOPS = 2 * B * N * D * 3 * H * HD + B * H * N * (4 * S + 1) * 4 * HD


def parts(o):
    move, rest = divmod(o, PLACES)
    if rest == 0:
        return ((0, PLACES, move, 0),)
    return ((rest, PLACES, move, 0), (0, rest, move + 1, PLACES - rest))


MIX_ORDER = (1, 0) + SHIFTED[2:]
HALVES = (1, 0)


def tile_dwarfattention_pa_t_kernel(
    tc, x, W_qkv_words, W_qkv_scales, b_qkv, gains, pos_bias, identity_bypass, out
):
    nc = tc.nc
    with ExitStack() as ctx:
        const = ctx.enter_context(tc.tile_pool(name="const", bufs=1))
        qkv = ctx.enter_context(tc.tile_pool(name="qkv", bufs=2))
        prods = ctx.enter_context(tc.tile_pool(name="prods", bufs=3))
        windows = ctx.enter_context(tc.tile_pool(name="windows", bufs=3))
        table = ctx.enter_context(tc.tile_pool(name="table", bufs=1))
        phase = ctx.enter_context(tc.tile_pool(name="phase", bufs=1))
        psum_x = ctx.enter_context(tc.psum_pool(name="psum_x", bufs=3))
        psum_dots = ctx.enter_context(tc.psum_pool(name="psum_dots", bufs=1))
        psum_acc = ctx.enter_context(tc.psum_pool(name="psum_acc", bufs=4))

        flat = out.rearrange("b n f -> (b n f)")

        def rows_of(at, count, width):
            return flat[at : at + count * width].rearrange("(r w) -> r w", w=width)

        x_rows_of, grouped_of, codes_of, qkv_ps_of = {}, {}, {}, {}

        def load_x(i):
            b, j = chunks[i]
            x_rows = phase.tile([P, CHUNK, D], BF16, bufs=2, offset=0, align_bytes=64)
            for c in range(0, CHUNK, 2) if i == 0 else (0,):
                width = 2 if i == 0 else CHUNK
                nc.sync.dma_start(
                    out=x_rows[:, c : c + width, :],
                    in_=x[b].rearrange("(p c) d -> p c d", c=PLACES)[:, j * CHUNK + c : j * CHUNK + c + width, :],
                )
            x_rows_of[i] = x_rows

        chunks = [(b, j) for b in range(B) for j in range(CHUNKS)]
        load_x(0)
        load_x(1)

        ident_twice = const.tile([P, 2 * P], F32)
        make_identity(nc, ident_twice[:, 0:P])
        make_identity(nc, ident_twice[:, P : 2 * P])
        ident = ident_twice[:, 0:P]
        move_by_one = const.tile([P, P], F32)
        nc.vector.tensor_copy(out=move_by_one[:], in_=ident_twice[:, P - 1 : 2 * P - 1])
        one_col = const.tile([P, 1], F32)
        nc.vector.memset(one_col[:], 1.0)
        minus_one_col = const.tile([P, 1], F32)
        nc.vector.memset(minus_one_col[:], -1.0)
        w_words = const.tile([P, PASSES, 2 * 3 * P], U8, align_bytes=64)
        for g in range(PASSES):
            nc.sync.dma_start(out=w_words[:, g, :].bitcast(I32), in_=W_qkv_words[g].bitcast(I32))
        w_scales = const.tile([P, PASSES, 3 * P], U8, align_bytes=64)
        nc.vector.memset(w_scales[:].bitcast(I32), 0)
        for quadrant in range(4):
            nc.sync.dma_start(
                out=w_scales[32 * quadrant : 32 * quadrant + 4, :, :].bitcast(I32),
                in_=W_qkv_scales[:, 4 * quadrant : 4 * quadrant + 4, :].rearrange("g r n -> r g n").bitcast(I32),
            )
        bias_bf16 = phase.tile([P, 3 * P], BF16, offset=63488)
        nc.sync.dma_start(out=bias_bf16[:], in_=b_qkv.partition_broadcast(P))
        bias = const.tile([P, 3, P], F32)
        nc.vector.tensor_copy(out=bias[:].rearrange("p r f -> p (r f)"), in_=bias_bf16[:])

        pos_bias_all = phase.tile([P, 4 * S * H], BF16, offset=64512)
        nc.sync.dma_start(out=pos_bias_all[:], in_=pos_bias.rearrange("r h -> (r h)").partition_broadcast(P))
        bias_plus_1 = const.tile([P, SLOTS, H], F32)
        nc.vector.memset(bias_plus_1[:], 1.0)
        for tau, first, last, at in NEAR_TAPS + FAR_TAPS:
            nc.vector.tensor_scalar_add(
                out=bias_plus_1[:, at : at + last - first, :],
                in0=pos_bias_all[:].rearrange("p (j t h) -> p t j h", t=4, h=H)[:, tau, first:last],
                scalar1=1.0,
            )

        bypass_bf16 = const.tile([P, H], BF16)
        nc.sync.dma_start(out=bypass_bf16[:], in_=identity_bypass.partition_broadcast(P))
        bypass = const.tile([P, H], F32)
        nc.vector.tensor_copy(out=bypass[:], in_=bypass_bf16[:])
        bypass_tail = const.tile([P, H], F32)
        nc.scalar.activation(out=bypass_tail[:], in_=bypass[:], func=ACT.Abs)
        nc.scalar.activation(out=bypass_tail[:], in_=bypass_tail[:], func=ACT.Exp, scale=-1.0)
        nc.scalar.activation(out=bypass_tail[:], in_=bypass_tail[:], func=ACT.Ln, bias=one_col[:, 0:1])
        local_gain = const.tile([P, H], F32)
        nc.vector.scalar_tensor_tensor(
            out=local_gain[:], in0=bypass[:], scalar=0.0, in1=bypass_tail[:], op0=ALU.max, op1=ALU.add
        )

        gains_in = phase.tile([P, B, H, PLACES, S], BF16, offset=65536)
        for b, h in STAGES:
            nc.sync.dma_start(out=gains_in[:, b, h, :, :], in_=gains[b, h].rearrange("(p c) j -> p c j", c=PLACES))
        gain = const.tile([P, B, H, S, PLACES], BF16)
        for b, h in STAGES:
            nc.vector.tensor_copy(out=gain[:, b, h], in_=gains_in[:, b, h].rearrange("p c j -> p j c"))
        u1 = const.tile([P, SLOTS - NEAR_SLOTS, PLACES], F32)

        q_splits = []
        for i in range(2):
            q_split = const.tile([P, CHUNK, 2, H * IN_CLASS], F32, name="q_split_%d" % i)
            nc.gpsimd.memset(q_split[:], 0.0)
            q_splits.append(q_split)

        bias_col = const.tile([P, 2], F32)
        warm_exp = const.tile([P, 1], F32)

        def turn_bias():
            bias_t = psum_x.tile([P, 2, P], F32, tag="xt")
            for part in range(2):
                nc.tensor.transpose(bias_t[:, part, :], bias[:, part, :], ident)
            nc.scalar.copy(out=bias_col[:], in_=bias_t[:, :, 0])
            nc.scalar.activation(out=warm_exp[:], in_=one_col[:], func=ACT.Exp)

        def zeros_tile():
            zeros = phase.tile([P, W_ROW // 4], F32, offset=45056)
            nc.gpsimd.memset(zeros[:], 0.0)
            return zeros

        zeros = zeros_tile()
        nc.sync.dma_start(out=rows_of(K_AT, P, K_PITCH)[:, 0:BACK], in_=zeros[:, 0:BACK])
        nc.sync.dma_start(out=rows_of(PARK_AT + P * PARK_ROW, PARK_PAD, PARK_ROW), in_=zeros[0:PARK_PAD, 0:PARK_ROW])

        q_of, v_of, v_tile_of, k_t_of, k_chunk_of, s_ps_of, s_of = {}, {}, {}, {}, {}, {}, {}

        def transpose_x(i, g):
            if g == 0:
                grouped = phase.tile([P, PASSES, CHUNK * P * PACK], BF16, bufs=2, offset=16384, align_bytes=64)
                grouped_of[i] = grouped
            grouped_words = grouped_of[i][:, g, :].bitcast(F32).rearrange("p (n u) -> p n u", u=2)
            for half in range(2):
                if i <= CHUNKS + HEAD + 1 and g == half == 0:
                    xt = psum_dots.tile([P, 2, 2 * P], F32, tag="dots_ps")
                else:
                    xt = psum_x.tile([P, 2, 2 * P], F32, tag="xt")
                for c in range(2):
                    place = 2 * half + c
                    for u in range(2):
                        words = x_rows_of[i][:, place, :].bitcast(F32)[:, g * 2 * P + u : (g + 1) * 2 * P : 2]
                        nc.tensor.transpose(xt[:, u, c * P : (c + 1) * P], words, ident)
                nc.scalar.copy(
                    out=grouped_words[:, half * 2 * P : (half + 1) * 2 * P, :],
                    in_=xt[:].rearrange("p u n -> p n u"),
                )

        def quantise_x(i):
            x_codes = phase.tile([P, PASSES, CHUNK * P], U32, bufs=2, offset=32768, align_bytes=64)
            x_scales = phase.tile([P, PASSES, CHUNK * P], U8, bufs=2, offset=40960, align_bytes=64)
            for g in range(PASSES):
                nc.vector.quantize_mx(
                    out=x_codes[:, g, :].bitcast(FP8X4), scales=x_scales[:, g, :], in_=grouped_of[i][:, g, :]
                )
            codes_of[i] = x_codes, x_scales

        def multiply(i):
            x_codes, x_scales = codes_of[i]
            for part in (0, 1):
                qkv_ps = psum_acc.tile([P, CHUNK, P], F32, tag="acc")
                for g in range(PASSES):
                    nc.tensor.matmul_mx(
                        out=qkv_ps[:].rearrange("p c n -> p (c n)"),
                        lhsT=w_words[:, g, part * 2 * P : (part + 1) * 2 * P].bitcast(FP4X4),
                        lhsT_scale=w_scales[:, g, part * P : (part + 1) * P],
                        rhs=x_codes[:, g, :].bitcast(FP8X4),
                        rhs_scale=x_scales[:, g, :],
                        start=(g == 0),
                        stop=(g == PASSES - 1),
                    )
                qkv_ps_of[i, part, "columns"] = qkv_ps
            for part in (0, 2):
                qkv_ps = psum_acc.tile([P, CHUNK, P], F32, tag="acc")
                for c in range(CHUNK):
                    tokens = slice(c * P, (c + 1) * P)
                    for g in range(PASSES):
                        nc.tensor.matmul_mx(
                            out=qkv_ps[:, c, :],
                            lhsT=x_codes[:, g, tokens].bitcast(FP8X4),
                            lhsT_scale=x_scales[:, g, tokens],
                            rhs=w_words[:, g, part * 2 * P : (part + 1) * 2 * P].bitcast(FP4X4),
                            rhs_scale=w_scales[:, g, part * P : (part + 1) * P],
                            start=(g == 0),
                            stop=(g == PASSES - 1),
                        )
                qkv_ps_of[i, part, "rows"] = qkv_ps

        def keep_rows(i):
            b, j = chunks[i]
            if j == 0:
                for h in range(H):
                    q = qkv.tile([P, HD, PLACES], F32, tag="q", bufs=4)
                    q_of[b, h] = q
                v = qkv.tile([P, H, PLACES, HD], F32)
                v_of[b] = v
            places = slice(j * CHUNK, (j + 1) * CHUNK)
            for h in range(H):
                features = slice(h * HD, (h + 1) * HD)
                nc.vector.tensor_tensor(
                    out=q_of[b, h][:, :, places],
                    in0=qkv_ps_of[i, 0, "rows"][:, :, features].rearrange("p c d -> p d c"),
                    in1=bias[:, 0, features].unsqueeze(2).to_broadcast([P, HD, CHUNK]),
                    op=ALU.add,
                )
            for h in range(H):
                features = slice(h * HD, (h + 1) * HD)
                nc.vector.tensor_tensor(
                    out=v_of[b][:, h, places, :],
                    in0=qkv_ps_of[i, 2, "rows"][:, :, features],
                    in1=bias[:, 2, features].unsqueeze(1).to_broadcast([P, CHUNK, HD]),
                    op=ALU.add,
                )

        def keep_columns(i, by_vector):
            b, j = chunks[i]
            q_ps, k_ps = qkv_ps_of[i, 0, "columns"], qkv_ps_of[i, 1, "columns"]
            for h in range(H):
                mine = slice(h * HD, (h + 1) * HD)
                nc.scalar.activation(
                    out=q_splits[i % 2][mine, :, :, h * IN_CLASS : (h + 1) * IN_CLASS],
                    in_=q_ps[mine, :, :].rearrange("p c (k s) -> p c s k", s=2),
                    func=ACT.Identity,
                    bias=bias_col[mine, 0:1],
                )
            k_chunk = phase.tile([P, CHUNK, 2, IN_CLASS], F32, bufs=2, offset=43008)
            nc.scalar.activation(
                out=k_chunk[:], in_=k_ps[:, :, ::-1].rearrange("p c (k s) -> p c s k", s=2), func=ACT.Identity, bias=bias_col[:, 1:2]
            )
            k_chunk_of[i] = k_chunk
            if j == 0:
                k_t = phase.tile([P, P, PLACES], F32, offset=47104)
                k_t_of[b] = k_t
            k_out = k_t_of[b][:, :, j * CHUNK : (j + 1) * CHUNK]
            k_in = k_ps[:].rearrange("p c n -> p n c")
            if by_vector:
                nc.vector.tensor_scalar_add(out=k_out, in0=k_in, scalar1=bias_col[:, 1:2])
            else:
                nc.scalar.activation(out=k_out, in_=k_in, func=ACT.Identity, bias=bias_col[:, 1:2])

        def far_dots(i):
            s_ps = psum_acc.tile([P, CHUNK, 2, IN_CLASS], F32, tag="acc")
            for c in range(CHUNK):
                for odd in range(2):
                    nc.tensor.matmul(
                        out=s_ps[:, c, odd, :],
                        lhsT=q_splits[i % 2][:, c, odd, :],
                        rhs=k_chunk_of[i][:, c, 1 - odd, :],
                        start=True,
                        stop=True,
                    )
            s_ps_of[i] = s_ps

        def far_dots_out(i, by_vector):
            b, j = chunks[i]
            group, place = divmod(j * CHUNK, HALF)
            if place == 0:
                s_rows = phase.tile([P, 2, IN_CLASS, HALF], F32, bufs=2, offset=63488)
                s_of[b, group] = s_rows
            out_view = s_of[b, group][:, :, :, place : place + CHUNK]
            in_view = s_ps_of[i][:].rearrange("p c s k -> p s k c")
            if by_vector:
                nc.vector.tensor_copy(out=out_view, in_=in_view)
            else:
                nc.scalar.copy(out=out_view, in_=in_view)

        dots_of = {}

        def store_far_dots(b, group):
            nc.sync.dma_start(
                out=rows_of(0, P, S_PITCH)[:, 0 : 2 * S_BLOCK].rearrange("r (s k) -> r s k", s=2)[:, :, 0 : IN_CLASS * HALF],
                in_=s_of[b, group][:].rearrange("p s k c -> p s (k c)"),
            )

        def fetch_far_dots(b, group):
            for h in range(H):
                if group == 0:
                    dots = table.tile([P, COLS - NEAR, PLACES], F32, bufs=4)
                    dots_of[2 * b + h] = dots
                rows = rows_of(h * IN_CLASS * S_PITCH + (IN_CLASS - 1) * HALF, P, S_BLOCK)
                for col, count in FAR_RUNS:
                    start = OFFSETS[col] // CLASS * HALF
                    step = HALF if count == 1 else start
                    nc.sync.dma_start(
                        out=dots_of[2 * b + h][:, col - NEAR : col - NEAR + count, group * HALF : (group + 1) * HALF],
                        in_=rows[:, start : start + count * step].rearrange("r (g k) -> r g k", k=step)[:, :, 0:HALF],
                    )

        prod_of, dots_ps_of, window_of = {}, {}, {}

        def park_k(b, h):
            nc.sync.dma_start(
                out=rows_of(K_AT + h * HD * K_PITCH, HD, K_PITCH)[:, BACK:K_PITCH],
                in_=k_t_of[b][h * HD : (h + 1) * HD].rearrange("p a c -> p (a c)"),
            )

        def load_window(n):
            s, group = divmod(n, HD // STEP_D)
            window = windows.tile([P, STEP_D, WINDOW], F32)
            rows = rows_of(K_AT + (s % H * HD + group * STEP_D) * K_PITCH, STEP_D, K_PITCH)
            for r in range(WINDOW // PLACES):
                nc.sync.dma_start(
                    out=window[r : P : WINDOW // PLACES],
                    in_=rows[:, r * PLACES : r * PLACES + N].rearrange("d (a t) -> a d t", t=WINDOW),
                )
            window_of[n] = window

        def product(t, i):
            s, step = divmod(t, STEPS)
            group, quad = divmod(step, QUADS)
            if i == 0:
                prod = prods.tile([P, STEP_D, QUAD, PLACES], F32)
                prod_of[t] = prod
            first = BACK - OFFSETS[quad * QUAD + i]
            nc.vector.tensor_tensor(
                out=prod_of[t][:, :, i, :],
                in0=q_of[STAGES[s]][:, group * STEP_D : (group + 1) * STEP_D, :],
                in1=window_of[t // QUADS][:, :, first : first + PLACES],
                op=ALU.mult,
            )

        def sum_products(t):
            s, step = divmod(t, STEPS)
            quad = step % QUADS
            if step == 0:
                dots_ps = psum_dots.tile([P, QUADS, P], F32, tag="dots_ps")
                dots_ps_of[s] = dots_ps
            for d in range(STEP_D):
                nc.tensor.matmul(
                    dots_ps_of[s][:, quad, :],
                    lhsT=prod_of[t][:, d, :, :].rearrange("p i c -> p (i c)"),
                    rhs=ident,
                    start=(step == 0 and d == 0),
                    stop=(step == STEPS - 1 and d == STEP_D - 1),
                    is_transpose=True,
                )


        turned_of, back_of, weight_of, moved_weight_of, z_of, one_over_z_of = {}, {}, {}, {}, {}, {}

        def dots_out(s):
            turned = table.tile([P, QUADS, P], F32)
            nc.scalar.copy(out=turned[:], in_=dots_ps_of[s][:])
            turned_of[s] = turned

        def dots_back(s):
            back = psum_x.tile([P, QUADS, P], F32, tag="xt")
            for quad in range(QUADS):
                nc.tensor.transpose(back[:, quad, :], turned_of[s][:, quad, :], ident)
            back_of[s] = back

        def scores(s, near):
            h = STAGES[s][1]
            if near:
                dots = back_of[s][:].rearrange("p q (i c) -> p (q i) c", c=PLACES)
                reads = ((0, NEAR, dots), (NEAR, SPLIT - 1, dots[:, 1:SPLIT, :]))
                slots = slice(0, NEAR_SLOTS)
            else:
                dots, zero = dots_of[s], ZERO - NEAR
                reads = (
                    (NEAR_SLOTS, COLS - NEAR, dots[:]),
                    (FAR_MORE, SPLIT - 1, dots[:, 0 : SPLIT - 1, :]),
                    (FAR_MORE + SPLIT - 1, S + 1, dots[:, zero : zero + 1, :].to_broadcast([P, S + 1, PLACES])),
                )
                slots = slice(NEAR_SLOTS, SLOTS)
                weight = table.tile([P, SLOTS, PLACES], F32, bufs=2)
                weight_of[s] = weight
                z = table.tile([P, 4, PLACES], F32, bufs=2)
                z_of[s] = z
            for at, count, dots_read in reads:
                nc.vector.tensor_tensor(
                    out=u1[:, at - slots.start : at - slots.start + count, :],
                    in0=dots_read,
                    in1=bias_plus_1[:, at : at + count, h : h + 1].to_broadcast([P, count, PLACES]),
                    op=ALU.add,
                )

        def exponentials(s, near):
            slots = slice(0, NEAR_SLOTS) if near else slice(NEAR_SLOTS, SLOTS)
            nc.scalar.activation(
                out=weight_of[s][:, slots, :],
                in_=u1[:, 0 : slots.stop - slots.start, :],
                func=ACT.Exp,
                bias=minus_one_col[:, 0:1],
            )

        def features(s, near):
            slots = slice(0, NEAR_SLOTS) if near else slice(NEAR_SLOTS, SLOTS)
            share, u1_read = weight_of[s][:, slots, :], u1[:, 0 : slots.stop - slots.start, :]
            nc.vector.scalar_tensor_tensor(
                out=share.rearrange("p s c -> p (s c)"),
                in0=share.rearrange("p s c -> p (s c)"),
                scalar=1.0,
                in1=u1_read.rearrange("p s c -> p (s c)"),
                op0=ALU.min,
                op1=ALU.max,
            )

        def shares(s, near):
            b, h = STAGES[s]
            weight = weight_of[s]
            for tau, first, last, at in NEAR_TAPS if near else FAR_TAPS:
                share = weight[:, at : at + last - first, :].rearrange("p s c -> p (s c)")
                nc.vector.scalar_tensor_tensor(
                    out=share,
                    in0=share,
                    scalar=D4[tau],
                    in1=gain[:, b, h, first:last, :].rearrange("p s c -> p (s c)"),
                    op0=ALU.mult,
                    op1=ALU.mult,
                )
            if not near:
                nc.vector.tensor_scalar_mul(out=weight[:, LOCAL, :], in0=weight[:, LOCAL, :], scalar1=local_gain[:, h : h + 1])

        def weights(s, near):
            weight = weight_of[s]
            at, more = (1, NEAR) if near else (NEAR_SLOTS, FAR_MORE)
            nc.vector.tensor_tensor(
                out=weight[:, at : at + SPLIT - 1, :],
                in0=weight[:, at : at + SPLIT - 1, :],
                in1=weight[:, more : more + SPLIT - 1, :],
                op=ALU.add,
            )
            if not near:
                nc.vector.tensor_reduce(
                    out=weight[:, FAR_ZERO, :],
                    in_=weight[:, FAR_MORE + SPLIT - 1 : SLOTS, :].rearrange("p s c -> p c s"),
                    axis=AXIS.X,
                    op=ALU.add,
                )

        def add_to_z(s, near):
            weight, z = weight_of[s], z_of[s]
            if near:
                runs = (slice(0, SPLIT), slice(SPLIT, NEAR))
            else:
                runs = (slice(NEAR_SLOTS, FAR_ZERO + 1), slice(FAR_ZERO + 1, FAR_MORE))
            at = 2 * near
            for i, slots in enumerate(runs):
                nc.vector.tensor_reduce(
                    out=z[:, at + i, :], in_=weight[:, slots, :].rearrange("p o c -> p c o"), axis=AXIS.X, op=ALU.add
                )

        def subtract_in_z(s, near):
            z, at = z_of[s], 2 * near
            nc.vector.tensor_tensor(out=z[:, at, :], in0=z[:, at, :], in1=z[:, at + 1, :], op=ALU.subtract)

        def add_up_z(s):
            one_over_z = table.tile([P, PLACES], F32, bufs=2)
            nc.vector.scalar_tensor_tensor(
                out=one_over_z[:], in0=z_of[s][:, 0, :], scalar=1e-06, in1=z_of[s][:, 2, :], op0=ALU.add, op1=ALU.add
            )
            one_over_z_of[s] = one_over_z

        def invert_z(s):
            nc.vector.reciprocal(out=one_over_z_of[s][:], in_=one_over_z_of[s][:])

        def park_weights(s):
            for run in range(2):
                columns = slice(run * SHIFTED_RUN * PLACES, (run + 1) * SHIFTED_RUN * PLACES)
                nc.sync.dma_start(
                    out=rows_of(PARK_AT, P, PARK_ROW)[:, columns],
                    in_=weight_of[s][:, run * SPLIT : run * SPLIT + SHIFTED_RUN, :].rearrange("p o c -> p (o c)"),
                )

        def move_weights(s):
            moved = table.tile([P, len(SHIFTED) + 1, PLACES], F32, bufs=2)
            nc.sync.dma_start(
                out=moved[:, 0 : len(SHIFTED), :].rearrange("p o c -> p (o c)"), in_=rows_of(PARK_AT + PARK_ROW, P, PARK_ROW)
            )
            nc.sync.dma_start(
                out=moved[:, EXTRA, :],
                in_=rows_of(PARK_AT + 2 * PARK_ROW, P, PARK_ROW)[:, (EXTRA - 1) * PLACES : EXTRA * PLACES],
            )
            moved_weight_of[s] = moved

        loaded_of, matrix_of = {}, {}

        def matrix_at(s, half):
            return W_TOO_AT if s == len(STAGES) - 1 and half == HALVES[1] else W_AT

        def clear_matrix(at, rows, zeros):
            for part in range(0, rows, 32):
                nc.sync.dma_start(out=rows_of(at + part * W_ROW, P, W_ROW // 4), in_=zeros[:])

        def write_matrix(s, half, columns):
            for col in columns:
                at = matrix_at(s, half) - OFFSETS[col] // PLACES * W_ROW
                nc.sync.dma_start(
                    out=rows_of(at, P, W_ROW + HALF)[:, 0:HALF],
                    in_=weight_of[s][:, slot_of(col), half * HALF : (half + 1) * HALF],
                )

        def read_matrix(s, half):
            if matrix_at(s, half) == W_AT:
                loaded = phase.tile([P, P, HALF], F32, offset=35840)
            else:
                loaded = phase.tile([P, P, HALF], F32, tag="loaded_too", offset=47104)
            nc.sync.dma_start(
                out=loaded[:].rearrange("p q c -> p (q c)"), in_=rows_of(matrix_at(s, half), P, W_ROW)
            )
            loaded_of[s, half] = loaded

        def turn_matrix(s, half):
            matrix = phase.tile([P, HALF, P], F32, bufs=2, offset=63488)
            turned_view = matrix[:].rearrange("p (g k) q -> p g q k", k=4)
            loaded_view = loaded_of[s, half][:].rearrange("p q (g k) -> p g q k", k=4)
            if s == len(STAGES) - 1:
                nc.vector.tensor_copy(out=turned_view, in_=loaded_view)
            else:
                nc.scalar.copy(out=turned_view, in_=loaded_view)
            matrix_of[s, half] = matrix

        weighted_of, acc_of, acc_cols_of, fin_of, result_of = {}, {}, {}, {}, {}

        def cells(col, half):
            found = []
            for cell in range(CELLS):
                place = half * HALF + 2 * cell
                moves = [[part[2] for part in parts(OFFSETS[col]) if part[0] <= p < part[1]][0] for p in (place, place + 1)]
                found.append((cell, 2 * cell, moves[0]))
                if moves[0] != moves[1]:
                    found.append((cell, HALF, moves[1]))
            return found

        def weigh(s, half, k, by_vector):
            b, h = STAGES[s]
            col = MIX_ORDER[k]
            weighted = phase.tile([P, HALF + 2, HD], F32, bufs=6, offset=0)
            split = [found[0] for found in cells(col, half) if found[1] == HALF]
            for cell in split:
                nc.vector.memset(weighted[:, 2 * cell + 1, :], 0.0)
                nc.vector.memset(weighted[:, HALF, :], 0.0)
            for first, last, move, source in parts(OFFSETS[col]):
                for place in range(max(first, half * HALF), min(last, (half + 1) * HALF)):
                    c = place - half * HALF
                    slot = HALF + 1 if c % 2 == 1 and c // 2 in split else c
                    v_read = v_of[b][:, h, source + place - first, :]
                    if move == 0:
                        scale = weight_of[s][:, col, place : place + 1]
                    else:
                        moved_col = SHIFTED.index(col) if move == 1 else EXTRA
                        scale = moved_weight_of[s][:, moved_col, place : place + 1]
                    if c >= HALF - by_vector:
                        nc.vector.tensor_scalar_mul(out=weighted[:, slot, :], in0=v_read, scalar1=scale)
                    else:
                        nc.scalar.activation(out=weighted[:, slot, :], in_=v_read, func=ACT.Copy, scale=scale)
            weighted_of[s, half, k] = weighted

        def sum_weighted(s, half, k):
            col = MIX_ORDER[k]
            opens, closes = k == 0, k == len(MIX_ORDER) - 1
            if opens:
                for bank in range(CELLS // 4):
                    acc = psum_acc.tile([P, 4, P], F32, tag="acc")
                    acc_of[s, half, bank] = acc
            for cell, slot, move in cells(col, half):
                nc.tensor.matmul(
                    acc_of[s, half, cell // 4][:, cell % 4, :],
                    lhsT=weighted_of[s, half, k][:, slot : slot + 2, :].rearrange("p c d -> p (c d)"),
                    rhs=move_by_one[:] if move == 1 else ident_twice[:, P - move : 2 * P - move],
                    start=(opens and cell % 4 == 0),
                    stop=(closes and cell % 4 == 3),
                    is_transpose=True,
                )

        def mix_out(s, half):
            acc_cols = phase.tile([P, CELLS, P], F32, bufs=2, offset=27648)
            for bank in range(CELLS // 4):
                nc.scalar.copy(out=acc_cols[:, 4 * bank : 4 * bank + 4, :], in_=acc_of[s, half, bank][:])
            acc_cols_of[s, half] = acc_cols

        def mix_far(s, half, i):
            b, h = STAGES[s]
            bank, place = divmod(i, 8)
            if place == 0:
                fin = psum_x.tile([P, 4, P], F32, tag="xt")
                fin_of[s, half, bank] = fin
            nc.tensor.matmul(
                fin_of[s, half, bank][:, place // 2, place % 2 * HD : (place % 2 + 1) * HD],
                lhsT=matrix_of[s, half][:, i, :],
                rhs=v_of[b][:, h, half * HALF + i, :],
                start=(place == 0),
                stop=False,
            )

        def mix_back(s, half, bank):
            for cell in range(4):
                nc.tensor.matmul(
                    fin_of[s, half, bank][:, cell, :],
                    lhsT=acc_cols_of[s, half][:, 4 * bank + cell, :],
                    rhs=ident,
                    start=False,
                    stop=(cell == 3),
                    is_transpose=True,
                )

        def finish(s, half, bank):
            if s not in result_of:
                result = qkv.tile([P, PLACES, HD], F32, tag="q", bufs=4)
                result_of[s] = result
            places = slice(half * HALF + 8 * bank, half * HALF + 8 * bank + 8)
            nc.vector.tensor_tensor(
                out=result_of[s][:, places, :],
                in0=fin_of[s, half, bank][:].rearrange("p k (c d) -> p (k c) d", d=HD),
                in1=one_over_z_of[s][:, places].unsqueeze(2).to_broadcast([P, 8, HD]),
                op=ALU.mult,
            )

        def store(s, first, last):
            b, h = STAGES[s]
            nc.sync.dma_start(
                out=out[b].rearrange("(p c) f -> p c f", c=PLACES)[:, first:last, h * HD : (h + 1) * HD],
                in_=result_of[s][:, first:last, :],
            )

        last_chunk = len(chunks) - 1
        near_rowed = tuple(col for col in ROWED if col < NEAR)
        far_rowed = tuple(col for col in ROWED if col >= NEAR)
        dot_steps = len(STAGES) * STEPS

        between, beside, units_at = {}, {}, {}

        def vector_job(t, *work):
            between.setdefault(t, []).append(work)

        def plan_at(t, *work):
            beside.setdefault(t, []).append(work)

        def clear_late():
            clear_matrix(W_TOO_AT, P, zeros_tile())

        for s in range(len(STAGES)):
            begin, start, last = STEPS * s, STEPS * (s + 1), s == len(STAGES) - 1
            f = begin + 5
            vector_job(f, scores, s, False)
            plan_at(f, exponentials, s, False)
            for work in (features, shares, weights, add_to_z):
                vector_job(f + 1, work, s, False)
            vector_job(f + 2, subtract_in_z, s, False)
            if not last:
                plan_at(start, dots_out, s)
                plan_at(start, dots_back, s)
                n = start + 2
                vector_job(n, scores, s, True)
                plan_at(n, exponentials, s, True)
                for work in (features, shares, weights):
                    vector_job(n + 1, work, s, True)
                plan_at(n + 1, park_weights, s)
                for work in (add_to_z, subtract_in_z):
                    vector_job(n + 2, work, s, True)
                for work in (add_up_z, invert_z):
                    vector_job(n + 2, work, s)
            far_at, near_at, read_at, turn_at, write_at, read_too_at, turn_too_at = (
                (6, 6, 8, 10, 9, 11, 13) if s == 0 else (-2, 1, 2, 3, 1, 2, 5) if last else (0 if s == 1 else -2, 3, 5, 7, 7, 9, 11)
            )
            plan_at(start + far_at, write_matrix, s, HALVES[0], far_rowed)
            if last:
                plan_at(start + far_at, clear_late)
                plan_at(start + far_at + 1, write_matrix, s, HALVES[1], far_rowed)
            plan_at(start + near_at, write_matrix, s, HALVES[0], near_rowed)
            plan_at(start + (2 if last else 5), move_weights, s)
            plan_at(start + read_at, read_matrix, s, HALVES[0])
            plan_at(start + turn_at, turn_matrix, s, HALVES[0])
            plan_at(start + write_at, write_matrix, s, HALVES[1], near_rowed if last else ROWED)
            plan_at(start + read_too_at, read_matrix, s, HALVES[1])
            plan_at(start + turn_too_at, turn_matrix, s, HALVES[1])
            units = [(half, k) for half in HALVES for k in range(len(MIX_ORDER))]
            for n, (half, k) in enumerate(units):
                if last:
                    t = start + 1 + n * 7 // len(units)
                elif s < len(STAGES) - 2 or n < 16:
                    t = start + 4 + n * 8 // len(units)
                else:
                    t = start + STEPS + (n - 16) // 2
                units_at.setdefault(t, []).append((s, half, k))
                if k == len(MIX_ORDER) - 1:
                    mixed = t + (3 if last else 2)
                    plan_at(mixed, mix_out, s, half)
                    for bank in range(2):
                        far_from, far_steps = (((4, 2), (6, 2), (9, 2), (11, 2)) if last else ((11, 2), (13, 2), (15, 3), (18, 3)) if s == 0 else ((8, 2), (10, 2), (13, 1), (14, 1)) if s == 2 else ((9, 2), (12, 2), (15, 2), (18, 2)))[(half != HALVES[0]) * 2 + bank]
                        for i in range(8):
                            plan_at(start + far_from + i * far_steps // 8, mix_far, s, half, 8 * bank + i)
                        done = max(mixed + 1, start + far_from + far_steps)
                        plan_at(done, mix_back, s, half, bank)
                        vector_job(done + 1, finish, s, half, bank)
        end = max(max(beside), max(between)) + 1

        def project(i, part, early):
            if part == 0:
                if i + 2 <= last_chunk:
                    transpose_x(i + 2, 0)
                if early and i > 0:
                    keep_rows(i - 1)
                if 0 <= i - 1 <= last_chunk:
                    far_dots(i - 1)
                    far_dots_out(i - 1, early)
                if i + 2 <= last_chunk:
                    transpose_x(i + 2, 1)
                    if i + 4 <= last_chunk:
                        load_x(i + 4)
            elif part == 1:
                if not early and i - 1 <= last_chunk:
                    keep_rows(i - 1)
                if i + 1 <= last_chunk:
                    quantise_x(i + 1)
            elif i <= last_chunk:
                multiply(i)
                keep_columns(i, early)

        with tc.manual_schedule():
            for g in range(PASSES):
                transpose_x(0, g)
            load_x(2)
            for g in range(PASSES):
                transpose_x(1, g)
            load_x(3)
            quantise_x(0)
            turn_bias()
            for i in range(CHUNKS + HEAD):
                for part in range(3):
                    project(i, part, True)
                if i == 0:
                    clear_matrix(0, K_AT // W_ROW, zeros)
                elif i == CHUNKS // 2:
                    store_far_dots(0, 0)
                elif i == CHUNKS // 2 + 1:
                    fetch_far_dots(0, 0)
                elif i == CHUNKS - 1:
                    park_k(0, 0)
                    park_k(0, 1)
                    load_window(0)
                    load_window(1)
                elif i == CHUNKS:
                    store_far_dots(0, 1)

            next_chunk = CHUNKS + HEAD
            for t in range(end):
                projecting = t % 2 == 0 and next_chunk <= last_chunk + 1
                if projecting:
                    project(next_chunk, 0, False)
                if t < dot_steps and t % QUADS == 0 and t // QUADS + 2 < dot_steps // QUADS:
                    load_window(t // QUADS + 2)
                if t == 1:
                    fetch_far_dots(0, 1)
                elif t == 6:
                    store_far_dots(1, 0)
                elif t == 6 + 1:
                    fetch_far_dots(1, 0)
                elif t == STEPS + 2:
                    store_far_dots(1, 1)
                elif t == STEPS + 2 + 2:
                    fetch_far_dots(1, 1)
                elif t == STEPS + 2 + 3:
                    clear_matrix(W_AT, P, zeros_tile())
                elif t == STEPS + 3:
                    park_k(1, 0)
                elif t == 2 * STEPS - 2:
                    park_k(1, 1)
                jobs = between.get(t, [])
                if t < dot_steps:
                    for i in range(QUAD):
                        product(t, i)
                        for work in jobs[i : i + 1] if i < QUAD - 1 else jobs[i:]:
                            work[0](*work[1:])
                elif t > dot_steps:
                    for work in jobs:
                        work[0](*work[1:])
                if projecting:
                    project(next_chunk, 1, False)
                if 1 <= t <= dot_steps:
                    sum_products(t - 1)
                if projecting:
                    project(next_chunk, 2, False)
                    next_chunk += 1
                if t == dot_steps:
                    for work in jobs:
                        work[0](*work[1:])
                    s = len(STAGES) - 1
                    dots_out(s)
                    dots_back(s)
                    scores(s, True)
                    exponentials(s, True)
                    features(s, True)
                    shares(s, True)
                    weights(s, True)
                    park_weights(s)
                elif t == dot_steps + 2:
                    add_to_z(s, True)
                    subtract_in_z(s, True)
                    add_up_z(s)
                    invert_z(s)
                late = [work for work in beside.get(t, ()) if work[0] in (exponentials, dots_out, dots_back)]
                for work in beside.get(t, ()):
                    if work not in late:
                        work[0](*work[1:])
                for when in range(dot_steps - 3, dot_steps) if t == dot_steps else () if dot_steps - 3 < t < dot_steps else (t - 1,):
                    for unit in units_at.get(when, ()):
                        sum_weighted(*unit)
                for unit in units_at.get(t, ()):
                    weigh(*unit, 0 if t < dot_steps else 6)
                for work in late:
                    work[0](*work[1:])
                if t == dot_steps + STEPS - 1:
                    for done in range(3):
                        store(done, 0, PLACES)
            for half in HALVES:
                for bank in range(2):
                    store(3, half * HALF + 8 * bank, half * HALF + 8 * bank + 8)
